import numpy as np
import ml_dtypes


def mxq(x, axis, fmt="e4m3"):
    dtype, down = {"e4m3": (ml_dtypes.float8_e4m3fn, 7), "e5m2": (ml_dtypes.float8_e5m2, 14)}[fmt]
    v = np.moveaxis(np.asarray(x, np.float32).astype(ml_dtypes.bfloat16).astype(np.float64), axis, -1)
    blocks = v.reshape(v.shape[:-1] + (-1, 32))
    amax = np.abs(blocks).max(-1, keepdims=True)
    byte = np.maximum(np.where(amax > 0, np.frexp(amax)[1] - 1 + 127, 0) - down, 1)
    scale = np.exp2(byte - 127.0)
    codes = (blocks / scale).astype(np.float32).astype(dtype).astype(np.float64)
    return np.moveaxis((codes * scale).reshape(v.shape), -1, axis)


WIDE = False


def mx_kscale(k):
    if not WIDE:
        return np.ones(k)
    levels = np.array([10, -10, 5, -5, 0])
    if k % 512:
        return np.exp2(np.random.permutation(np.resize(levels, k // 32))).repeat(32)
    a = np.empty((k // 512, 16))
    for p in range(k // 512):
        a[p, :8] = np.random.permutation(np.resize(levels, 8))
        for g in range(8):
            far = levels[np.abs(levels - a[p, g]) >= 10]
            a[p, g + 8] = far[np.random.randint(len(far))]
    return np.exp2(a.ravel()).repeat(32)


BF16 = ml_dtypes.bfloat16


def bf(x):
    return np.asarray(x, np.float32).astype(BF16)


def f64(x):
    return np.asarray(x).astype(np.float64)


B, T, D, H = 4, 256, 512, 2048
N = B * T
EMA0 = 1.0


def sigmoid(v):
    return 1.0 / (1.0 + np.exp(-v))


def surprise_gate(err):
    err_mag = np.sqrt(np.sum(err * err)) / N
    ema = 0.95 * EMA0 + 0.05 * err_mag
    return np.minimum(err_mag / np.maximum(ema, 1e-8), 3.0)


def setup_inputs():
    s, t = mx_kscale(D), mx_kscale(N)
    return {"err": bf(np.random.standard_normal((N, D)) * 2.3 * s[None, :] * t[:, None]),
            "W_down": bf(np.random.standard_normal((D, H)) / np.sqrt(D) / s[:, None]),
            "gate_pre": bf(np.random.standard_normal((N, H))),
            "up_pre": bf(np.random.standard_normal((N, H))),
            "x_pred": bf(np.random.standard_normal((N, D)) / t[:, None])}


def reference(err, W_down, gate_pre, up_pre, x_pred):
    err, gate_pre, up_pre = f64(err), f64(gate_pre), f64(up_pre)
    sg = surprise_gate(err)
    d_h = f64(bf(mxq(err, 1, "e4m3") @ mxq(f64(W_down), 0, "e4m3")))
    sig = sigmoid(gate_pre)
    gate_act = gate_pre * sig
    d_gate_act = d_h * up_pre
    d_up_val = d_h * gate_act
    d_gate_pre = d_gate_act * sig * (1.0 + gate_pre * (1.0 - sig))
    xq = mxq(f64(x_pred), 0, "e4m3")
    grad_gate = (mxq(d_gate_pre, 0, "e4m3").T @ xq) / N
    grad_up = (mxq(d_up_val, 0, "e4m3").T @ xq) / N
    return grad_up * sg, grad_gate * sg

@@ -1,0 +1,338 @@
+from contextlib import ExitStack
+
+import concourse.mybir as mybir
+from concourse.masks import make_identity
+
+F32 = mybir.dt.float32
+BF16 = mybir.dt.bfloat16
+U32 = mybir.dt.uint32
+U8 = mybir.dt.uint8
+FP8X4 = mybir.dt.float8_e4m3fn_x4
+ACT = mybir.ActivationFunctionType
+ALU = mybir.AluOpType
+ENG = mybir.EngineType
+
+N_TOK, D, H = 1024, 512, 2048
+FLOPS = 3 * 2 * N_TOK * D * H
+
+P = 128
+PACK = 4
+K_PASS = P * PACK
+G = N_TOK // K_PASS
+HT = 128
+N_HT = H // HT
+HB = 256
+N_HB = H // HB
+HL = 512
+N_HL = H // HL
+NQ = G * PACK // 2
+BANK_DT = BF16
+
+
+def tile_continuummemorysystem_pa_kernel(tc, err, W_down, gate_pre, up_pre, x_pred, out_0, out_1):
+    nc = tc.nc
+    outs = (out_0, out_1)
+
+    with ExitStack() as ctx:
+        keep = ctx.enter_context(tc.tile_pool(name="keep", bufs=1))
+        raw = ctx.enter_context(tc.tile_pool(name="raw", bufs=4))
+        grp = ctx.enter_context(tc.tile_pool(name="grp", bufs=3))
+        elem = ctx.enter_context(tc.tile_pool(name="elem", bufs=3))
+        prod = ctx.enter_context(tc.tile_pool(name="prod", bufs=3))
+        stage = ctx.enter_context(tc.tile_pool(name="stage", bufs=4))
+        psum = ctx.enter_context(tc.psum_pool(name="psum", bufs=4))
+
+        gate_sb = [keep.tile([P, G * PACK, HL], BF16, name="gate%d" % c, tag="gate%d" % c) for c in range(N_HL)]
+        up_sb = [keep.tile([P, G * PACK, HL], BF16, name="up%d" % c, tag="up%d" % c) for c in range(N_HL)]
+        w_codes = keep.tile([P, H], U32, name="w_codes", tag="w_codes", align_bytes=64)
+        w_scales = keep.tile([P, H], U8, name="w_scales", tag="w_scales", align_bytes=64)
+        e_codes = keep.tile([P, N_TOK], U32, name="e_codes", tag="e_codes", align_bytes=64)
+        e_scales = keep.tile([P, N_TOK], U8, name="e_scales", tag="e_scales", align_bytes=64)
+        x_codes = keep.tile([P, G * D], U32, name="x_codes", tag="x_codes", align_bytes=64)
+        x_scales = keep.tile([P, G * D], U8, name="x_scales", tag="x_scales", align_bytes=64)
+        ident = keep.tile([P, P], F32, name="ident", tag="ident")
+        ones = keep.tile([P, P], F32, name="ones", tag="ones")
+        diag = keep.tile([P, P], F32, name="diag", tag="diag")
+        ssq = keep.tile([P, 2], F32, name="ssq", tag="ssq")
+        warm_in = keep.tile([P, 1], F32, name="warm_in", tag="warm_in")
+        warm_out = keep.tile([P, 1], F32, name="warm_out", tag="warm_out")
+        em = keep.tile([P, 1], F32, name="em", tag="em")
+        ema = keep.tile([P, 1], F32, name="ema", tag="ema")
+        emc = keep.tile([P, 1], F32, name="emc", tag="emc")
+        rec = keep.tile([P, 1], F32, name="rec", tag="rec")
+        sgv = keep.tile([P, 1], F32, name="sgv", tag="sgv")
+        sgs = keep.tile([P, 1], F32, name="sgs", tag="sgs")
+
+        def load_w(c):
+            t = raw.tile([P, PACK, HL], BF16, name="w_raw", tag="raw")
+            nc.sync.dma_start(out=t[:], in_=W_down[:, c * HL:(c + 1) * HL].rearrange("(p j) h -> p j h", j=PACK))
+            return t
+
+        def load_rows(src, g):
+            t = raw.tile([P, PACK * D], BF16, name="rows_raw", tag="raw")
+            nc.sync.dma_start(out=t[:], in_=src[g * K_PASS:(g + 1) * K_PASS, :].rearrange("(p j) d -> p (j d)", j=PACK))
+            return t
+
+        def load_act(dst, src, c):
+            for g in range(G):
+                nc.sync.dma_start(
+                    out=dst[c][:, g * PACK:(g + 1) * PACK, :],
+                    in_=src[g * K_PASS:(g + 1) * K_PASS, c * HL:(c + 1) * HL].rearrange("(p t) h -> p t h", t=PACK),
+                )
+
+        w_raw, e_raw, x_raw = {}, {}, {}
+        load_act(gate_sb, gate_pre, 0)
+        w_raw[0] = load_w(0)
+        e_raw[0] = load_rows(err, 0)
+        e_raw[1] = load_rows(err, 1)
+        load_act(gate_sb, gate_pre, 1)
+        load_act(up_sb, up_pre, 0)
+        w_raw[1] = load_w(1)
+
+        nc.gpsimd.memset(warm_in[:], 0.0)
+        nc.scalar.activation(out=warm_out[:], in_=warm_in[:], func=ACT.Sigmoid)
+        make_identity(nc, ident[:])
+        nc.gpsimd.memset(ones[:], 1.0)
+        nc.gpsimd.memset(ssq[:], 0.0)
+
+        def interleave(engine, src3):
+            t = grp.tile([P, HL * PACK], BF16, name="grouped", tag="grouped", align_bytes=64)
+            dst = t[:].rearrange("p (c i j) -> p c j i", i=4, j=PACK)
+            src = src3.rearrange("p j (c i) -> p c j i", i=4)
+            if engine == "v":
+                nc.vector.tensor_copy(out=dst, in_=src)
+            else:
+                nc.scalar.copy(out=dst, in_=src)
+            return t
+
+        def quantize(t, codes, scales, lo):
+            nc.vector.quantize_mx(
+                out=codes[:, lo:lo + HL].bitcast(FP8X4),
+                scales=scales[:, lo:lo + HL],
+                in_=t[:],
+            )
+
+        def gate_pairs(b):
+            c, off = divmod(b * HB, HL)
+            return gate_sb[c][:, :, off:off + HB].rearrange("p (q e) h -> p q h e", e=2)
+
+        sx, mb, lt = {}, {}, {}
+
+        def act_sig(b):
+            sx[b] = elem.tile([P, NQ, HB, 2], F32, name="sx", tag="sx", bufs=5)
+            nc.scalar.activation(out=sx[b][:], in_=gate_pairs(b), func=ACT.Sigmoid)
+
+        def act_m(b):
+            mb[b] = elem.tile([P, NQ, HB, 2], F32, name="mb", tag="mb")
+            nc.scalar.activation(out=mb[b][:], in_=gate_pairs(b), func=ACT.Silu, scale=-1.0)
+
+        def act_l(b):
+            lt[b] = elem.tile([P, NQ, HB, 2], F32, name="lt", tag="lt")
+            nc.scalar.activation(out=lt[b][:], in_=gate_pairs(b), func=ACT.Silu)
+
+        def xmul(b):
+            c, off = divmod(b * HB, HL)
+            for q in range(NQ):
+                nc.vector.scalar_tensor_tensor(
+                    out=sx[b][:, q, :, :], in0=sx[b][:, q, :, :], scalar=-1.0,
+                    in1=up_sb[c][:, 2 * q:2 * q + 2, off:off + HB].rearrange("p e h -> p h e"),
+                    op0=ALU.mult, op1=ALU.mult,
+                )
+
+        def bmul(b):
+            flat = mb[b][:].rearrange("p q h e -> p (q h e)")
+            nc.vector.scalar_tensor_tensor(
+                out=flat, in0=flat, scalar=1.0, in1=sx[b][:].rearrange("p q h e -> p (q h e)"),
+                op0=ALU.subtract, op1=ALU.mult,
+            )
+
+        dh = {}
+
+        def stage1(u):
+            ht, g = divmod(u, G)
+            dh[u] = psum.tile([P, PACK, HT], BANK_DT, name="dh", tag="dh")
+            for t in range(PACK):
+                lo = g * K_PASS + t * P
+                nc.tensor.matmul_mx(
+                    out=dh[u][:, t, :],
+                    lhsT=e_codes[:, lo:lo + P].bitcast(FP8X4),
+                    lhsT_scale=e_scales[:, lo:lo + P],
+                    rhs=w_codes[:, ht * HT:(ht + 1) * HT].bitcast(FP8X4),
+                    rhs_scale=w_scales[:, ht * HT:(ht + 1) * HT],
+                    start=True, stop=True,
+                )
+
+        pq = {}
+
+        def pmul(u):
+            ht, g = divmod(u, G)
+            b, hl = divmod(ht, HB // HT)
+            if g == 0:
+                pq[ht] = prod.tile([P, 2, G, HT * PACK], BF16, name="pq", tag="pq", align_bytes=64)
+            bank = dh[u][:].rearrange("p (s e) h -> p h s e", e=2)
+            cols = slice(hl * HT, (hl + 1) * HT)
+            prs = slice(2 * g, 2 * g + 2)
+            for a, factor in ((0, lt[b]), (1, mb[b])):
+                nc.vector.tensor_tensor(
+                    out=pq[ht][:, a, g, :].rearrange("p (h s e) -> p h s e", s=2, e=2),
+                    in0=bank, in1=factor[:, prs, cols, :].rearrange("p s h e -> p h s e"), op=ALU.mult,
+                )
+
+        pc, ps = {}, {}
+
+        def pquant(ht):
+            pc[ht] = prod.tile([P, 2 * G * HT], U32, name="pc", tag="pc", align_bytes=64)
+            ps[ht] = prod.tile([P, 2 * G * HT], U8, name="ps", tag="ps", align_bytes=64)
+            nc.vector.quantize_mx(
+                out=pc[ht][:].bitcast(FP8X4), scales=ps[ht][:],
+                in_=pq[ht][:].rearrange("p a g c -> p (a g c)"),
+            )
+
+        acc = {}
+
+        def stage2(ht):
+            for a in range(2):
+                acc[ht, a] = psum.tile([P, D], F32, name="acc", tag="acc")
+                for g in range(G):
+                    lo = (a * G + g) * HT
+                    nc.tensor.matmul_mx(
+                        out=acc[ht, a][:],
+                        lhsT=pc[ht][:, lo:lo + HT].bitcast(FP8X4),
+                        lhsT_scale=ps[ht][:, lo:lo + HT],
+                        rhs=x_codes[:, g * D:(g + 1) * D].bitcast(FP8X4),
+                        rhs_scale=x_scales[:, g * D:(g + 1) * D],
+                        start=(g == 0), stop=(g == G - 1),
+                    )
+
+        def evac(ht):
+            for a in range(2):
+                res = stage.tile([P, D], F32, name="res", tag="res")
+                if ht == N_HT - 1 and a == 1:
+                    nc.vector.tensor_scalar(out=res[:], in0=acc[ht, a][:], scalar1=sgs[:, 0:1], scalar2=None, op0=ALU.mult)
+                else:
+                    nc.scalar.activation(out=res[:], in_=acc[ht, a][:], func=ACT.Copy, scale=sgs[:, 0:1])
+                nc.sync.dma_start(out=outs[a][ht * HT:(ht + 1) * HT, :], in_=res[:])
+
+        ctx.enter_context(tc.manual_schedule(engines={ENG.Activation, ENG.DVE}))
+
+        act_sig(0)
+        act_sig(1)
+        gw0 = interleave("v", w_raw[0][:])
+
+        e_grp = {}
+        for g in range(G):
+            words = e_raw[g][:].bitcast(F32)
+            e_grp[g] = grp.tile([P, HL * PACK], BF16, name="e_grouped", tag="grouped", align_bytes=64)
+            egw = e_grp[g][:].bitcast(F32).rearrange("p (t m u) -> p t m u", t=PACK, u=2)
+            for half in range(2):
+                xt = psum.tile([P, PACK, P], F32, name="xt", tag="dh")
+                for tt in range(2):
+                    t = 2 * half + tt
+                    for u in range(2):
+                        nc.tensor.transpose(
+                            out=xt[:, 2 * tt + u, :],
+                            in_=words[:, t * 256 + u:(t + 1) * 256:2],
+                            identity=ident[:],
+                        )
+                nc.scalar.copy(
+                    out=egw[:, 2 * half:2 * half + 2, :, :],
+                    in_=xt[:].rearrange("p (tt u) m -> p tt m u", u=2),
+                )
+        quantize(gw0, w_codes, w_scales, 0)
+        gram = psum.tile([P, P], F32, name="gram", tag="acc")
+        n_mm = G * PACK * (D // P)
+        i_mm = 0
+        for g in range(G):
+            for t in range(PACK):
+                for fb in range(D // P):
+                    blk = e_raw[g][:, t * D + fb * P:t * D + (fb + 1) * P]
+                    nc.tensor.matmul(out=gram[:], lhsT=blk, rhs=blk, start=(i_mm == 0), stop=(i_mm == n_mm - 1))
+                    i_mm += 1
+        act_sig(2)
+        act_sig(3)
+        for g in range(G):
+            quantize(e_grp[g], e_codes, e_scales, g * K_PASS)
+        nc.vector.scalar_tensor_tensor(
+            out=diag[:], in0=gram[:], scalar=1.0, in1=ident[:], op0=ALU.mult, op1=ALU.mult,
+            accum_out=ssq[:, 0:1],
+        )
+        tot = psum.tile([P, 2], F32, name="tot", tag="acc")
+        nc.tensor.matmul(out=tot[:], lhsT=ones[:], rhs=ssq[:], start=True, stop=True)
+
+        x_raw[0] = load_rows(x_pred, 0)
+        x_raw[1] = load_rows(x_pred, 1)
+        load_act(up_sb, up_pre, 1)
+        load_act(gate_sb, gate_pre, 2)
+        load_act(up_sb, up_pre, 2)
+        w_raw[2] = load_w(2)
+        load_act(gate_sb, gate_pre, 3)
+        load_act(up_sb, up_pre, 3)
+        w_raw[3] = load_w(3)
+
+        xmul(0)
+        xmul(1)
+        nc.scalar.activation(out=em[:], in_=tot[:, 0:1], func=ACT.Sqrt, scale=1.0 / (N_TOK * N_TOK))
+        nc.gpsimd.tensor_scalar(out=ema[:], in0=em[:], scalar1=0.05, scalar2=0.95, op0=ALU.mult, op1=ALU.add)
+        nc.gpsimd.tensor_scalar(out=emc[:], in0=ema[:], scalar1=1e-8, scalar2=None, op0=ALU.max)
+        act_m(0)
+        act_l(0)
+        gw1 = interleave("v", w_raw[1][:])
+        nc.vector.reciprocal(out=rec[:], in_=emc[:])
+        quantize(gw1, w_codes, w_scales, HL)
+        nc.gpsimd.tensor_scalar(out=sgv[:], in0=rec[:], scalar1=em[:, 0:1], scalar2=3.0, op0=ALU.mult, op1=ALU.min)
+        nc.gpsimd.tensor_scalar(out=sgs[:], in0=sgv[:], scalar1=1.0 / N_TOK, scalar2=None, op0=ALU.mult)
+        gx0 = interleave("s", x_raw[0][:].rearrange("p (j d) -> p j d", j=PACK))
+        gx1 = interleave("s", x_raw[1][:].rearrange("p (j d) -> p j d", j=PACK))
+        act_m(1)
+        act_l(1)
+        xmul(2)
+        xmul(3)
+        bmul(0)
+
+        N_U = N_HT * G
+        AHEAD = 4
+        gw_late = {}
+        for u in range(AHEAD):
+            stage1(u)
+        for u in range(N_U):
+            b, r = divmod(u, 4)
+            ht = u // G
+            pmul(u)
+            if u + AHEAD < N_U:
+                stage1(u + AHEAD)
+            if u == 0:
+                quantize(gx0, x_codes, x_scales, 0)
+            if u == 1:
+                quantize(gx1, x_codes, x_scales, D)
+            if r % 2 == 0 and ht >= 1:
+                pquant(ht - 1)
+                stage2(ht - 1)
+            if r == 0:
+                if u == 12:
+                    act_sig(7)
+                if b + 2 < N_HB:
+                    act_m(b + 2)
+            if r == 1:
+                if b >= 1:
+                    evac(2 * b - 1)
+                if 4 <= b + 1 < N_HB:
+                    xmul(b + 1)
+            if r == 2:
+                if b + 2 < N_HB:
+                    act_l(b + 2)
+                if u == 10:
+                    act_sig(4)
+                if b in (1, 2):
+                    quantize(gw_late[b + 1], w_codes, w_scales, (b + 1) * HL)
+                if b + 1 < N_HB:
+                    bmul(b + 1)
+            if r == 3:
+                evac(2 * b)
+                if b in (0, 1):
+                    gw_late[b + 2] = interleave("s", w_raw[b + 2][:])
+                if u == 11:
+                    act_sig(5)
+                    act_sig(6)
+        pquant(N_HT - 1)
+        stage2(N_HT - 1)
+        evac(N_HT - 1)

@@ -73,16 +73,17 @@ def tile_continuummemorysystem_pa_kernel(tc, err, W_down, gate_pre, up_pre, x_pr
             nc.sync.dma_start(out=t[:], in_=src[g * K_PASS:(g + 1) * K_PASS, :].rearrange("(p j) d -> p (j d)", j=PACK))
             return t
 
-        def load_act(dst, src, c):
+        def load_act(dst, src, c, lo=0, hi=HL):
             for g in range(G):
                 nc.sync.dma_start(
-                    out=dst[c][:, g * PACK:(g + 1) * PACK, :],
-                    in_=src[g * K_PASS:(g + 1) * K_PASS, c * HL:(c + 1) * HL].rearrange("(p t) h -> p t h", t=PACK),
+                    out=dst[c][:, g * PACK:(g + 1) * PACK, lo:hi],
+                    in_=src[g * K_PASS:(g + 1) * K_PASS, c * HL + lo:c * HL + hi].rearrange("(p t) h -> p t h", t=PACK),
                 )
 
         w_raw, e_raw, x_raw = {}, {}, {}
-        load_act(gate_sb, gate_pre, 0)
+        load_act(gate_sb, gate_pre, 0, 0, HB)
         w_raw[0] = load_w(0)
+        load_act(gate_sb, gate_pre, 0, HB, HL)
         e_raw[0] = load_rows(err, 0)
         e_raw[1] = load_rows(err, 1)
         load_act(gate_sb, gate_pre, 1)
@@ -104,6 +105,14 @@ def tile_continuummemorysystem_pa_kernel(tc, err, W_down, gate_pre, up_pre, x_pr
             else:
                 nc.scalar.copy(out=dst, in_=src)
             return t
+
+        def interleave_half(t, src3, half):
+            for lo in (half * 256, half * 256 + 128):
+                nc.gpsimd.tensor_scalar(
+                    out=t[:, lo * PACK:(lo + 128) * PACK].rearrange("p (w j) -> p w j", j=PACK),
+                    in0=src3[:, :, lo:lo + 128].rearrange("p j w -> p w j"),
+                    scalar1=1.0, scalar2=0.0, op0=ALU.mult, op1=ALU.add,
+                )
 
         def quantize(t, codes, scales, lo):
             nc.vector.quantize_mx(
@@ -162,18 +171,38 @@ def tile_continuummemorysystem_pa_kernel(tc, err, W_down, gate_pre, up_pre, x_pr
                     start=True, stop=True,
                 )
 
-        pq = {}
+        pq, dhs = {}, {}
+
+        def new_pq(ht):
+            pq[ht] = prod.tile([P, 2, G, HT * PACK], BF16, name="pq", tag="pq", align_bytes=64)
 
         def pmul(u):
             ht, g = divmod(u, G)
             b, hl = divmod(ht, HB // HT)
-            if g == 0:
-                pq[ht] = prod.tile([P, 2, G, HT * PACK], BF16, name="pq", tag="pq", align_bytes=64)
             bank = dh[u][:].rearrange("p (s e) h -> p h s e", e=2)
             cols = slice(hl * HT, (hl + 1) * HT)
             prs = slice(2 * g, 2 * g + 2)
             for a, factor in ((0, lt[b]), (1, mb[b])):
                 nc.vector.tensor_tensor(
+                    out=pq[ht][:, a, g, :].rearrange("p (h s e) -> p h s e", s=2, e=2),
+                    in0=bank, in1=factor[:, prs, cols, :].rearrange("p s h e -> p h s e"), op=ALU.mult,
+                )
+
+        def dhcopy(u):
+            dhs[u] = prod.tile([P, HT * PACK], BANK_DT, name="dhs", tag="dhs", bufs=2)
+            nc.scalar.copy(
+                out=dhs[u][:].rearrange("p (h t) -> p h t", t=PACK),
+                in_=dh[u][:].rearrange("p t h -> p h t"),
+            )
+
+        def gp_pmul(u):
+            ht, g = divmod(u, G)
+            b, hl = divmod(ht, HB // HT)
+            bank = dhs[u][:].rearrange("p (h s e) -> p h s e", s=2, e=2)
+            cols = slice(hl * HT, (hl + 1) * HT)
+            prs = slice(2 * g, 2 * g + 2)
+            for a, factor in ((1, mb[b]), (0, lt[b])):
+                nc.gpsimd.tensor_tensor(
                     out=pq[ht][:, a, g, :].rearrange("p (h s e) -> p h s e", s=2, e=2),
                     in0=bank, in1=factor[:, prs, cols, :].rearrange("p s h e -> p h s e"), op=ALU.mult,
                 )
@@ -204,16 +233,15 @@ def tile_continuummemorysystem_pa_kernel(tc, err, W_down, gate_pre, up_pre, x_pr
                         start=(g == 0), stop=(g == G - 1),
                     )
 
-        def evac(ht):
-            for a in range(2):
-                res = stage.tile([P, D], F32, name="res", tag="res")
-                if ht == N_HT - 1 and a == 1:
-                    nc.vector.tensor_scalar(out=res[:], in0=acc[ht, a][:], scalar1=sgs[:, 0:1], scalar2=None, op0=ALU.mult)
-                else:
-                    nc.scalar.activation(out=res[:], in_=acc[ht, a][:], func=ACT.Copy, scale=sgs[:, 0:1])
-                nc.sync.dma_start(out=outs[a][ht * HT:(ht + 1) * HT, :], in_=res[:])
+        def evac(engine, ht, a):
+            res = stage.tile([P, D], F32, name="res", tag="res")
+            if engine == "v":
+                nc.vector.tensor_scalar(out=res[:], in0=acc[ht, a][:], scalar1=sgs[:, 0:1], scalar2=None, op0=ALU.mult)
+            else:
+                nc.scalar.activation(out=res[:], in_=acc[ht, a][:], func=ACT.Copy, scale=sgs[:, 0:1])
+            nc.sync.dma_start(out=outs[a][ht * HT:(ht + 1) * HT, :], in_=res[:])
 
-        ctx.enter_context(tc.manual_schedule(engines={ENG.Activation, ENG.DVE}))
+        ctx.enter_context(tc.manual_schedule(engines={ENG.Activation, ENG.DVE, ENG.Pool}))
 
         act_sig(0)
         act_sig(1)
@@ -276,63 +304,69 @@ def tile_continuummemorysystem_pa_kernel(tc, err, W_down, gate_pre, up_pre, x_pr
         nc.gpsimd.tensor_scalar(out=emc[:], in0=ema[:], scalar1=1e-8, scalar2=None, op0=ALU.max)
         act_m(0)
         act_l(0)
+        stage1(3)
+        dhcopy(3)
         gw1 = interleave("v", w_raw[1][:])
         nc.vector.reciprocal(out=rec[:], in_=emc[:])
         quantize(gw1, w_codes, w_scales, HL)
         nc.gpsimd.tensor_scalar(out=sgv[:], in0=rec[:], scalar1=em[:, 0:1], scalar2=3.0, op0=ALU.mult, op1=ALU.min)
         nc.gpsimd.tensor_scalar(out=sgs[:], in0=sgv[:], scalar1=1.0 / N_TOK, scalar2=None, op0=ALU.mult)
-        gx0 = interleave("s", x_raw[0][:].rearrange("p (j d) -> p j d", j=PACK))
-        gx1 = interleave("s", x_raw[1][:].rearrange("p (j d) -> p j d", j=PACK))
+        gx0 = interleave("v", x_raw[0][:].rearrange("p (j d) -> p j d", j=PACK))
+        gx1 = interleave("v", x_raw[1][:].rearrange("p (j d) -> p j d", j=PACK))
+        quantize(gx0, x_codes, x_scales, 0)
+        quantize(gx1, x_codes, x_scales, D)
         act_m(1)
         act_l(1)
-        xmul(2)
-        xmul(3)
         bmul(0)
 
-        N_U = N_HT * G
-        AHEAD = 4
         gw_late = {}
-        for u in range(AHEAD):
+        for u in range(3):
             stage1(u)
-        for u in range(N_U):
-            b, r = divmod(u, 4)
-            ht = u // G
-            pmul(u)
-            if u + AHEAD < N_U:
-                stage1(u + AHEAD)
-            if u == 0:
-                quantize(gx0, x_codes, x_scales, 0)
-            if u == 1:
-                quantize(gx1, x_codes, x_scales, D)
-            if r % 2 == 0 and ht >= 1:
-                pquant(ht - 1)
-                stage2(ht - 1)
-            if r == 0:
-                if u == 12:
-                    act_sig(7)
-                if b + 2 < N_HB:
-                    act_m(b + 2)
-            if r == 1:
-                if b >= 1:
-                    evac(2 * b - 1)
-                if 4 <= b + 1 < N_HB:
-                    xmul(b + 1)
-            if r == 2:
-                if b + 2 < N_HB:
-                    act_l(b + 2)
-                if u == 10:
-                    act_sig(4)
-                if b in (1, 2):
-                    quantize(gw_late[b + 1], w_codes, w_scales, (b + 1) * HL)
-                if b + 1 < N_HB:
-                    bmul(b + 1)
-            if r == 3:
-                evac(2 * b)
-                if b in (0, 1):
-                    gw_late[b + 2] = interleave("s", w_raw[b + 2][:])
-                if u == 11:
-                    act_sig(5)
-                    act_sig(6)
-        pquant(N_HT - 1)
-        stage2(N_HT - 1)
-        evac(N_HT - 1)
+        for b in range(N_HB):
+            u0 = 4 * b
+            ht0, ht1 = 2 * b, 2 * b + 1
+            more = b + 1 < N_HB
+            new_pq(ht0)
+            new_pq(ht1)
+            gp_pmul(u0 + 3)
+            if b < 4:
+                c_late, half = 2 + b // 2, b % 2
+                if half == 0:
+                    gw_late[c_late] = grp.tile([P, HL * PACK], BF16, name="grouped", tag="grouped", align_bytes=64)
+                interleave_half(gw_late[c_late], w_raw[c_late], half)
+            if more:
+                stage1(u0 + 7)
+                dhcopy(u0 + 7)
+            if b >= 1:
+                evac("s", ht0 - 1, 0)
+                evac("s", ht0 - 1, 1)
+            if b == 3:
+                act_sig(7)
+            if b + 2 < N_HB:
+                act_m(b + 2)
+                act_l(b + 2)
+            if b == 2:
+                act_sig(4)
+            for i in range(3):
+                pmul(u0 + i)
+                if more:
+                    stage1(u0 + 4 + i)
+            pquant(ht0)
+            stage2(ht0)
+            if b < 2:
+                xmul(b + 2)
+            if 4 <= b + 1 < N_HB:
+                xmul(b + 1)
+            if b in (2, 4):
+                quantize(gw_late[1 + b // 2], w_codes, w_scales, (1 + b // 2) * HL)
+            pquant(ht1)
+            stage2(ht1)
+            if more:
+                bmul(b + 1)
+            evac("s", ht0, 0)
+            evac("s", ht0, 1)
+            if b == 2:
+                act_sig(5)
+                act_sig(6)
+        evac("s", N_HT - 1, 0)
+        evac("v", N_HT - 1, 1)

@@ -35,8 +35,8 @@ def tile_continuummemorysystem_pa_kernel(tc, err, W_down, gate_pre, up_pre, x_pr
 
     with ExitStack() as ctx:
         keep = ctx.enter_context(tc.tile_pool(name="keep", bufs=1))
-        raw = ctx.enter_context(tc.tile_pool(name="raw", bufs=4))
-        grp = ctx.enter_context(tc.tile_pool(name="grp", bufs=3))
+        raw = ctx.enter_context(tc.tile_pool(name="raw", bufs=5))
+        grp = ctx.enter_context(tc.tile_pool(name="grp", bufs=4))
         elem = ctx.enter_context(tc.tile_pool(name="elem", bufs=3))
         prod = ctx.enter_context(tc.tile_pool(name="prod", bufs=3))
         stage = ctx.enter_context(tc.tile_pool(name="stage", bufs=4))
@@ -83,12 +83,13 @@ def tile_continuummemorysystem_pa_kernel(tc, err, W_down, gate_pre, up_pre, x_pr
         w_raw, e_raw, x_raw = {}, {}, {}
         load_act(gate_sb, gate_pre, 0, 0, HB)
         w_raw[0] = load_w(0)
-        load_act(gate_sb, gate_pre, 0, HB, HL)
+        x_raw[0] = load_rows(x_pred, 0)
         e_raw[0] = load_rows(err, 0)
         e_raw[1] = load_rows(err, 1)
-        load_act(gate_sb, gate_pre, 1)
+        x_raw[1] = load_rows(x_pred, 1)
         load_act(up_sb, up_pre, 0)
-        w_raw[1] = load_w(1)
+        load_act(gate_sb, gate_pre, 0, HB, HL)
+        load_act(gate_sb, gate_pre, 1)
 
         nc.gpsimd.memset(warm_in[:], 0.0)
         nc.scalar.activation(out=warm_out[:], in_=warm_in[:], func=ACT.Sigmoid)
@@ -125,35 +126,31 @@ def tile_continuummemorysystem_pa_kernel(tc, err, W_down, gate_pre, up_pre, x_pr
             c, off = divmod(b * HB, HL)
             return gate_sb[c][:, :, off:off + HB].rearrange("p (q e) h -> p q h e", e=2)
 
-        sx, mb, lt = {}, {}, {}
+        sx, lt = {}, {}
 
         def act_sig(b):
             sx[b] = elem.tile([P, NQ, HB, 2], F32, name="sx", tag="sx", bufs=5)
-            nc.scalar.activation(out=sx[b][:], in_=gate_pairs(b), func=ACT.Sigmoid)
-
-        def act_m(b):
-            mb[b] = elem.tile([P, NQ, HB, 2], F32, name="mb", tag="mb")
-            nc.scalar.activation(out=mb[b][:], in_=gate_pairs(b), func=ACT.Silu, scale=-1.0)
+            nc.scalar.activation(out=sx[b][:], in_=gate_pairs(b), func=ACT.Sigmoid, scale=-1.0)
 
         def act_l(b):
             lt[b] = elem.tile([P, NQ, HB, 2], F32, name="lt", tag="lt")
             nc.scalar.activation(out=lt[b][:], in_=gate_pairs(b), func=ACT.Silu)
 
+        def fmul(b):
+            flat = sx[b][:].rearrange("p q h e -> p (q h e)")
+            nc.vector.scalar_tensor_tensor(
+                out=flat, in0=lt[b][:].rearrange("p q h e -> p (q h e)"), scalar=1.0, in1=flat,
+                op0=ALU.subtract, op1=ALU.mult,
+            )
+
         def xmul(b):
             c, off = divmod(b * HB, HL)
             for q in range(NQ):
                 nc.vector.scalar_tensor_tensor(
-                    out=sx[b][:, q, :, :], in0=sx[b][:, q, :, :], scalar=-1.0,
+                    out=sx[b][:, q, :, :], in0=sx[b][:, q, :, :], scalar=1.0,
                     in1=up_sb[c][:, 2 * q:2 * q + 2, off:off + HB].rearrange("p e h -> p h e"),
-                    op0=ALU.mult, op1=ALU.mult,
+                    op0=ALU.add, op1=ALU.mult,
                 )
-
-        def bmul(b):
-            flat = mb[b][:].rearrange("p q h e -> p (q h e)")
-            nc.vector.scalar_tensor_tensor(
-                out=flat, in0=flat, scalar=1.0, in1=sx[b][:].rearrange("p q h e -> p (q h e)"),
-                op0=ALU.subtract, op1=ALU.mult,
-            )
 
         dh = {}
 
@@ -182,7 +179,7 @@ def tile_continuummemorysystem_pa_kernel(tc, err, W_down, gate_pre, up_pre, x_pr
             bank = dh[u][:].rearrange("p (s e) h -> p h s e", e=2)
             cols = slice(hl * HT, (hl + 1) * HT)
             prs = slice(2 * g, 2 * g + 2)
-            for a, factor in ((0, lt[b]), (1, mb[b])):
+            for a, factor in ((0, lt[b]), (1, sx[b])):
                 nc.vector.tensor_tensor(
                     out=pq[ht][:, a, g, :].rearrange("p (h s e) -> p h s e", s=2, e=2),
                     in0=bank, in1=factor[:, prs, cols, :].rearrange("p s h e -> p h s e"), op=ALU.mult,
@@ -201,7 +198,7 @@ def tile_continuummemorysystem_pa_kernel(tc, err, W_down, gate_pre, up_pre, x_pr
             bank = dhs[u][:].rearrange("p (h s e) -> p h s e", s=2, e=2)
             cols = slice(hl * HT, (hl + 1) * HT)
             prs = slice(2 * g, 2 * g + 2)
-            for a, factor in ((1, mb[b]), (0, lt[b])):
+            for a, factor in ((1, sx[b]), (0, lt[b])):
                 nc.gpsimd.tensor_tensor(
                     out=pq[ht][:, a, g, :].rearrange("p (h s e) -> p h s e", s=2, e=2),
                     in0=bank, in1=factor[:, prs, cols, :].rearrange("p s h e -> p h s e"), op=ALU.mult,
@@ -244,8 +241,15 @@ def tile_continuummemorysystem_pa_kernel(tc, err, W_down, gate_pre, up_pre, x_pr
         ctx.enter_context(tc.manual_schedule(engines={ENG.Activation, ENG.DVE, ENG.Pool}))
 
         act_sig(0)
-        act_sig(1)
         gw0 = interleave("v", w_raw[0][:])
+        w_raw[1] = load_w(1)
+        act_l(0)
+        quantize(gw0, w_codes, w_scales, 0)
+        gx0 = interleave("v", x_raw[0][:].rearrange("p (j d) -> p j d", j=PACK))
+        w_raw[2] = load_w(2)
+        load_act(up_sb, up_pre, 1)
+        load_act(gate_sb, gate_pre, 2)
+        load_act(up_sb, up_pre, 2)
 
         e_grp = {}
         for g in range(G):
@@ -266,7 +270,8 @@ def tile_continuummemorysystem_pa_kernel(tc, err, W_down, gate_pre, up_pre, x_pr
                     out=egw[:, 2 * half:2 * half + 2, :, :],
                     in_=xt[:].rearrange("p (tt u) m -> p tt m u", u=2),
                 )
-        quantize(gw0, w_codes, w_scales, 0)
+        gx1 = interleave("v", x_raw[1][:].rearrange("p (j d) -> p j d", j=PACK))
+        quantize(gx0, x_codes, x_scales, 0)
         gram = psum.tile([P, P], F32, name="gram", tag="acc")
         n_mm = G * PACK * (D // P)
         i_mm = 0
@@ -276,8 +281,10 @@ def tile_continuummemorysystem_pa_kernel(tc, err, W_down, gate_pre, up_pre, x_pr
                     blk = e_raw[g][:, t * D + fb * P:t * D + (fb + 1) * P]
                     nc.tensor.matmul(out=gram[:], lhsT=blk, rhs=blk, start=(i_mm == 0), stop=(i_mm == n_mm - 1))
                     i_mm += 1
-        act_sig(2)
-        act_sig(3)
+        w_raw[3] = load_w(3)
+        load_act(gate_sb, gate_pre, 3)
+        load_act(up_sb, up_pre, 3)
+        fmul(0)
         for g in range(G):
             quantize(e_grp[g], e_codes, e_scales, g * K_PASS)
         nc.vector.scalar_tensor_tensor(
@@ -286,39 +293,26 @@ def tile_continuummemorysystem_pa_kernel(tc, err, W_down, gate_pre, up_pre, x_pr
         )
         tot = psum.tile([P, 2], F32, name="tot", tag="acc")
         nc.tensor.matmul(out=tot[:], lhsT=ones[:], rhs=ssq[:], start=True, stop=True)
-
-        x_raw[0] = load_rows(x_pred, 0)
-        x_raw[1] = load_rows(x_pred, 1)
-        load_act(up_sb, up_pre, 1)
-        load_act(gate_sb, gate_pre, 2)
-        load_act(up_sb, up_pre, 2)
-        w_raw[2] = load_w(2)
-        load_act(gate_sb, gate_pre, 3)
-        load_act(up_sb, up_pre, 3)
-        w_raw[3] = load_w(3)
-
-        xmul(0)
-        xmul(1)
+        act_l(1)
+        stage1(3)
+        dhcopy(3)
         nc.scalar.activation(out=em[:], in_=tot[:, 0:1], func=ACT.Sqrt, scale=1.0 / (N_TOK * N_TOK))
         nc.gpsimd.tensor_scalar(out=ema[:], in0=em[:], scalar1=0.05, scalar2=0.95, op0=ALU.mult, op1=ALU.add)
         nc.gpsimd.tensor_scalar(out=emc[:], in0=ema[:], scalar1=1e-8, scalar2=None, op0=ALU.max)
-        act_m(0)
-        act_l(0)
-        stage1(3)
-        dhcopy(3)
-        gw1 = interleave("v", w_raw[1][:])
+        xmul(0)
+        quantize(gx1, x_codes, x_scales, D)
         nc.vector.reciprocal(out=rec[:], in_=emc[:])
-        quantize(gw1, w_codes, w_scales, HL)
         nc.gpsimd.tensor_scalar(out=sgv[:], in0=rec[:], scalar1=em[:, 0:1], scalar2=3.0, op0=ALU.mult, op1=ALU.min)
         nc.gpsimd.tensor_scalar(out=sgs[:], in0=sgv[:], scalar1=1.0 / N_TOK, scalar2=None, op0=ALU.mult)
-        gx0 = interleave("v", x_raw[0][:].rearrange("p (j d) -> p j d", j=PACK))
-        gx1 = interleave("v", x_raw[1][:].rearrange("p (j d) -> p j d", j=PACK))
-        quantize(gx0, x_codes, x_scales, 0)
-        quantize(gx1, x_codes, x_scales, D)
-        act_m(1)
-        act_l(1)
-        bmul(0)
 
+        acts = {
+            0: (("sig", 1), ("sig", 2), ("sig", 3)),
+            1: (("silu", 2), ("silu", 3)),
+            2: (("silu", 4), ("sig", 4)),
+            3: (("sig", 5), ("sig", 6), ("sig", 7)),
+            4: (("silu", 5), ("silu", 6)),
+            5: (("silu", 7),),
+        }
         gw_late = {}
         for u in range(3):
             stage1(u)
@@ -337,36 +331,33 @@ def tile_continuummemorysystem_pa_kernel(tc, err, W_down, gate_pre, up_pre, x_pr
             if more:
                 stage1(u0 + 7)
                 dhcopy(u0 + 7)
+            for func, slab in acts.get(b, ()):
+                if func == "sig":
+                    act_sig(slab)
+                else:
+                    act_l(slab)
             if b >= 1:
                 evac("s", ht0 - 1, 0)
                 evac("s", ht0 - 1, 1)
-            if b == 3:
-                act_sig(7)
-            if b + 2 < N_HB:
-                act_m(b + 2)
-                act_l(b + 2)
-            if b == 2:
-                act_sig(4)
             for i in range(3):
                 pmul(u0 + i)
                 if more:
                     stage1(u0 + 4 + i)
             pquant(ht0)
             stage2(ht0)
-            if b < 2:
-                xmul(b + 2)
-            if 4 <= b + 1 < N_HB:
-                xmul(b + 1)
+            if b == 0:
+                gw1 = interleave("v", w_raw[1][:])
+            if more:
+                fmul(b + 1)
             if b in (2, 4):
                 quantize(gw_late[1 + b // 2], w_codes, w_scales, (1 + b // 2) * HL)
             pquant(ht1)
             stage2(ht1)
             if more:
-                bmul(b + 1)
+                xmul(b + 1)
+            if b == 0:
+                quantize(gw1, w_codes, w_scales, HL)
             evac("s", ht0, 0)
             evac("s", ht0, 1)
-            if b == 2:
-                act_sig(5)
-                act_sig(6)
         evac("s", N_HT - 1, 0)
         evac("v", N_HT - 1, 1)

@@ -43,7 +43,7 @@ def tile_continuummemorysystem_pa_kernel(tc, err, W_down, gate_pre, up_pre, x_pr
         psum = ctx.enter_context(tc.psum_pool(name="psum", bufs=4))
 
         gate_sb = [keep.tile([P, G * PACK, HL], BF16, name="gate%d" % c, tag="gate%d" % c) for c in range(N_HL)]
-        up_sb = [keep.tile([P, G * PACK, HL], BF16, name="up%d" % c, tag="up%d" % c) for c in range(N_HL)]
+        up_sb = [keep.tile([P, 2, NQ, HB], BF16, name="up%d" % b, tag="up%d" % b) for b in range(N_HB)]
         w_codes = keep.tile([P, H], U32, name="w_codes", tag="w_codes", align_bytes=64)
         w_scales = keep.tile([P, H], U8, name="w_scales", tag="w_scales", align_bytes=64)
         e_codes = keep.tile([P, N_TOK], U32, name="e_codes", tag="e_codes", align_bytes=64)
@@ -80,6 +80,14 @@ def tile_continuummemorysystem_pa_kernel(tc, err, W_down, gate_pre, up_pre, x_pr
                     in_=src[g * K_PASS:(g + 1) * K_PASS, c * HL + lo:c * HL + hi].rearrange("(p t) h -> p t h", t=PACK),
                 )
 
+        def load_up(b):
+            for g in range(G):
+                for e in range(2):
+                    nc.sync.dma_start(
+                        out=up_sb[b][:, e, 2 * g:2 * g + 2, :],
+                        in_=up_pre[g * K_PASS + e:(g + 1) * K_PASS:2, b * HB:(b + 1) * HB].rearrange("(p s) h -> p s h", s=2),
+                    )
+
         w_raw, e_raw, x_raw = {}, {}, {}
         load_act(gate_sb, gate_pre, 0, 0, HB)
         w_raw[0] = load_w(0)
@@ -87,7 +95,8 @@ def tile_continuummemorysystem_pa_kernel(tc, err, W_down, gate_pre, up_pre, x_pr
         e_raw[0] = load_rows(err, 0)
         e_raw[1] = load_rows(err, 1)
         x_raw[1] = load_rows(x_pred, 1)
-        load_act(up_sb, up_pre, 0)
+        load_up(0)
+        load_up(1)
         load_act(gate_sb, gate_pre, 0, HB, HL)
         load_act(gate_sb, gate_pre, 1)
 
@@ -144,87 +153,73 @@ def tile_continuummemorysystem_pa_kernel(tc, err, W_down, gate_pre, up_pre, x_pr
             )
 
         def xmul(b):
-            c, off = divmod(b * HB, HL)
-            for q in range(NQ):
-                nc.vector.scalar_tensor_tensor(
-                    out=sx[b][:, q, :, :], in0=sx[b][:, q, :, :], scalar=1.0,
-                    in1=up_sb[c][:, 2 * q:2 * q + 2, off:off + HB].rearrange("p e h -> p h e"),
-                    op0=ALU.add, op1=ALU.mult,
-                )
+            pairs = sx[b][:].rearrange("p q h e -> p (q h) e")
+            nc.vector.scalar_tensor_tensor(
+                out=pairs, in0=pairs, scalar=1.0, in1=up_sb[b][:].rearrange("p e q h -> p (q h) e"),
+                op0=ALU.add, op1=ALU.mult,
+            )
 
-        dh = {}
+        dh, dhs, pq, pc, ps, acc = {}, {}, {}, {}, {}, {}
+        banks = {"A": (0, 0, HB), "B": (1, 0, HT), "C": (1, HT, HT)}
 
-        def stage1(u):
-            ht, g = divmod(u, G)
-            dh[u] = psum.tile([P, PACK, HT], BANK_DT, name="dh", tag="dh")
+        def stage1(b, k):
+            g, h0, nh = banks[k]
+            dh[b, k] = psum.tile([P, PACK, nh], BANK_DT, name="dh", tag="dh")
             for t in range(PACK):
                 lo = g * K_PASS + t * P
                 nc.tensor.matmul_mx(
-                    out=dh[u][:, t, :],
+                    out=dh[b, k][:, t, :],
                     lhsT=e_codes[:, lo:lo + P].bitcast(FP8X4),
                     lhsT_scale=e_scales[:, lo:lo + P],
-                    rhs=w_codes[:, ht * HT:(ht + 1) * HT].bitcast(FP8X4),
-                    rhs_scale=w_scales[:, ht * HT:(ht + 1) * HT],
+                    rhs=w_codes[:, b * HB + h0:b * HB + h0 + nh].bitcast(FP8X4),
+                    rhs_scale=w_scales[:, b * HB + h0:b * HB + h0 + nh],
                     start=True, stop=True,
                 )
 
-        pq, dhs = {}, {}
+        def new_pq(b):
+            pq[b] = prod.tile([P, 2, G, HB * PACK], BF16, name="pq", tag="pq", bufs=2, align_bytes=64)
 
-        def new_pq(ht):
-            pq[ht] = prod.tile([P, 2, G, HT * PACK], BF16, name="pq", tag="pq", align_bytes=64)
+        def product(engine, b, k, a, bank):
+            g, h0, nh = banks[k]
+            factor = (lt[b], sx[b])[a]
+            engine.tensor_tensor(
+                out=pq[b][:, a, g, h0 * PACK:(h0 + nh) * PACK].rearrange("p (h s e) -> p h s e", s=2, e=2),
+                in0=bank,
+                in1=factor[:, 2 * g:2 * g + 2, h0:h0 + nh, :].rearrange("p s h e -> p h s e"), op=ALU.mult,
+            )
 
-        def pmul(u):
-            ht, g = divmod(u, G)
-            b, hl = divmod(ht, HB // HT)
-            bank = dh[u][:].rearrange("p (s e) h -> p h s e", e=2)
-            cols = slice(hl * HT, (hl + 1) * HT)
-            prs = slice(2 * g, 2 * g + 2)
-            for a, factor in ((0, lt[b]), (1, sx[b])):
-                nc.vector.tensor_tensor(
-                    out=pq[ht][:, a, g, :].rearrange("p (h s e) -> p h s e", s=2, e=2),
-                    in0=bank, in1=factor[:, prs, cols, :].rearrange("p s h e -> p h s e"), op=ALU.mult,
-                )
+        def pmul(b, k, a):
+            product(nc.vector, b, k, a, dh[b, k][:].rearrange("p (s e) h -> p h s e", e=2))
 
-        def dhcopy(u):
-            dhs[u] = prod.tile([P, HT * PACK], BANK_DT, name="dhs", tag="dhs", bufs=2)
+        def dhcopy(b):
+            dhs[b] = prod.tile([P, HT * PACK], BANK_DT, name="dhs", tag="dhs", bufs=2)
             nc.scalar.copy(
-                out=dhs[u][:].rearrange("p (h t) -> p h t", t=PACK),
-                in_=dh[u][:].rearrange("p t h -> p h t"),
+                out=dhs[b][:].rearrange("p (h t) -> p h t", t=PACK),
+                in_=dh[b, "C"][:].rearrange("p t h -> p h t"),
             )
 
-        def gp_pmul(u):
-            ht, g = divmod(u, G)
-            b, hl = divmod(ht, HB // HT)
-            bank = dhs[u][:].rearrange("p (h s e) -> p h s e", s=2, e=2)
-            cols = slice(hl * HT, (hl + 1) * HT)
-            prs = slice(2 * g, 2 * g + 2)
-            for a, factor in ((1, sx[b]), (0, lt[b])):
-                nc.gpsimd.tensor_tensor(
-                    out=pq[ht][:, a, g, :].rearrange("p (h s e) -> p h s e", s=2, e=2),
-                    in0=bank, in1=factor[:, prs, cols, :].rearrange("p s h e -> p h s e"), op=ALU.mult,
-                )
-
-        pc, ps = {}, {}
-
-        def pquant(ht):
-            pc[ht] = prod.tile([P, 2 * G * HT], U32, name="pc", tag="pc", align_bytes=64)
-            ps[ht] = prod.tile([P, 2 * G * HT], U8, name="ps", tag="ps", align_bytes=64)
-            nc.vector.quantize_mx(
-                out=pc[ht][:].bitcast(FP8X4), scales=ps[ht][:],
-                in_=pq[ht][:].rearrange("p a g c -> p (a g c)"),
-            )
-
-        acc = {}
-
-        def stage2(ht):
+        def gp_pmul(b):
             for a in range(2):
+                product(nc.gpsimd, b, "C", a, dhs[b][:].rearrange("p (h s e) -> p h s e", s=2, e=2))
+
+        def pquant(b, a):
+            pc[b, a] = prod.tile([P, G * HB], U32, name="pc", tag="pc", align_bytes=64)
+            ps[b, a] = prod.tile([P, G * HB], U8, name="ps", tag="ps", align_bytes=64)
+            nc.vector.quantize_mx(
+                out=pc[b, a][:].bitcast(FP8X4), scales=ps[b, a][:],
+                in_=pq[b][:, a, :, :].rearrange("p g c -> p (g c)"),
+            )
+
+        def stage2(b, a):
+            for hl in range(HB // HT):
+                ht = b * (HB // HT) + hl
                 acc[ht, a] = psum.tile([P, D], F32, name="acc", tag="acc")
                 for g in range(G):
-                    lo = (a * G + g) * HT
+                    lo = g * HB + hl * HT
                     nc.tensor.matmul_mx(
                         out=acc[ht, a][:],
-                        lhsT=pc[ht][:, lo:lo + HT].bitcast(FP8X4),
-                        lhsT_scale=ps[ht][:, lo:lo + HT],
+                        lhsT=pc[b, a][:, lo:lo + HT].bitcast(FP8X4),
+                        lhsT_scale=ps[b, a][:, lo:lo + HT],
                         rhs=x_codes[:, g * D:(g + 1) * D].bitcast(FP8X4),
                         rhs_scale=x_scales[:, g * D:(g + 1) * D],
                         start=(g == 0), stop=(g == G - 1),
@@ -247,9 +242,11 @@ def tile_continuummemorysystem_pa_kernel(tc, err, W_down, gate_pre, up_pre, x_pr
         quantize(gw0, w_codes, w_scales, 0)
         gx0 = interleave("v", x_raw[0][:].rearrange("p (j d) -> p j d", j=PACK))
         w_raw[2] = load_w(2)
-        load_act(up_sb, up_pre, 1)
+        load_up(2)
+        load_up(3)
         load_act(gate_sb, gate_pre, 2)
-        load_act(up_sb, up_pre, 2)
+        load_up(4)
+        load_up(5)
 
         e_grp = {}
         for g in range(G):
@@ -283,7 +280,8 @@ def tile_continuummemorysystem_pa_kernel(tc, err, W_down, gate_pre, up_pre, x_pr
                     i_mm += 1
         w_raw[3] = load_w(3)
         load_act(gate_sb, gate_pre, 3)
-        load_act(up_sb, up_pre, 3)
+        load_up(6)
+        load_up(7)
         fmul(0)
         for g in range(G):
             quantize(e_grp[g], e_codes, e_scales, g * K_PASS)
@@ -294,16 +292,13 @@ def tile_continuummemorysystem_pa_kernel(tc, err, W_down, gate_pre, up_pre, x_pr
         tot = psum.tile([P, 2], F32, name="tot", tag="acc")
         nc.tensor.matmul(out=tot[:], lhsT=ones[:], rhs=ssq[:], start=True, stop=True)
         act_l(1)
-        stage1(3)
-        dhcopy(3)
+        stage1(0, "C")
+        dhcopy(0)
         nc.scalar.activation(out=em[:], in_=tot[:, 0:1], func=ACT.Sqrt, scale=1.0 / (N_TOK * N_TOK))
         nc.gpsimd.tensor_scalar(out=ema[:], in0=em[:], scalar1=0.05, scalar2=0.95, op0=ALU.mult, op1=ALU.add)
         nc.gpsimd.tensor_scalar(out=emc[:], in0=ema[:], scalar1=1e-8, scalar2=None, op0=ALU.max)
         xmul(0)
         quantize(gx1, x_codes, x_scales, D)
-        nc.vector.reciprocal(out=rec[:], in_=emc[:])
-        nc.gpsimd.tensor_scalar(out=sgv[:], in0=rec[:], scalar1=em[:, 0:1], scalar2=3.0, op0=ALU.mult, op1=ALU.min)
-        nc.gpsimd.tensor_scalar(out=sgs[:], in0=sgv[:], scalar1=1.0 / N_TOK, scalar2=None, op0=ALU.mult)
 
         acts = {
             0: (("sig", 1), ("sig", 2), ("sig", 3)),
@@ -314,50 +309,53 @@ def tile_continuummemorysystem_pa_kernel(tc, err, W_down, gate_pre, up_pre, x_pr
             5: (("silu", 7),),
         }
         gw_late = {}
-        for u in range(3):
-            stage1(u)
+        stage1(0, "A")
+        stage1(0, "B")
         for b in range(N_HB):
-            u0 = 4 * b
-            ht0, ht1 = 2 * b, 2 * b + 1
+            ht0 = b * (HB // HT)
             more = b + 1 < N_HB
-            new_pq(ht0)
-            new_pq(ht1)
-            gp_pmul(u0 + 3)
+            new_pq(b)
+            gp_pmul(b)
             if b < 4:
                 c_late, half = 2 + b // 2, b % 2
                 if half == 0:
                     gw_late[c_late] = grp.tile([P, HL * PACK], BF16, name="grouped", tag="grouped", align_bytes=64)
                 interleave_half(gw_late[c_late], w_raw[c_late], half)
             if more:
-                stage1(u0 + 7)
-                dhcopy(u0 + 7)
-            for func, slab in acts.get(b, ()):
+                stage1(b + 1, "C")
+            for i, (func, slab) in enumerate(acts.get(b, (("none", 0),))):
                 if func == "sig":
                     act_sig(slab)
-                else:
+                elif func == "silu":
                     act_l(slab)
+                if i == 0 and more:
+                    dhcopy(b + 1)
             if b >= 1:
-                evac("s", ht0 - 1, 0)
+                evac("s", ht0 - 2, 1)
                 evac("s", ht0 - 1, 1)
-            for i in range(3):
-                pmul(u0 + i)
-                if more:
-                    stage1(u0 + 4 + i)
-            pquant(ht0)
-            stage2(ht0)
+            for a in range(2):
+                for k in ("A", "B"):
+                    pmul(b, k, a)
+                    if more and a == 1:
+                        stage1(b + 1, k)
+            pquant(b, 0)
+            stage2(b, 0)
             if b == 0:
+                nc.vector.reciprocal(out=rec[:], in_=emc[:])
+                nc.gpsimd.tensor_scalar(out=sgv[:], in0=rec[:], scalar1=em[:, 0:1], scalar2=3.0, op0=ALU.mult, op1=ALU.min)
+                nc.gpsimd.tensor_scalar(out=sgs[:], in0=sgv[:], scalar1=1.0 / N_TOK, scalar2=None, op0=ALU.mult)
                 gw1 = interleave("v", w_raw[1][:])
             if more:
                 fmul(b + 1)
-            if b in (2, 4):
-                quantize(gw_late[1 + b // 2], w_codes, w_scales, (1 + b // 2) * HL)
-            pquant(ht1)
-            stage2(ht1)
-            if more:
-                xmul(b + 1)
             if b == 0:
                 quantize(gw1, w_codes, w_scales, HL)
+            if b in (2, 4):
+                quantize(gw_late[1 + b // 2], w_codes, w_scales, (1 + b // 2) * HL)
+            pquant(b, 1)
+            stage2(b, 1)
+            if more:
+                xmul(b + 1)
             evac("s", ht0, 0)
-            evac("s", ht0, 1)
-        evac("s", N_HT - 1, 0)
+            evac("s", ht0 + 1, 0)
+        evac("s", N_HT - 2, 1)
         evac("v", N_HT - 1, 1)

@@ -51,6 +51,7 @@ def tile_continuummemorysystem_pa_kernel(tc, err, W_down, gate_pre, up_pre, x_pr
         x_codes = keep.tile([P, G * D], U32, name="x_codes", tag="x_codes", align_bytes=64)
         x_scales = keep.tile([P, G * D], U8, name="x_scales", tag="x_scales", align_bytes=64)
         ident = keep.tile([P, P], F32, name="ident", tag="ident")
+        ident_bf = keep.tile([P, P], BF16, name="ident_bf", tag="ident_bf")
         ones = keep.tile([P, P], F32, name="ones", tag="ones")
         diag = keep.tile([P, P], F32, name="diag", tag="diag")
         ssq = keep.tile([P, 2], F32, name="ssq", tag="ssq")
@@ -105,6 +106,7 @@ def tile_continuummemorysystem_pa_kernel(tc, err, W_down, gate_pre, up_pre, x_pr
         make_identity(nc, ident[:])
         nc.gpsimd.memset(ones[:], 1.0)
         nc.gpsimd.memset(ssq[:], 0.0)
+        make_identity(nc, ident_bf[:])
 
         def interleave(engine, src3):
             t = grp.tile([P, HL * PACK], BF16, name="grouped", tag="grouped", align_bytes=64)
@@ -152,19 +154,30 @@ def tile_continuummemorysystem_pa_kernel(tc, err, W_down, gate_pre, up_pre, x_pr
                 op0=ALU.subtract, op1=ALU.mult,
             )
 
-        def xmul(b):
-            pairs = sx[b][:].rearrange("p q h e -> p (q h) e")
-            nc.vector.scalar_tensor_tensor(
-                out=pairs, in0=pairs, scalar=1.0, in1=up_sb[b][:].rearrange("p e q h -> p (q h) e"),
-                op0=ALU.add, op1=ALU.mult,
-            )
+        ups = {}
+
+        def upmm(b):
+            ups[b] = psum.tile([P, 2, 2 * HB], BF16, name="ups", tag="ups", bufs=1)
+            for e in range(2):
+                nc.tensor.matmul(
+                    out=ups[b][:, e, :], lhsT=ident_bf[:],
+                    rhs=up_sb[b][:, e, 0:2, :].rearrange("p s h -> p (s h)"), start=True, stop=True,
+                )
+
+        def xmul(b, g):
+            pairs = sx[b][:, 2 * g:2 * g + 2, :, :].rearrange("p s h e -> p (s h) e")
+            if g == 0:
+                up_half = ups[b][:].rearrange("p e n -> p n e")
+            else:
+                up_half = up_sb[b][:, :, 2:4, :].rearrange("p e s h -> p (s h) e")
+            nc.vector.scalar_tensor_tensor(out=pairs, in0=pairs, scalar=1.0, in1=up_half, op0=ALU.add, op1=ALU.mult)
 
         dh, dhs, pq, pc, ps, acc = {}, {}, {}, {}, {}, {}
         banks = {"A": (0, 0, HB), "B": (1, 0, HT), "C": (1, HT, HT)}
 
         def stage1(b, k):
             g, h0, nh = banks[k]
-            dh[b, k] = psum.tile([P, PACK, nh], BANK_DT, name="dh", tag="dh")
+            dh[b, k] = psum.tile([P, PACK, nh], BANK_DT, name="dh", tag="dh", bufs=3)
             for t in range(PACK):
                 lo = g * K_PASS + t * P
                 nc.tensor.matmul_mx(
@@ -177,7 +190,7 @@ def tile_continuummemorysystem_pa_kernel(tc, err, W_down, gate_pre, up_pre, x_pr
                 )
 
         def new_pq(b):
-            pq[b] = prod.tile([P, 2, G, HB * PACK], BF16, name="pq", tag="pq", bufs=2, align_bytes=64)
+            pq[b] = prod.tile([P, 2, G, HB * PACK], BF16, name="pq", tag="pq", bufs=1, align_bytes=64)
 
         def product(engine, b, k, a, bank):
             g, h0, nh = banks[k]
@@ -254,7 +267,7 @@ def tile_continuummemorysystem_pa_kernel(tc, err, W_down, gate_pre, up_pre, x_pr
             e_grp[g] = grp.tile([P, HL * PACK], BF16, name="e_grouped", tag="grouped", align_bytes=64)
             egw = e_grp[g][:].bitcast(F32).rearrange("p (t m u) -> p t m u", t=PACK, u=2)
             for half in range(2):
-                xt = psum.tile([P, PACK, P], F32, name="xt", tag="dh")
+                xt = psum.tile([P, PACK, P], F32, name="xt", tag="dh", bufs=3)
                 for tt in range(2):
                     t = 2 * half + tt
                     for u in range(2):
@@ -278,6 +291,7 @@ def tile_continuummemorysystem_pa_kernel(tc, err, W_down, gate_pre, up_pre, x_pr
                     blk = e_raw[g][:, t * D + fb * P:t * D + (fb + 1) * P]
                     nc.tensor.matmul(out=gram[:], lhsT=blk, rhs=blk, start=(i_mm == 0), stop=(i_mm == n_mm - 1))
                     i_mm += 1
+        upmm(0)
         w_raw[3] = load_w(3)
         load_act(gate_sb, gate_pre, 3)
         load_up(6)
@@ -297,8 +311,9 @@ def tile_continuummemorysystem_pa_kernel(tc, err, W_down, gate_pre, up_pre, x_pr
         nc.scalar.activation(out=em[:], in_=tot[:, 0:1], func=ACT.Sqrt, scale=1.0 / (N_TOK * N_TOK))
         nc.gpsimd.tensor_scalar(out=ema[:], in0=em[:], scalar1=0.05, scalar2=0.95, op0=ALU.mult, op1=ALU.add)
         nc.gpsimd.tensor_scalar(out=emc[:], in0=ema[:], scalar1=1e-8, scalar2=None, op0=ALU.max)
-        xmul(0)
+        xmul(0, 1)
         quantize(gx1, x_codes, x_scales, D)
+        xmul(0, 0)
 
         acts = {
             0: (("sig", 1), ("sig", 2), ("sig", 3)),
@@ -323,6 +338,7 @@ def tile_continuummemorysystem_pa_kernel(tc, err, W_down, gate_pre, up_pre, x_pr
                 interleave_half(gw_late[c_late], w_raw[c_late], half)
             if more:
                 stage1(b + 1, "C")
+                upmm(b + 1)
             for i, (func, slab) in enumerate(acts.get(b, (("none", 0),))):
                 if func == "sig":
                     act_sig(slab)
@@ -338,8 +354,6 @@ def tile_continuummemorysystem_pa_kernel(tc, err, W_down, gate_pre, up_pre, x_pr
                     pmul(b, k, a)
                     if more and a == 1:
                         stage1(b + 1, k)
-            pquant(b, 0)
-            stage2(b, 0)
             if b == 0:
                 nc.vector.reciprocal(out=rec[:], in_=emc[:])
                 nc.gpsimd.tensor_scalar(out=sgv[:], in0=rec[:], scalar1=em[:, 0:1], scalar2=3.0, op0=ALU.mult, op1=ALU.min)
@@ -347,14 +361,18 @@ def tile_continuummemorysystem_pa_kernel(tc, err, W_down, gate_pre, up_pre, x_pr
                 gw1 = interleave("v", w_raw[1][:])
             if more:
                 fmul(b + 1)
+            pquant(b, 0)
+            stage2(b, 0)
             if b == 0:
                 quantize(gw1, w_codes, w_scales, HL)
             if b in (2, 4):
                 quantize(gw_late[1 + b // 2], w_codes, w_scales, (1 + b // 2) * HL)
+            if more:
+                xmul(b + 1, 1)
             pquant(b, 1)
             stage2(b, 1)
             if more:
-                xmul(b + 1)
+                xmul(b + 1, 0)
             evac("s", ht0, 0)
             evac("s", ht0 + 1, 0)
         evac("s", N_HT - 2, 1)

@@ -27,6 +27,7 @@ HL = 512
 N_HL = H // HL
 NQ = G * PACK // 2
 BANK_DT = BF16
+GP_MORE = 4
 
 
 def tile_continuummemorysystem_pa_kernel(tc, err, W_down, gate_pre, up_pre, x_pred, out_0, out_1):
@@ -39,7 +40,7 @@ def tile_continuummemorysystem_pa_kernel(tc, err, W_down, gate_pre, up_pre, x_pr
         grp = ctx.enter_context(tc.tile_pool(name="grp", bufs=4))
         elem = ctx.enter_context(tc.tile_pool(name="elem", bufs=3))
         prod = ctx.enter_context(tc.tile_pool(name="prod", bufs=3))
-        stage = ctx.enter_context(tc.tile_pool(name="stage", bufs=4))
+        stage = ctx.enter_context(tc.tile_pool(name="stage", bufs=8))
         psum = ctx.enter_context(tc.psum_pool(name="psum", bufs=4))
 
         gate_sb = [keep.tile([P, G * PACK, HL], BF16, name="gate%d" % c, tag="gate%d" % c) for c in range(N_HL)]
@@ -95,10 +96,10 @@ def tile_continuummemorysystem_pa_kernel(tc, err, W_down, gate_pre, up_pre, x_pr
         x_raw[0] = load_rows(x_pred, 0)
         e_raw[0] = load_rows(err, 0)
         e_raw[1] = load_rows(err, 1)
+        load_act(gate_sb, gate_pre, 0, HB, HL)
         x_raw[1] = load_rows(x_pred, 1)
         load_up(0)
         load_up(1)
-        load_act(gate_sb, gate_pre, 0, HB, HL)
         load_act(gate_sb, gate_pre, 1)
 
         nc.gpsimd.memset(warm_in[:], 0.0)
@@ -139,18 +140,20 @@ def tile_continuummemorysystem_pa_kernel(tc, err, W_down, gate_pre, up_pre, x_pr
 
         sx, lt = {}, {}
 
-        def act_sig(b):
-            sx[b] = elem.tile([P, NQ, HB, 2], F32, name="sx", tag="sx", bufs=5)
-            nc.scalar.activation(out=sx[b][:], in_=gate_pairs(b), func=ACT.Sigmoid, scale=-1.0)
+        def act_sig(b, q_lo=0, q_hi=NQ):
+            if q_lo == 0:
+                sx[b] = elem.tile([P, NQ, HB, 2], F32, name="sx", tag="sx", bufs=5)
+            nc.scalar.activation(out=sx[b][:, q_lo:q_hi, :, :], in_=gate_pairs(b)[:, q_lo:q_hi, :, :], func=ACT.Sigmoid, scale=-1.0)
 
-        def act_l(b):
-            lt[b] = elem.tile([P, NQ, HB, 2], F32, name="lt", tag="lt")
-            nc.scalar.activation(out=lt[b][:], in_=gate_pairs(b), func=ACT.Silu)
+        def act_l(b, q_lo=0, q_hi=NQ):
+            if q_lo == 0:
+                lt[b] = elem.tile([P, NQ, HB, 2], F32, name="lt", tag="lt")
+            nc.scalar.activation(out=lt[b][:, q_lo:q_hi, :, :], in_=gate_pairs(b)[:, q_lo:q_hi, :, :], func=ACT.Silu)
 
-        def fmul(b):
-            flat = sx[b][:].rearrange("p q h e -> p (q h e)")
+        def fmul(b, q_lo=0, q_hi=NQ):
+            flat = sx[b][:, q_lo:q_hi, :, :].rearrange("p q h e -> p (q h e)")
             nc.vector.scalar_tensor_tensor(
-                out=flat, in0=lt[b][:].rearrange("p q h e -> p (q h e)"), scalar=1.0, in1=flat,
+                out=flat, in0=lt[b][:, q_lo:q_hi, :, :].rearrange("p q h e -> p (q h e)"), scalar=1.0, in1=flat,
                 op0=ALU.subtract, op1=ALU.mult,
             )
 
@@ -204,16 +207,19 @@ def tile_continuummemorysystem_pa_kernel(tc, err, W_down, gate_pre, up_pre, x_pr
         def pmul(b, k, a):
             product(nc.vector, b, k, a, dh[b, k][:].rearrange("p (s e) h -> p h s e", e=2))
 
-        def dhcopy(b):
-            dhs[b] = prod.tile([P, HT * PACK], BANK_DT, name="dhs", tag="dhs", bufs=2)
+        def dhcopy(b, k):
+            dhs[b, k] = prod.tile([P, HT * PACK], BANK_DT, name="dhs", tag="dhs", bufs=4)
             nc.scalar.copy(
-                out=dhs[b][:].rearrange("p (h t) -> p h t", t=PACK),
-                in_=dh[b, "C"][:].rearrange("p t h -> p h t"),
+                out=dhs[b, k][:].rearrange("p (h t) -> p h t", t=PACK),
+                in_=dh[b, k][:].rearrange("p t h -> p h t"),
             )
 
         def gp_pmul(b):
-            for a in range(2):
-                product(nc.gpsimd, b, "C", a, dhs[b][:].rearrange("p (h s e) -> p h s e", s=2, e=2))
+            todo = [("C", 0), ("C", 1)]
+            if b >= GP_MORE:
+                todo.append(("B", 1))
+            for k, a in todo:
+                product(nc.gpsimd, b, k, a, dhs[b, k][:].rearrange("p (h s e) -> p h s e", s=2, e=2))
 
         def pquant(b, a):
             pc[b, a] = prod.tile([P, G * HB], U32, name="pc", tag="pc", align_bytes=64)
@@ -248,12 +254,15 @@ def tile_continuummemorysystem_pa_kernel(tc, err, W_down, gate_pre, up_pre, x_pr
 
         ctx.enter_context(tc.manual_schedule(engines={ENG.Activation, ENG.DVE, ENG.Pool}))
 
-        act_sig(0)
+        act_sig(0, 0, 2)
+        act_sig(0, 2, 4)
         gw0 = interleave("v", w_raw[0][:])
         w_raw[1] = load_w(1)
-        act_l(0)
-        quantize(gw0, w_codes, w_scales, 0)
+        act_l(0, 0, 2)
+        act_l(0, 2, 4)
         gx0 = interleave("v", x_raw[0][:].rearrange("p (j d) -> p j d", j=PACK))
+        quantize(gw0, w_codes, w_scales, 0)
+        quantize(gx0, x_codes, x_scales, 0)
         w_raw[2] = load_w(2)
         load_up(2)
         load_up(3)
@@ -280,8 +289,6 @@ def tile_continuummemorysystem_pa_kernel(tc, err, W_down, gate_pre, up_pre, x_pr
                     out=egw[:, 2 * half:2 * half + 2, :, :],
                     in_=xt[:].rearrange("p (tt u) m -> p tt m u", u=2),
                 )
-        gx1 = interleave("v", x_raw[1][:].rearrange("p (j d) -> p j d", j=PACK))
-        quantize(gx0, x_codes, x_scales, 0)
         gram = psum.tile([P, P], F32, name="gram", tag="acc")
         n_mm = G * PACK * (D // P)
         i_mm = 0
@@ -291,12 +298,12 @@ def tile_continuummemorysystem_pa_kernel(tc, err, W_down, gate_pre, up_pre, x_pr
                     blk = e_raw[g][:, t * D + fb * P:t * D + (fb + 1) * P]
                     nc.tensor.matmul(out=gram[:], lhsT=blk, rhs=blk, start=(i_mm == 0), stop=(i_mm == n_mm - 1))
                     i_mm += 1
-        upmm(0)
         w_raw[3] = load_w(3)
         load_act(gate_sb, gate_pre, 3)
         load_up(6)
         load_up(7)
-        fmul(0)
+        fmul(0, 0, 2)
+        fmul(0, 2, 4)
         for g in range(G):
             quantize(e_grp[g], e_codes, e_scales, g * K_PASS)
         nc.vector.scalar_tensor_tensor(
@@ -306,23 +313,28 @@ def tile_continuummemorysystem_pa_kernel(tc, err, W_down, gate_pre, up_pre, x_pr
         tot = psum.tile([P, 2], F32, name="tot", tag="acc")
         nc.tensor.matmul(out=tot[:], lhsT=ones[:], rhs=ssq[:], start=True, stop=True)
         act_l(1)
-        stage1(0, "C")
-        dhcopy(0)
         nc.scalar.activation(out=em[:], in_=tot[:, 0:1], func=ACT.Sqrt, scale=1.0 / (N_TOK * N_TOK))
         nc.gpsimd.tensor_scalar(out=ema[:], in0=em[:], scalar1=0.05, scalar2=0.95, op0=ALU.mult, op1=ALU.add)
         nc.gpsimd.tensor_scalar(out=emc[:], in0=ema[:], scalar1=1e-8, scalar2=None, op0=ALU.max)
+        stage1(0, "C")
+        dhcopy(0, "C")
+        upmm(0)
+        gx1 = interleave("v", x_raw[1][:].rearrange("p (j d) -> p j d", j=PACK))
         xmul(0, 1)
         quantize(gx1, x_codes, x_scales, D)
+        nc.vector.reciprocal(out=rec[:], in_=emc[:])
+        nc.gpsimd.tensor_scalar(out=sgv[:], in0=rec[:], scalar1=em[:, 0:1], scalar2=3.0, op0=ALU.mult, op1=ALU.min)
+        nc.gpsimd.tensor_scalar(out=sgs[:], in0=sgv[:], scalar1=1.0 / N_TOK, scalar2=None, op0=ALU.mult)
         xmul(0, 0)
 
         acts = {
             0: (("sig", 1), ("sig", 2), ("sig", 3)),
-            1: (("silu", 2), ("silu", 3)),
-            2: (("silu", 4), ("sig", 4)),
-            3: (("sig", 5), ("sig", 6), ("sig", 7)),
-            4: (("silu", 5), ("silu", 6)),
-            5: (("silu", 7),),
+            1: (("silu", 3),),
+            2: (("sig", 4), ("sig", 5)),
+            3: (("sig", 7),),
+            4: (("silu", 6),),
         }
+        acts_late = {0: ("silu", 2), 1: ("silu", 4), 2: ("sig", 6), 3: ("silu", 5), 4: ("silu", 7)}
         gw_late = {}
         stage1(0, "A")
         stage1(0, "B")
@@ -345,24 +357,30 @@ def tile_continuummemorysystem_pa_kernel(tc, err, W_down, gate_pre, up_pre, x_pr
                 elif func == "silu":
                     act_l(slab)
                 if i == 0 and more:
-                    dhcopy(b + 1)
+                    dhcopy(b + 1, "C")
             if b >= 1:
                 evac("s", ht0 - 2, 1)
                 evac("s", ht0 - 1, 1)
-            for a in range(2):
-                for k in ("A", "B"):
-                    pmul(b, k, a)
-                    if more and a == 1:
-                        stage1(b + 1, k)
+            pmul(b, "A", 0)
+            pmul(b, "B", 0)
+            if not more:
+                pquant(b, 0)
+                stage2(b, 0)
+            pmul(b, "A", 1)
+            if more:
+                stage1(b + 1, "A")
+            if b < GP_MORE:
+                pmul(b, "B", 1)
+            if more:
+                stage1(b + 1, "B")
+                if b + 1 >= GP_MORE:
+                    dhcopy(b + 1, "B")
             if b == 0:
-                nc.vector.reciprocal(out=rec[:], in_=emc[:])
-                nc.gpsimd.tensor_scalar(out=sgv[:], in0=rec[:], scalar1=em[:, 0:1], scalar2=3.0, op0=ALU.mult, op1=ALU.min)
-                nc.gpsimd.tensor_scalar(out=sgs[:], in0=sgv[:], scalar1=1.0 / N_TOK, scalar2=None, op0=ALU.mult)
                 gw1 = interleave("v", w_raw[1][:])
             if more:
                 fmul(b + 1)
-            pquant(b, 0)
-            stage2(b, 0)
+                pquant(b, 0)
+                stage2(b, 0)
             if b == 0:
                 quantize(gw1, w_codes, w_scales, HL)
             if b in (2, 4):
@@ -373,6 +391,12 @@ def tile_continuummemorysystem_pa_kernel(tc, err, W_down, gate_pre, up_pre, x_pr
             stage2(b, 1)
             if more:
                 xmul(b + 1, 0)
+            if b in acts_late:
+                func, slab = acts_late[b]
+                if func == "sig":
+                    act_sig(slab)
+                else:
+                    act_l(slab)
             evac("s", ht0, 0)
             evac("s", ht0 + 1, 0)
         evac("s", N_HT - 2, 1)

@@ -20,14 +20,12 @@ PACK = 4
 K_PASS = P * PACK
 G = N_TOK // K_PASS
 HT = 128
-N_HT = H // HT
 HB = 256
 N_HB = H // HB
 HL = 512
 N_HL = H // HL
 NQ = G * PACK // 2
-BANK_DT = BF16
-GP_MORE = 4
+N_TILE = HB // HT
 
 
 def tile_continuummemorysystem_pa_kernel(tc, err, W_down, gate_pre, up_pre, x_pred, out_0, out_1):
@@ -36,15 +34,14 @@ def tile_continuummemorysystem_pa_kernel(tc, err, W_down, gate_pre, up_pre, x_pr
 
     with ExitStack() as ctx:
         keep = ctx.enter_context(tc.tile_pool(name="keep", bufs=1))
-        raw = ctx.enter_context(tc.tile_pool(name="raw", bufs=5))
-        grp = ctx.enter_context(tc.tile_pool(name="grp", bufs=4))
+        raw = ctx.enter_context(tc.tile_pool(name="raw", bufs=8))
+        grp = ctx.enter_context(tc.tile_pool(name="grp", bufs=3))
         elem = ctx.enter_context(tc.tile_pool(name="elem", bufs=3))
-        prod = ctx.enter_context(tc.tile_pool(name="prod", bufs=3))
-        stage = ctx.enter_context(tc.tile_pool(name="stage", bufs=8))
+        prod = ctx.enter_context(tc.tile_pool(name="prod", bufs=2))
+        stage = ctx.enter_context(tc.tile_pool(name="stage", bufs=6))
         psum = ctx.enter_context(tc.psum_pool(name="psum", bufs=4))
 
         gate_sb = [keep.tile([P, G * PACK, HL], BF16, name="gate%d" % c, tag="gate%d" % c) for c in range(N_HL)]
-        up_sb = [keep.tile([P, 2, NQ, HB], BF16, name="up%d" % b, tag="up%d" % b) for b in range(N_HB)]
         w_codes = keep.tile([P, H], U32, name="w_codes", tag="w_codes", align_bytes=64)
         w_scales = keep.tile([P, H], U8, name="w_scales", tag="w_scales", align_bytes=64)
         e_codes = keep.tile([P, N_TOK], U32, name="e_codes", tag="e_codes", align_bytes=64)
@@ -53,9 +50,12 @@ def tile_continuummemorysystem_pa_kernel(tc, err, W_down, gate_pre, up_pre, x_pr
         x_scales = keep.tile([P, G * D], U8, name="x_scales", tag="x_scales", align_bytes=64)
         ident = keep.tile([P, P], F32, name="ident", tag="ident")
         ident_bf = keep.tile([P, P], BF16, name="ident_bf", tag="ident_bf")
+        minus_bf = keep.tile([P, P], BF16, name="minus_bf", tag="minus_bf")
         ones = keep.tile([P, P], F32, name="ones", tag="ones")
         diag = keep.tile([P, P], F32, name="diag", tag="diag")
-        ssq = keep.tile([P, 2], F32, name="ssq", tag="ssq")
+        squares = keep.tile([P, 2 * D], BF16, name="squares", tag="squares")
+        ssq_mm = keep.tile([P, 2], F32, name="ssq_mm", tag="ssq_mm")
+        ssq_act = keep.tile([P, 2], F32, name="ssq_act", tag="ssq_act")
         warm_in = keep.tile([P, 1], F32, name="warm_in", tag="warm_in")
         warm_out = keep.tile([P, 1], F32, name="warm_out", tag="warm_out")
         em = keep.tile([P, 1], F32, name="em", tag="em")
@@ -65,67 +65,72 @@ def tile_continuummemorysystem_pa_kernel(tc, err, W_down, gate_pre, up_pre, x_pr
         sgv = keep.tile([P, 1], F32, name="sgv", tag="sgv")
         sgs = keep.tile([P, 1], F32, name="sgs", tag="sgs")
 
-        def load_w(c):
-            t = raw.tile([P, PACK, HL], BF16, name="w_raw", tag="raw")
-            nc.sync.dma_start(out=t[:], in_=W_down[:, c * HL:(c + 1) * HL].rearrange("(p j) h -> p j h", j=PACK))
+        def load_cols(name, src, c, g):
+            t = raw.tile([P, PACK, HL], BF16, name=name, tag="raw")
+            nc.sync.dma_start(
+                out=t[:],
+                in_=src[g * K_PASS:(g + 1) * K_PASS, c * HL:(c + 1) * HL].rearrange("(p j) h -> p j h", j=PACK),
+            )
             return t
 
-        def load_rows(src, g):
-            t = raw.tile([P, PACK * D], BF16, name="rows_raw", tag="raw")
-            nc.sync.dma_start(out=t[:], in_=src[g * K_PASS:(g + 1) * K_PASS, :].rearrange("(p j) d -> p (j d)", j=PACK))
-            return t
+        def load_gate(c, g, lo=0, hi=HL):
+            nc.sync.dma_start(
+                out=gate_sb[c][:, g * PACK:(g + 1) * PACK, lo:hi],
+                in_=gate_pre[g * K_PASS:(g + 1) * K_PASS, c * HL + lo:c * HL + hi].rearrange("(p t) h -> p t h", t=PACK),
+            )
 
-        def load_act(dst, src, c, lo=0, hi=HL):
-            for g in range(G):
-                nc.sync.dma_start(
-                    out=dst[c][:, g * PACK:(g + 1) * PACK, lo:hi],
-                    in_=src[g * K_PASS:(g + 1) * K_PASS, c * HL + lo:c * HL + hi].rearrange("(p t) h -> p t h", t=PACK),
-                )
-
-        def load_up(b):
-            for g in range(G):
-                for e in range(2):
-                    nc.sync.dma_start(
-                        out=up_sb[b][:, e, 2 * g:2 * g + 2, :],
-                        in_=up_pre[g * K_PASS + e:(g + 1) * K_PASS:2, b * HB:(b + 1) * HB].rearrange("(p s) h -> p s h", s=2),
-                    )
-
-        w_raw, e_raw, x_raw = {}, {}, {}
-        load_act(gate_sb, gate_pre, 0, 0, HB)
-        w_raw[0] = load_w(0)
-        x_raw[0] = load_rows(x_pred, 0)
-        e_raw[0] = load_rows(err, 0)
-        e_raw[1] = load_rows(err, 1)
-        load_act(gate_sb, gate_pre, 0, HB, HL)
-        x_raw[1] = load_rows(x_pred, 1)
-        load_up(0)
-        load_up(1)
-        load_act(gate_sb, gate_pre, 1)
+        w_raw, e_raw, x_raw, up_raw = {}, {}, {}, {}
+        e_raw[0] = load_cols("e_raw", err, 0, 0)
+        w_raw[0] = load_cols("w_raw", W_down, 0, 0)
+        load_gate(0, 0, 0, HB)
+        e_raw[1] = load_cols("e_raw", err, 0, 1)
+        load_gate(0, 1, 0, HB)
+        w_raw[1] = load_cols("w_raw", W_down, 1, 0)
+        load_gate(0, 0, HB, HL)
+        load_gate(0, 1, HB, HL)
+        load_gate(1, 0)
+        load_gate(1, 1)
+        w_raw[2] = load_cols("w_raw", W_down, 2, 0)
+        load_gate(2, 0)
+        load_gate(2, 1)
+        w_raw[3] = load_cols("w_raw", W_down, 3, 0)
+        load_gate(3, 0)
+        load_gate(3, 1)
+        x_raw[0] = load_cols("x_raw", x_pred, 0, 0)
+        x_raw[1] = load_cols("x_raw", x_pred, 0, 1)
 
         nc.gpsimd.memset(warm_in[:], 0.0)
         nc.scalar.activation(out=warm_out[:], in_=warm_in[:], func=ACT.Sigmoid)
         make_identity(nc, ident[:])
         nc.gpsimd.memset(ones[:], 1.0)
-        nc.gpsimd.memset(ssq[:], 0.0)
+        nc.gpsimd.memset(ssq_mm[:], 0.0)
+        nc.gpsimd.memset(ssq_act[:], 0.0)
         make_identity(nc, ident_bf[:])
+        nc.gpsimd.tensor_scalar(out=minus_bf[:], in0=ident_bf[:], scalar1=-1.0, scalar2=0.0, op0=ALU.mult, op1=ALU.add)
 
-        def interleave(engine, src3):
+        def group_tile():
             t = grp.tile([P, HL * PACK], BF16, name="grouped", tag="grouped", align_bytes=64)
-            dst = t[:].rearrange("p (c i j) -> p c j i", i=4, j=PACK)
-            src = src3.rearrange("p j (c i) -> p c j i", i=4)
-            if engine == "v":
-                nc.vector.tensor_copy(out=dst, in_=src)
-            else:
-                nc.scalar.copy(out=dst, in_=src)
             return t
 
-        def interleave_half(t, src3, half):
-            for lo in (half * 256, half * 256 + 128):
+        def interleave(engine, src):
+            t = group_tile()
+            dst4 = t[:].rearrange("p (c i j) -> p c j i", i=4, j=PACK)
+            src4 = src[:].rearrange("p j (c i) -> p c j i", i=4)
+            if engine == "v":
+                nc.vector.tensor_copy(out=dst4, in_=src4)
+            else:
+                nc.scalar.copy(out=dst4, in_=src4)
+            return t
+
+        def interleave_gp(src):
+            t = group_tile()
+            for lo in range(0, HL, HT):
                 nc.gpsimd.tensor_scalar(
-                    out=t[:, lo * PACK:(lo + 128) * PACK].rearrange("p (w j) -> p w j", j=PACK),
-                    in0=src3[:, :, lo:lo + 128].rearrange("p j w -> p w j"),
+                    out=t[:, lo * PACK:(lo + HT) * PACK].rearrange("p (w j) -> p w j", j=PACK),
+                    in0=src[:, :, lo:lo + HT].rearrange("p j w -> p w j"),
                     scalar1=1.0, scalar2=0.0, op0=ALU.mult, op1=ALU.add,
                 )
+            return t
 
         def quantize(t, codes, scales, lo):
             nc.vector.quantize_mx(
@@ -134,104 +139,100 @@ def tile_continuummemorysystem_pa_kernel(tc, err, W_down, gate_pre, up_pre, x_pr
                 in_=t[:],
             )
 
-        def gate_pairs(b):
+        def gate_slab(b):
             c, off = divmod(b * HB, HL)
-            return gate_sb[c][:, :, off:off + HB].rearrange("p (q e) h -> p q h e", e=2)
+            return gate_sb[c][:, :, off:off + HB]
 
-        sx, lt = {}, {}
+        ex, tx, dh, ups = {}, {}, {}, {}
 
-        def act_sig(b, q_lo=0, q_hi=NQ):
-            if q_lo == 0:
-                sx[b] = elem.tile([P, NQ, HB, 2], F32, name="sx", tag="sx", bufs=5)
-            nc.scalar.activation(out=sx[b][:, q_lo:q_hi, :, :], in_=gate_pairs(b)[:, q_lo:q_hi, :, :], func=ACT.Sigmoid, scale=-1.0)
-
-        def act_l(b, q_lo=0, q_hi=NQ):
-            if q_lo == 0:
-                lt[b] = elem.tile([P, NQ, HB, 2], F32, name="lt", tag="lt")
-            nc.scalar.activation(out=lt[b][:, q_lo:q_hi, :, :], in_=gate_pairs(b)[:, q_lo:q_hi, :, :], func=ACT.Silu)
-
-        def fmul(b, q_lo=0, q_hi=NQ):
-            flat = sx[b][:, q_lo:q_hi, :, :].rearrange("p q h e -> p (q h e)")
-            nc.vector.scalar_tensor_tensor(
-                out=flat, in0=lt[b][:, q_lo:q_hi, :, :].rearrange("p q h e -> p (q h e)"), scalar=1.0, in1=flat,
-                op0=ALU.subtract, op1=ALU.mult,
+        def act_sig(b, g_lo=0, g_hi=G):
+            if g_lo == 0:
+                ex[b] = elem.tile([P, NQ, HB, 2], F32, name="ex", tag="ex", bufs=N_HB)
+            pairs = gate_slab(b).rearrange("p (q e) h -> p q h e", e=2)
+            nc.scalar.activation(
+                out=ex[b][:, 2 * g_lo:2 * g_hi, :, :], in_=pairs[:, 2 * g_lo:2 * g_hi, :, :], func=ACT.Sigmoid,
             )
 
-        ups = {}
+        def act_silu(b):
+            tx[b] = elem.tile([P, NQ, HB, 2], F32, name="tx", tag="tx")
+            nc.scalar.activation(
+                out=tx[b][:], in_=gate_slab(b).rearrange("p (q e) h -> p q h e", e=2), func=ACT.Silu, scale=-1.0,
+            )
 
-        def upmm(b):
-            ups[b] = psum.tile([P, 2, 2 * HB], BF16, name="ups", tag="ups", bufs=1)
-            for e in range(2):
-                nc.tensor.matmul(
-                    out=ups[b][:, e, :], lhsT=ident_bf[:],
-                    rhs=up_sb[b][:, e, 0:2, :].rearrange("p s h -> p (s h)"), start=True, stop=True,
-                )
-
-        def xmul(b, g):
-            pairs = sx[b][:, 2 * g:2 * g + 2, :, :].rearrange("p s h e -> p (s h) e")
-            if g == 0:
-                up_half = ups[b][:].rearrange("p e n -> p n e")
-            else:
-                up_half = up_sb[b][:, :, 2:4, :].rearrange("p e s h -> p (s h) e")
-            nc.vector.scalar_tensor_tensor(out=pairs, in0=pairs, scalar=1.0, in1=up_half, op0=ALU.add, op1=ALU.mult)
-
-        dh, dhs, pq, pc, ps, acc = {}, {}, {}, {}, {}, {}
-        banks = {"A": (0, 0, HB), "B": (1, 0, HT), "C": (1, HT, HT)}
-
-        def stage1(b, k):
-            g, h0, nh = banks[k]
-            dh[b, k] = psum.tile([P, PACK, nh], BANK_DT, name="dh", tag="dh", bufs=3)
+        def stage1(b, g):
+            dh[b, g] = psum.tile([P, PACK, HB], BF16, name="dh", tag="dh")
             for t in range(PACK):
                 lo = g * K_PASS + t * P
                 nc.tensor.matmul_mx(
-                    out=dh[b, k][:, t, :],
+                    out=dh[b, g][:, t, :],
                     lhsT=e_codes[:, lo:lo + P].bitcast(FP8X4),
                     lhsT_scale=e_scales[:, lo:lo + P],
-                    rhs=w_codes[:, b * HB + h0:b * HB + h0 + nh].bitcast(FP8X4),
-                    rhs_scale=w_scales[:, b * HB + h0:b * HB + h0 + nh],
+                    rhs=w_codes[:, b * HB:(b + 1) * HB].bitcast(FP8X4),
+                    rhs_scale=w_scales[:, b * HB:(b + 1) * HB],
                     start=True, stop=True,
                 )
 
-        def new_pq(b):
-            pq[b] = prod.tile([P, 2, G, HB * PACK], BF16, name="pq", tag="pq", bufs=1, align_bytes=64)
-
-        def product(engine, b, k, a, bank):
-            g, h0, nh = banks[k]
-            factor = (lt[b], sx[b])[a]
-            engine.tensor_tensor(
-                out=pq[b][:, a, g, h0 * PACK:(h0 + nh) * PACK].rearrange("p (h s e) -> p h s e", s=2, e=2),
-                in0=bank,
-                in1=factor[:, 2 * g:2 * g + 2, h0:h0 + nh, :].rearrange("p s h e -> p h s e"), op=ALU.mult,
+        def e_mul(b, g):
+            half = ex[b][:, 2 * g:2 * g + 2, :, :]
+            nc.vector.tensor_tensor(
+                out=half, in0=dh[b, g][:].rearrange("p (s e) h -> p s h e", e=2), in1=half, op=ALU.mult,
             )
 
-        def pmul(b, k, a):
-            product(nc.vector, b, k, a, dh[b, k][:].rearrange("p (s e) h -> p h s e", e=2))
+        def upmm(b, g):
+            c, off = divmod(b * HB, HL)
+            ups[b, g] = psum.tile([P, 2, 2 * HB], BF16, name="ups", tag="dh")
+            for e in range(2):
+                nc.tensor.matmul(
+                    out=ups[b, g][:, e, :], lhsT=minus_bf[:],
+                    rhs=up_raw[c, g][:, e:PACK:2, off:off + HB], start=True, stop=True,
+                )
 
-        def dhcopy(b, k):
-            dhs[b, k] = prod.tile([P, HT * PACK], BANK_DT, name="dhs", tag="dhs", bufs=4)
-            nc.scalar.copy(
-                out=dhs[b, k][:].rearrange("p (h t) -> p h t", t=PACK),
-                in_=dh[b, k][:].rearrange("p t h -> p h t"),
+        def x_mul(b, g):
+            pairs = tx[b][:, 2 * g:2 * g + 2, :, :].rearrange("p s h e -> p (s h) e")
+            nc.vector.scalar_tensor_tensor(
+                out=pairs, in0=pairs, scalar=1.0, in1=ups[b, g][:].rearrange("p e n -> p n e"),
+                op0=ALU.subtract, op1=ALU.mult,
             )
 
-        def gp_pmul(b):
-            todo = [("C", 0), ("C", 1)]
-            if b >= GP_MORE:
-                todo.append(("B", 1))
-            for k, a in todo:
-                product(nc.gpsimd, b, k, a, dhs[b, k][:].rearrange("p (h s e) -> p h s e", s=2, e=2))
+        pq, pc, ps, acc = {}, {}, {}, {}
+
+        def new_pq(b, a):
+            pq[b, a] = prod.tile([P, G, HB * PACK], BF16, name="pq%d" % a, tag="pq%d" % a, bufs=3 - a, align_bytes=64)
+
+        def e_pairs(b, g, lo, hi):
+            return ex[b][:, 2 * g:2 * g + 2, lo:hi, :].rearrange("p s h e -> p h s e")
+
+        def up_mul(b, g, lo, hi):
+            nc.gpsimd.tensor_tensor(
+                out=pq[b, 0][:, g, lo * PACK:hi * PACK].rearrange("p (h s e) -> p h s e", s=2, e=2),
+                in0=gate_slab(b)[:, g * PACK:(g + 1) * PACK, lo:hi].rearrange("p (s e) h -> p h s e", e=2),
+                in1=e_pairs(b, g, lo, hi), op=ALU.mult,
+            )
+
+        def gp_up(b):
+            new_pq(b, 0)
+            for g in range(G):
+                for lo in range(0, HB, HT):
+                    up_mul(b, g, lo, lo + HT)
+
+        def gate_mul(b, g):
+            nc.vector.tensor_tensor(
+                out=pq[b, 1][:, g, :].rearrange("p (h s e) -> p h s e", s=2, e=2),
+                in0=e_pairs(b, g, 0, HB),
+                in1=tx[b][:, 2 * g:2 * g + 2, :, :].rearrange("p s h e -> p h s e"), op=ALU.mult,
+            )
 
         def pquant(b, a):
-            pc[b, a] = prod.tile([P, G * HB], U32, name="pc", tag="pc", align_bytes=64)
-            ps[b, a] = prod.tile([P, G * HB], U8, name="ps", tag="ps", align_bytes=64)
+            pc[b, a] = prod.tile([P, G * HB], U32, name="pc", tag="pc", bufs=4, align_bytes=64)
+            ps[b, a] = prod.tile([P, G * HB], U8, name="ps", tag="ps", bufs=4, align_bytes=64)
             nc.vector.quantize_mx(
                 out=pc[b, a][:].bitcast(FP8X4), scales=ps[b, a][:],
-                in_=pq[b][:, a, :, :].rearrange("p g c -> p (g c)"),
+                in_=pq[b, a][:].rearrange("p g c -> p (g c)"),
             )
 
         def stage2(b, a):
-            for hl in range(HB // HT):
-                ht = b * (HB // HT) + hl
+            for hl in range(N_TILE):
+                ht = b * N_TILE + hl
                 acc[ht, a] = psum.tile([P, D], F32, name="acc", tag="acc")
                 for g in range(G):
                     lo = g * HB + hl * HT
@@ -252,31 +253,14 @@ def tile_continuummemorysystem_pa_kernel(tc, err, W_down, gate_pre, up_pre, x_pr
                 nc.scalar.activation(out=res[:], in_=acc[ht, a][:], func=ACT.Copy, scale=sgs[:, 0:1])
             nc.sync.dma_start(out=outs[a][ht * HT:(ht + 1) * HT, :], in_=res[:])
 
-        ctx.enter_context(tc.manual_schedule(engines={ENG.Activation, ENG.DVE, ENG.Pool}))
-
-        act_sig(0, 0, 2)
-        act_sig(0, 2, 4)
-        gw0 = interleave("v", w_raw[0][:])
-        w_raw[1] = load_w(1)
-        act_l(0, 0, 2)
-        act_l(0, 2, 4)
-        gx0 = interleave("v", x_raw[0][:].rearrange("p (j d) -> p j d", j=PACK))
-        quantize(gw0, w_codes, w_scales, 0)
-        quantize(gx0, x_codes, x_scales, 0)
-        w_raw[2] = load_w(2)
-        load_up(2)
-        load_up(3)
-        load_act(gate_sb, gate_pre, 2)
-        load_up(4)
-        load_up(5)
-
         e_grp = {}
-        for g in range(G):
-            words = e_raw[g][:].bitcast(F32)
-            e_grp[g] = grp.tile([P, HL * PACK], BF16, name="e_grouped", tag="grouped", align_bytes=64)
+
+        def err_turn(g):
+            words = e_raw[g][:].rearrange("p j d -> p (j d)").bitcast(F32)
+            e_grp[g] = group_tile()
             egw = e_grp[g][:].bitcast(F32).rearrange("p (t m u) -> p t m u", t=PACK, u=2)
             for half in range(2):
-                xt = psum.tile([P, PACK, P], F32, name="xt", tag="dh", bufs=3)
+                xt = psum.tile([P, PACK, P], F32, name="xt", tag="dh")
                 for tt in range(2):
                     t = 2 * half + tt
                     for u in range(2):
@@ -289,115 +273,114 @@ def tile_continuummemorysystem_pa_kernel(tc, err, W_down, gate_pre, up_pre, x_pr
                     out=egw[:, 2 * half:2 * half + 2, :, :],
                     in_=xt[:].rearrange("p (tt u) m -> p tt m u", u=2),
                 )
-        gram = psum.tile([P, P], F32, name="gram", tag="acc")
-        n_mm = G * PACK * (D // P)
-        i_mm = 0
-        for g in range(G):
-            for t in range(PACK):
-                for fb in range(D // P):
-                    blk = e_raw[g][:, t * D + fb * P:t * D + (fb + 1) * P]
-                    nc.tensor.matmul(out=gram[:], lhsT=blk, rhs=blk, start=(i_mm == 0), stop=(i_mm == n_mm - 1))
-                    i_mm += 1
-        w_raw[3] = load_w(3)
-        load_act(gate_sb, gate_pre, 3)
-        load_up(6)
-        load_up(7)
-        fmul(0, 0, 2)
-        fmul(0, 2, 4)
-        for g in range(G):
-            quantize(e_grp[g], e_codes, e_scales, g * K_PASS)
-        nc.vector.scalar_tensor_tensor(
-            out=diag[:], in0=gram[:], scalar=1.0, in1=ident[:], op0=ALU.mult, op1=ALU.mult,
-            accum_out=ssq[:, 0:1],
-        )
-        tot = psum.tile([P, 2], F32, name="tot", tag="acc")
-        nc.tensor.matmul(out=tot[:], lhsT=ones[:], rhs=ssq[:], start=True, stop=True)
-        act_l(1)
-        nc.scalar.activation(out=em[:], in_=tot[:, 0:1], func=ACT.Sqrt, scale=1.0 / (N_TOK * N_TOK))
-        nc.gpsimd.tensor_scalar(out=ema[:], in0=em[:], scalar1=0.05, scalar2=0.95, op0=ALU.mult, op1=ALU.add)
-        nc.gpsimd.tensor_scalar(out=emc[:], in0=ema[:], scalar1=1e-8, scalar2=None, op0=ALU.max)
-        stage1(0, "C")
-        dhcopy(0, "C")
-        upmm(0)
-        gx1 = interleave("v", x_raw[1][:].rearrange("p (j d) -> p j d", j=PACK))
-        xmul(0, 1)
-        quantize(gx1, x_codes, x_scales, D)
-        nc.vector.reciprocal(out=rec[:], in_=emc[:])
-        nc.gpsimd.tensor_scalar(out=sgv[:], in0=rec[:], scalar1=em[:, 0:1], scalar2=3.0, op0=ALU.mult, op1=ALU.min)
-        nc.gpsimd.tensor_scalar(out=sgs[:], in0=sgv[:], scalar1=1.0 / N_TOK, scalar2=None, op0=ALU.mult)
-        xmul(0, 0)
 
-        acts = {
-            0: (("sig", 1), ("sig", 2), ("sig", 3)),
-            1: (("silu", 3),),
-            2: (("sig", 4), ("sig", 5)),
-            3: (("sig", 7),),
-            4: (("silu", 6),),
-        }
-        acts_late = {0: ("silu", 2), 1: ("silu", 4), 2: ("sig", 6), 3: ("silu", 5), 4: ("silu", 7)}
-        gw_late = {}
-        stage1(0, "A")
-        stage1(0, "B")
+        ctx.enter_context(tc.manual_schedule(engines={ENG.Activation, ENG.DVE, ENG.Pool, ENG.PE}))
+
+        err_turn(0)
+        gw = {0: interleave("v", w_raw[0])}
+        act_sig(0, 0, 1)
+        err_turn(1)
+        act_sig(0, 1, 2)
+        quantize(gw[0], w_codes, w_scales, 0)
+        quantize(e_grp[0], e_codes, e_scales, 0)
+        stage1(0, 0)
+        gw[1] = interleave_gp(w_raw[1])
+        e_mul(0, 0)
+        quantize(e_grp[1], e_codes, e_scales, K_PASS)
+        stage1(0, 1)
+        act_sig(1)
+        gram = psum.tile([P, P], F32, name="gram", tag="acc")
+        rows = [(g, j) for g in range(G) for j in range(PACK)][:-2]
+        n_mm = len(rows) * (D // P)
+        i_mm = 0
+        for g, j in rows:
+            for fb in range(D // P):
+                blk = e_raw[g][:, j, fb * P:(fb + 1) * P]
+                nc.tensor.matmul(out=gram[:], lhsT=blk, rhs=blk, start=(i_mm == 0), stop=(i_mm == n_mm - 1))
+                i_mm += 1
+
         for b in range(N_HB):
-            ht0 = b * (HB // HT)
-            more = b + 1 < N_HB
-            new_pq(b)
-            gp_pmul(b)
-            if b < 4:
-                c_late, half = 2 + b // 2, b % 2
-                if half == 0:
-                    gw_late[c_late] = grp.tile([P, HL * PACK], BF16, name="grouped", tag="grouped", align_bytes=64)
-                interleave_half(gw_late[c_late], w_raw[c_late], half)
-            if more:
-                stage1(b + 1, "C")
-                upmm(b + 1)
-            for i, (func, slab) in enumerate(acts.get(b, (("none", 0),))):
-                if func == "sig":
-                    act_sig(slab)
-                elif func == "silu":
-                    act_l(slab)
-                if i == 0 and more:
-                    dhcopy(b + 1, "C")
-            if b >= 1:
-                evac("s", ht0 - 2, 1)
-                evac("s", ht0 - 1, 1)
-            pmul(b, "A", 0)
-            pmul(b, "B", 0)
-            if not more:
+            if b > 0:
+                e_mul(b, 0)
+            if b + 1 < N_HB and (b + 1) % 2 == 0:
+                c = (b + 1) // 2
+                quantize(gw[c], w_codes, w_scales, c * HL)
+            if b == 7:
+                pquant(0, 0)
+            if b + 1 < N_HB:
+                stage1(b + 1, 0)
+                stage1(b + 1, 1)
+            if b + 2 < N_HB:
+                act_sig(b + 2)
+            e_mul(b, 1)
+            if b == 0:
+                gw[2] = interleave_gp(w_raw[2])
+            if b == 1:
+                gp_up(0)
+                nc.scalar.activation(
+                    out=squares[:], in_=e_raw[1][:, 2:4, :].rearrange("p j d -> p (j d)"), func=ACT.Square,
+                    accum_out=ssq_act[:, 0:1],
+                )
+            if b == 3:
+                nc.vector.scalar_tensor_tensor(
+                    out=diag[:], in0=gram[:], scalar=1.0, in1=ident[:], op0=ALU.mult, op1=ALU.mult,
+                    accum_out=ssq_mm[:, 0:1],
+                )
+            if b == 4:
+                tot = psum.tile([P, 2], F32, name="tot", tag="acc")
+                nc.tensor.matmul(out=tot[:], lhsT=ones[:], rhs=ssq_mm[:], start=True, stop=False)
+                nc.tensor.matmul(out=tot[:], lhsT=ones[:], rhs=ssq_act[:], start=False, stop=True)
+                gw[3] = interleave("v", w_raw[3])
+                gp_up(1)
+        for c in range(N_HL):
+            for g in range(G):
+                up_raw[c, g] = load_cols("up_raw", up_pre, c, g)
+
+        nc.scalar.activation(out=em[:], in_=tot[:, 0:1], func=ACT.Sqrt, scale=1.0 / (N_TOK * N_TOK))
+        act_silu(0)
+        act_silu(1)
+        gx = [interleave("s", x_raw[g]) for g in range(G)]
+        upmm(0, 0)
+        upmm(0, 1)
+        gp_up(2)
+        nc.vector.tensor_scalar(out=ema[:], in0=em[:], scalar1=0.05, scalar2=0.95, op0=ALU.mult, op1=ALU.add)
+        for b in range(N_HB):
+            x_mul(b, 0)
+            if b == 0:
+                nc.vector.tensor_scalar(out=emc[:], in0=ema[:], scalar1=1e-8, scalar2=None, op0=ALU.max)
+            x_mul(b, 1)
+            if b + 1 < N_HB:
+                upmm(b + 1, 0)
+                upmm(b + 1, 1)
+            if b == 0:
+                nc.vector.reciprocal(out=rec[:], in_=emc[:])
+            if b == 1:
+                quantize(gx[0], x_codes, x_scales, 0)
+            if b > 0:
+                pquant(b - 1, 1)
+            new_pq(b, 1)
+            gate_mul(b, 0)
+            if b == 0:
+                nc.vector.tensor_scalar(
+                    out=sgv[:], in0=rec[:], scalar1=em[:, 0:1], scalar2=3.0, op0=ALU.mult, op1=ALU.min)
+            if b == 1:
+                quantize(gx[1], x_codes, x_scales, D)
+                stage2(0, 0)
+            if b > 0:
+                stage2(b - 1, 1)
                 pquant(b, 0)
                 stage2(b, 0)
-            pmul(b, "A", 1)
-            if more:
-                stage1(b + 1, "A")
-            if b < GP_MORE:
-                pmul(b, "B", 1)
-            if more:
-                stage1(b + 1, "B")
-                if b + 1 >= GP_MORE:
-                    dhcopy(b + 1, "B")
+            gate_mul(b, 1)
             if b == 0:
-                gw1 = interleave("v", w_raw[1][:])
-            if more:
-                fmul(b + 1)
-                pquant(b, 0)
-                stage2(b, 0)
-            if b == 0:
-                quantize(gw1, w_codes, w_scales, HL)
-            if b in (2, 4):
-                quantize(gw_late[1 + b // 2], w_codes, w_scales, (1 + b // 2) * HL)
-            if more:
-                xmul(b + 1, 1)
-            pquant(b, 1)
-            stage2(b, 1)
-            if more:
-                xmul(b + 1, 0)
-            if b in acts_late:
-                func, slab = acts_late[b]
-                if func == "sig":
-                    act_sig(slab)
-                else:
-                    act_l(slab)
-            evac("s", ht0, 0)
-            evac("s", ht0 + 1, 0)
-        evac("s", N_HT - 2, 1)
-        evac("v", N_HT - 1, 1)
+                nc.vector.tensor_scalar(out=sgs[:], in0=sgv[:], scalar1=1.0 / N_TOK, scalar2=None, op0=ALU.mult)
+            if b + 3 < N_HB:
+                gp_up(b + 3)
+            if b + 2 < N_HB:
+                act_silu(b + 2)
+            for a, k in ((0, 0),) * (b == 1) + ((1, b - 1), (0, b)) * (b > 0):
+                for hl in range(N_TILE):
+                    evac("s", k * N_TILE + hl, a)
+        pquant(N_HB - 1, 1)
+        stage2(N_HB - 1, 1)
+        evac("s", N_HB * N_TILE - 2, 1)
+        evac("v", N_HB * N_TILE - 1, 1)

@@ -34,11 +34,11 @@ def tile_continuummemorysystem_pa_kernel(tc, err, W_down, gate_pre, up_pre, x_pr
 
     with ExitStack() as ctx:
         keep = ctx.enter_context(tc.tile_pool(name="keep", bufs=1))
-        raw = ctx.enter_context(tc.tile_pool(name="raw", bufs=8))
+        raw = ctx.enter_context(tc.tile_pool(name="raw", bufs=7))
         grp = ctx.enter_context(tc.tile_pool(name="grp", bufs=3))
         elem = ctx.enter_context(tc.tile_pool(name="elem", bufs=3))
         prod = ctx.enter_context(tc.tile_pool(name="prod", bufs=2))
-        stage = ctx.enter_context(tc.tile_pool(name="stage", bufs=6))
+        stage = ctx.enter_context(tc.tile_pool(name="stage", bufs=4))
         psum = ctx.enter_context(tc.psum_pool(name="psum", bufs=4))
 
         gate_sb = [keep.tile([P, G * PACK, HL], BF16, name="gate%d" % c, tag="gate%d" % c) for c in range(N_HL)]
@@ -197,23 +197,22 @@ def tile_continuummemorysystem_pa_kernel(tc, err, W_down, gate_pre, up_pre, x_pr
         pq, pc, ps, acc = {}, {}, {}, {}
 
         def new_pq(b, a):
-            pq[b, a] = prod.tile([P, G, HB * PACK], BF16, name="pq%d" % a, tag="pq%d" % a, bufs=3 - a, align_bytes=64)
+            pq[b, a] = prod.tile([P, G, HB * PACK], BF16, name="pq%d" % a, tag="pq%d" % a, bufs=2, align_bytes=64)
 
         def e_pairs(b, g, lo, hi):
             return ex[b][:, 2 * g:2 * g + 2, lo:hi, :].rearrange("p s h e -> p h s e")
 
         def up_mul(b, g, lo, hi):
-            nc.gpsimd.tensor_tensor(
+            nc.vector.tensor_tensor(
                 out=pq[b, 0][:, g, lo * PACK:hi * PACK].rearrange("p (h s e) -> p h s e", s=2, e=2),
                 in0=gate_slab(b)[:, g * PACK:(g + 1) * PACK, lo:hi].rearrange("p (s e) h -> p h s e", e=2),
                 in1=e_pairs(b, g, lo, hi), op=ALU.mult,
             )
 
-        def gp_up(b):
+        def v_up(b):
             new_pq(b, 0)
             for g in range(G):
-                for lo in range(0, HB, HT):
-                    up_mul(b, g, lo, lo + HT)
+                up_mul(b, g, 0, HB)
 
         def gate_mul(b, g):
             nc.vector.tensor_tensor(
@@ -223,8 +222,8 @@ def tile_continuummemorysystem_pa_kernel(tc, err, W_down, gate_pre, up_pre, x_pr
             )
 
         def pquant(b, a):
-            pc[b, a] = prod.tile([P, G * HB], U32, name="pc", tag="pc", bufs=4, align_bytes=64)
-            ps[b, a] = prod.tile([P, G * HB], U8, name="ps", tag="ps", bufs=4, align_bytes=64)
+            pc[b, a] = prod.tile([P, G * HB], U32, name="pc", tag="pc", bufs=11, align_bytes=64)
+            ps[b, a] = prod.tile([P, G * HB], U8, name="ps", tag="ps", bufs=11, align_bytes=64)
             nc.vector.quantize_mx(
                 out=pc[b, a][:].bitcast(FP8X4), scales=ps[b, a][:],
                 in_=pq[b, a][:].rearrange("p g c -> p (g c)"),
@@ -285,53 +284,59 @@ def tile_continuummemorysystem_pa_kernel(tc, err, W_down, gate_pre, up_pre, x_pr
         quantize(e_grp[0], e_codes, e_scales, 0)
         stage1(0, 0)
         gw[1] = interleave_gp(w_raw[1])
-        e_mul(0, 0)
         quantize(e_grp[1], e_codes, e_scales, K_PASS)
         stage1(0, 1)
+        e_mul(0, 0)
         act_sig(1)
         gram = psum.tile([P, P], F32, name="gram", tag="acc")
         rows = [(g, j) for g in range(G) for j in range(PACK)][:-2]
-        n_mm = len(rows) * (D // P)
-        i_mm = 0
-        for g, j in rows:
+
+        def gram_rows(i):
+            g, j = rows[i]
             for fb in range(D // P):
                 blk = e_raw[g][:, j, fb * P:(fb + 1) * P]
-                nc.tensor.matmul(out=gram[:], lhsT=blk, rhs=blk, start=(i_mm == 0), stop=(i_mm == n_mm - 1))
-                i_mm += 1
+                nc.tensor.matmul(
+                    out=gram[:], lhsT=blk, rhs=blk,
+                    start=(i == 0 and fb == 0), stop=(i == len(rows) - 1 and fb == D // P - 1),
+                )
+
 
         for b in range(N_HB):
             if b > 0:
                 e_mul(b, 0)
-            if b + 1 < N_HB and (b + 1) % 2 == 0:
-                c = (b + 1) // 2
-                quantize(gw[c], w_codes, w_scales, c * HL)
-            if b == 7:
-                pquant(0, 0)
             if b + 1 < N_HB:
                 stage1(b + 1, 0)
                 stage1(b + 1, 1)
+            if 1 <= b <= 3:
+                gram_rows(2 * b - 2)
+                gram_rows(2 * b - 1)
             if b + 2 < N_HB:
                 act_sig(b + 2)
             e_mul(b, 1)
+            if b % 2 == 0 and b + 2 < N_HB:
+                c = (b + 2) // 2
+                quantize(gw[c], w_codes, w_scales, c * HL)
+            v_up(b)
+            if b > 0:
+                pquant(b - 1, 0)
             if b == 0:
                 gw[2] = interleave_gp(w_raw[2])
             if b == 1:
-                gp_up(0)
                 nc.scalar.activation(
                     out=squares[:], in_=e_raw[1][:, 2:4, :].rearrange("p j d -> p (j d)"), func=ACT.Square,
                     accum_out=ssq_act[:, 0:1],
                 )
             if b == 3:
+                gw[3] = interleave("v", w_raw[3])
+            if b == 4:
                 nc.vector.scalar_tensor_tensor(
                     out=diag[:], in0=gram[:], scalar=1.0, in1=ident[:], op0=ALU.mult, op1=ALU.mult,
                     accum_out=ssq_mm[:, 0:1],
                 )
-            if b == 4:
+            if b == 5:
                 tot = psum.tile([P, 2], F32, name="tot", tag="acc")
                 nc.tensor.matmul(out=tot[:], lhsT=ones[:], rhs=ssq_mm[:], start=True, stop=False)
                 nc.tensor.matmul(out=tot[:], lhsT=ones[:], rhs=ssq_act[:], start=False, stop=True)
-                gw[3] = interleave("v", w_raw[3])
-                gp_up(1)
         for c in range(N_HL):
             for g in range(G):
                 up_raw[c, g] = load_cols("up_raw", up_pre, c, g)
@@ -342,7 +347,6 @@ def tile_continuummemorysystem_pa_kernel(tc, err, W_down, gate_pre, up_pre, x_pr
         gx = [interleave("s", x_raw[g]) for g in range(G)]
         upmm(0, 0)
         upmm(0, 1)
-        gp_up(2)
         nc.vector.tensor_scalar(out=ema[:], in0=em[:], scalar1=0.05, scalar2=0.95, op0=ALU.mult, op1=ALU.add)
         for b in range(N_HB):
             x_mul(b, 0)
@@ -354,6 +358,8 @@ def tile_continuummemorysystem_pa_kernel(tc, err, W_down, gate_pre, up_pre, x_pr
                 upmm(b + 1, 1)
             if b == 0:
                 nc.vector.reciprocal(out=rec[:], in_=emc[:])
+            if b == 0:
+                pquant(N_HB - 1, 0)
             if b == 1:
                 quantize(gx[0], x_codes, x_scales, 0)
             if b > 0:
@@ -368,13 +374,10 @@ def tile_continuummemorysystem_pa_kernel(tc, err, W_down, gate_pre, up_pre, x_pr
                 stage2(0, 0)
             if b > 0:
                 stage2(b - 1, 1)
-                pquant(b, 0)
                 stage2(b, 0)
             gate_mul(b, 1)
             if b == 0:
                 nc.vector.tensor_scalar(out=sgs[:], in0=sgv[:], scalar1=1.0 / N_TOK, scalar2=None, op0=ALU.mult)
-            if b + 3 < N_HB:
-                gp_up(b + 3)
             if b + 2 < N_HB:
                 act_silu(b + 2)
             for a, k in ((0, 0),) * (b == 1) + ((1, b - 1), (0, b)) * (b > 0):

@@ -34,11 +34,11 @@ def tile_continuummemorysystem_pa_kernel(tc, err, W_down, gate_pre, up_pre, x_pr
 
     with ExitStack() as ctx:
         keep = ctx.enter_context(tc.tile_pool(name="keep", bufs=1))
-        raw = ctx.enter_context(tc.tile_pool(name="raw", bufs=7))
-        grp = ctx.enter_context(tc.tile_pool(name="grp", bufs=3))
+        raw = ctx.enter_context(tc.tile_pool(name="raw", bufs=8))
+        grp = ctx.enter_context(tc.tile_pool(name="grp", bufs=4))
         elem = ctx.enter_context(tc.tile_pool(name="elem", bufs=3))
         prod = ctx.enter_context(tc.tile_pool(name="prod", bufs=2))
-        stage = ctx.enter_context(tc.tile_pool(name="stage", bufs=4))
+        stage = ctx.enter_context(tc.tile_pool(name="stage", bufs=8))
         psum = ctx.enter_context(tc.psum_pool(name="psum", bufs=4))
 
         gate_sb = [keep.tile([P, G * PACK, HL], BF16, name="gate%d" % c, tag="gate%d" % c) for c in range(N_HL)]
@@ -53,9 +53,10 @@ def tile_continuummemorysystem_pa_kernel(tc, err, W_down, gate_pre, up_pre, x_pr
         minus_bf = keep.tile([P, P], BF16, name="minus_bf", tag="minus_bf")
         ones = keep.tile([P, P], F32, name="ones", tag="ones")
         diag = keep.tile([P, P], F32, name="diag", tag="diag")
-        squares = keep.tile([P, 2 * D], BF16, name="squares", tag="squares")
+        half = keep.tile([P, 1], F32, name="half", tag="half")
+        msq = keep.tile([P, 1], F32, name="msq", tag="msq")
+        up_first = keep.tile([P, PACK, HB], BF16, name="up_first", tag="up_first")
         ssq_mm = keep.tile([P, 2], F32, name="ssq_mm", tag="ssq_mm")
-        ssq_act = keep.tile([P, 2], F32, name="ssq_act", tag="ssq_act")
         warm_in = keep.tile([P, 1], F32, name="warm_in", tag="warm_in")
         warm_out = keep.tile([P, 1], F32, name="warm_out", tag="warm_out")
         em = keep.tile([P, 1], F32, name="em", tag="em")
@@ -80,33 +81,25 @@ def tile_continuummemorysystem_pa_kernel(tc, err, W_down, gate_pre, up_pre, x_pr
             )
 
         w_raw, e_raw, x_raw, up_raw = {}, {}, {}, {}
+        load_gate(0, 0, 0, HB)
         e_raw[0] = load_cols("e_raw", err, 0, 0)
         w_raw[0] = load_cols("w_raw", W_down, 0, 0)
-        load_gate(0, 0, 0, HB)
-        e_raw[1] = load_cols("e_raw", err, 0, 1)
         load_gate(0, 1, 0, HB)
-        w_raw[1] = load_cols("w_raw", W_down, 1, 0)
+        e_raw[1] = load_cols("e_raw", err, 0, 1)
+        up_raw[0, 0] = load_cols("up_raw", up_pre, 0, 0)
+        up_raw[0, 1] = load_cols("up_raw", up_pre, 0, 1)
         load_gate(0, 0, HB, HL)
         load_gate(0, 1, HB, HL)
-        load_gate(1, 0)
-        load_gate(1, 1)
-        w_raw[2] = load_cols("w_raw", W_down, 2, 0)
-        load_gate(2, 0)
-        load_gate(2, 1)
-        w_raw[3] = load_cols("w_raw", W_down, 3, 0)
-        load_gate(3, 0)
-        load_gate(3, 1)
-        x_raw[0] = load_cols("x_raw", x_pred, 0, 0)
-        x_raw[1] = load_cols("x_raw", x_pred, 0, 1)
+        w_raw[1] = load_cols("w_raw", W_down, 1, 0)
 
         nc.gpsimd.memset(warm_in[:], 0.0)
-        nc.scalar.activation(out=warm_out[:], in_=warm_in[:], func=ACT.Sigmoid)
+        nc.scalar.activation(out=warm_out[:], in_=warm_in[:], func=ACT.Silu)
         make_identity(nc, ident[:])
         nc.gpsimd.memset(ones[:], 1.0)
         nc.gpsimd.memset(ssq_mm[:], 0.0)
-        nc.gpsimd.memset(ssq_act[:], 0.0)
+        nc.gpsimd.memset(half[:], 0.5)
         make_identity(nc, ident_bf[:])
-        nc.gpsimd.tensor_scalar(out=minus_bf[:], in0=ident_bf[:], scalar1=-1.0, scalar2=0.0, op0=ALU.mult, op1=ALU.add)
+        nc.gpsimd.tensor_scalar(out=minus_bf[:], in0=ident_bf[:], scalar1=-0.5, scalar2=0.0, op0=ALU.mult, op1=ALU.add)
 
         def group_tile():
             t = grp.tile([P, HL * PACK], BF16, name="grouped", tag="grouped", align_bytes=64)
@@ -122,15 +115,13 @@ def tile_continuummemorysystem_pa_kernel(tc, err, W_down, gate_pre, up_pre, x_pr
                 nc.scalar.copy(out=dst4, in_=src4)
             return t
 
-        def interleave_gp(src):
-            t = group_tile()
-            for lo in range(0, HL, HT):
+        def interleave_gp(t, src, lo, hi):
+            for lo in range(lo, hi, HT):
                 nc.gpsimd.tensor_scalar(
                     out=t[:, lo * PACK:(lo + HT) * PACK].rearrange("p (w j) -> p w j", j=PACK),
                     in0=src[:, :, lo:lo + HT].rearrange("p j w -> p w j"),
                     scalar1=1.0, scalar2=0.0, op0=ALU.mult, op1=ALU.add,
                 )
-            return t
 
         def quantize(t, codes, scales, lo):
             nc.vector.quantize_mx(
@@ -143,24 +134,20 @@ def tile_continuummemorysystem_pa_kernel(tc, err, W_down, gate_pre, up_pre, x_pr
             c, off = divmod(b * HB, HL)
             return gate_sb[c][:, :, off:off + HB]
 
-        ex, tx, dh, ups = {}, {}, {}, {}
+        ex, lx, tx, dh, ups = {}, {}, {}, {}, {}
+        funcs = {"t": (ex, ACT.Tanh, 0.5), "L": (lx, ACT.Silu, 1.0), "T": (tx, ACT.Silu, -1.0)}
 
-        def act_sig(b, g_lo=0, g_hi=G):
+        def act(what, b, g_lo=0, g_hi=G):
+            tiles, func, scale = funcs[what]
             if g_lo == 0:
-                ex[b] = elem.tile([P, NQ, HB, 2], F32, name="ex", tag="ex", bufs=N_HB)
+                tiles[b] = elem.tile([P, NQ, HB, 2], F32, name="f_" + what, tag="f_" + what, bufs=3 if what == "L" else 4)
             pairs = gate_slab(b).rearrange("p (q e) h -> p q h e", e=2)
             nc.scalar.activation(
-                out=ex[b][:, 2 * g_lo:2 * g_hi, :, :], in_=pairs[:, 2 * g_lo:2 * g_hi, :, :], func=ACT.Sigmoid,
-            )
-
-        def act_silu(b):
-            tx[b] = elem.tile([P, NQ, HB, 2], F32, name="tx", tag="tx")
-            nc.scalar.activation(
-                out=tx[b][:], in_=gate_slab(b).rearrange("p (q e) h -> p q h e", e=2), func=ACT.Silu, scale=-1.0,
+                out=tiles[b][:, 2 * g_lo:2 * g_hi, :, :], in_=pairs[:, 2 * g_lo:2 * g_hi, :, :], func=func, scale=scale,
             )
 
         def stage1(b, g):
-            dh[b, g] = psum.tile([P, PACK, HB], BF16, name="dh", tag="dh")
+            dh[b, g] = psum.tile([P, PACK, HB], BF16, name="dh", tag="dh", bufs=2)
             for t in range(PACK):
                 lo = g * K_PASS + t * P
                 nc.tensor.matmul_mx(
@@ -173,14 +160,16 @@ def tile_continuummemorysystem_pa_kernel(tc, err, W_down, gate_pre, up_pre, x_pr
                 )
 
         def e_mul(b, g):
-            half = ex[b][:, 2 * g:2 * g + 2, :, :]
-            nc.vector.tensor_tensor(
-                out=half, in0=dh[b, g][:].rearrange("p (s e) h -> p s h e", e=2), in1=half, op=ALU.mult,
-            )
+            for s in range(2):
+                pairs = ex[b][:, 2 * g + s, :, :]
+                nc.vector.scalar_tensor_tensor(
+                    out=pairs, in0=pairs, scalar=1.0, in1=dh[b, g][:, 2 * s:2 * s + 2, :].rearrange("p e h -> p h e"),
+                    op0=ALU.add, op1=ALU.mult,
+                )
 
         def upmm(b, g):
             c, off = divmod(b * HB, HL)
-            ups[b, g] = psum.tile([P, 2, 2 * HB], BF16, name="ups", tag="dh")
+            ups[b, g] = psum.tile([P, 2, 2 * HB], BF16, name="ups", tag="ups", bufs=2)
             for e in range(2):
                 nc.tensor.matmul(
                     out=ups[b, g][:, e, :], lhsT=minus_bf[:],
@@ -189,41 +178,37 @@ def tile_continuummemorysystem_pa_kernel(tc, err, W_down, gate_pre, up_pre, x_pr
 
         def x_mul(b, g):
             pairs = tx[b][:, 2 * g:2 * g + 2, :, :].rearrange("p s h e -> p (s h) e")
+            if (b, g) == (0, 0):
+                other = up_first[:].rearrange("p (e s) h -> p (s h) e", e=2)
+            else:
+                other = ups[b, g][:].rearrange("p e n -> p n e")
             nc.vector.scalar_tensor_tensor(
-                out=pairs, in0=pairs, scalar=1.0, in1=ups[b, g][:].rearrange("p e n -> p n e"),
-                op0=ALU.subtract, op1=ALU.mult,
+                out=pairs, in0=pairs, scalar=1.0, in1=other, op0=ALU.subtract, op1=ALU.mult,
             )
 
         pq, pc, ps, acc = {}, {}, {}, {}
 
         def new_pq(b, a):
-            pq[b, a] = prod.tile([P, G, HB * PACK], BF16, name="pq%d" % a, tag="pq%d" % a, bufs=2, align_bytes=64)
+            pq[b, a] = prod.tile(
+                [P, G, HB * PACK], BF16, name="pq%d" % a, tag="pq_last" if (b, a) == (N_HB - 1, 1) else "pq%d" % a,
+                bufs=2 if a == 0 else 1, align_bytes=64)
 
-        def e_pairs(b, g, lo, hi):
-            return ex[b][:, 2 * g:2 * g + 2, lo:hi, :].rearrange("p s h e -> p h s e")
-
-        def up_mul(b, g, lo, hi):
-            nc.vector.tensor_tensor(
-                out=pq[b, 0][:, g, lo * PACK:hi * PACK].rearrange("p (h s e) -> p h s e", s=2, e=2),
-                in0=gate_slab(b)[:, g * PACK:(g + 1) * PACK, lo:hi].rearrange("p (s e) h -> p h s e", e=2),
-                in1=e_pairs(b, g, lo, hi), op=ALU.mult,
+        def product(engine, b, g, a, bank_or_e, factor, lo=0, hi=HB):
+            engine.tensor_tensor(
+                out=pq[b, a][:, g, lo * PACK:hi * PACK].rearrange("p (h s e) -> p h s e", s=2, e=2),
+                in0=bank_or_e,
+                in1=factor[b][:, 2 * g:2 * g + 2, lo:hi, :].rearrange("p s h e -> p h s e"), op=ALU.mult,
             )
 
-        def v_up(b):
-            new_pq(b, 0)
-            for g in range(G):
-                up_mul(b, g, 0, HB)
+        def up_mul(b, g):
+            product(nc.vector, b, g, 0, dh[b, g][:].rearrange("p (s e) h -> p h s e", e=2), lx)
 
-        def gate_mul(b, g):
-            nc.vector.tensor_tensor(
-                out=pq[b, 1][:, g, :].rearrange("p (h s e) -> p h s e", s=2, e=2),
-                in0=e_pairs(b, g, 0, HB),
-                in1=tx[b][:, 2 * g:2 * g + 2, :, :].rearrange("p s h e -> p h s e"), op=ALU.mult,
-            )
+        def gate_mul(engine, b, g):
+            product(engine, b, g, 1, ex[b][:, 2 * g:2 * g + 2, :, :].rearrange("p s h e -> p h s e"), tx)
 
         def pquant(b, a):
-            pc[b, a] = prod.tile([P, G * HB], U32, name="pc", tag="pc", bufs=11, align_bytes=64)
-            ps[b, a] = prod.tile([P, G * HB], U8, name="ps", tag="ps", bufs=11, align_bytes=64)
+            pc[b, a] = prod.tile([P, G * HB], U32, name="pc", tag="pc", bufs=4, align_bytes=64)
+            ps[b, a] = prod.tile([P, G * HB], U8, name="ps", tag="ps", bufs=4, align_bytes=64)
             nc.vector.quantize_mx(
                 out=pc[b, a][:].bitcast(FP8X4), scales=ps[b, a][:],
                 in_=pq[b, a][:].rearrange("p g c -> p (g c)"),
@@ -258,10 +243,10 @@ def tile_continuummemorysystem_pa_kernel(tc, err, W_down, gate_pre, up_pre, x_pr
             words = e_raw[g][:].rearrange("p j d -> p (j d)").bitcast(F32)
             e_grp[g] = group_tile()
             egw = e_grp[g][:].bitcast(F32).rearrange("p (t m u) -> p t m u", t=PACK, u=2)
-            for half in range(2):
-                xt = psum.tile([P, PACK, P], F32, name="xt", tag="dh")
+            for half_t in range(2):
+                xt = psum.tile([P, PACK, P], F32, name="xt", tag="dh" if half_t else "ups", bufs=2)
                 for tt in range(2):
-                    t = 2 * half + tt
+                    t = 2 * half_t + tt
                     for u in range(2):
                         nc.tensor.transpose(
                             out=xt[:, 2 * tt + u, :],
@@ -269,121 +254,151 @@ def tile_continuummemorysystem_pa_kernel(tc, err, W_down, gate_pre, up_pre, x_pr
                             identity=ident[:],
                         )
                 nc.scalar.copy(
-                    out=egw[:, 2 * half:2 * half + 2, :, :],
+                    out=egw[:, 2 * half_t:2 * half_t + 2, :, :],
                     in_=xt[:].rearrange("p (tt u) m -> p tt m u", u=2),
                 )
 
         ctx.enter_context(tc.manual_schedule(engines={ENG.Activation, ENG.DVE, ENG.Pool, ENG.PE}))
 
+        gw, gx = {}, {}
+        gw[0] = interleave("v", w_raw[0])
+        act("t", 0, 0, 1)
+        act("t", 0, 1, 2)
         err_turn(0)
-        gw = {0: interleave("v", w_raw[0])}
-        act_sig(0, 0, 1)
         err_turn(1)
-        act_sig(0, 1, 2)
         quantize(gw[0], w_codes, w_scales, 0)
         quantize(e_grp[0], e_codes, e_scales, 0)
         stage1(0, 0)
-        gw[1] = interleave_gp(w_raw[1])
         quantize(e_grp[1], e_codes, e_scales, K_PASS)
         stage1(0, 1)
-        e_mul(0, 0)
-        act_sig(1)
+        act("L", 0)
+        act("T", 0)
+        nc.gpsimd.tensor_scalar(
+            out=up_first[:].rearrange("p (e s) h -> p s e h", e=2),
+            in0=up_raw[0, 0][:, :, 0:HB].rearrange("p (s e) h -> p s e h", e=2),
+            scalar1=-0.5, scalar2=0.0, op0=ALU.mult, op1=ALU.add,
+        )
+        gw[1] = group_tile()
+        interleave_gp(gw[1], w_raw[1], 0, HL)
+        x_raw[0] = load_cols("x_raw", x_pred, 0, 0)
+        x_raw[1] = load_cols("x_raw", x_pred, 0, 1)
+        load_gate(1, 0)
+        load_gate(1, 1)
+        for g in range(G):
+            up_raw[1, g] = load_cols("up_raw", up_pre, 1, g)
+        w_raw[2] = load_cols("w_raw", W_down, 2, 0)
+        gx[0] = group_tile()
+        interleave_gp(gx[0], x_raw[0], 0, HL)
         gram = psum.tile([P, P], F32, name="gram", tag="acc")
-        rows = [(g, j) for g in range(G) for j in range(PACK)][:-2]
-
-        def gram_rows(i):
-            g, j = rows[i]
-            for fb in range(D // P):
-                blk = e_raw[g][:, j, fb * P:(fb + 1) * P]
-                nc.tensor.matmul(
-                    out=gram[:], lhsT=blk, rhs=blk,
-                    start=(i == 0 and fb == 0), stop=(i == len(rows) - 1 and fb == D // P - 1),
-                )
-
+        for g in range(G):
+            for j in range(PACK):
+                for fb in range(D // P):
+                    blk = e_raw[g][:, j, fb * P:(fb + 1) * P]
+                    nc.tensor.matmul(
+                        out=gram[:], lhsT=blk, rhs=blk, start=(g == 0 and j == 0 and fb == 0),
+                        stop=(g == G - 1 and j == PACK - 1 and fb == D // P - 1),
+                    )
+        upmm(0, 1)
+        for what in ("t", "L", "T"):
+            act(what, 1)
 
         for b in range(N_HB):
-            if b > 0:
-                e_mul(b, 0)
-            if b + 1 < N_HB:
-                stage1(b + 1, 0)
-                stage1(b + 1, 1)
-            if 1 <= b <= 3:
-                gram_rows(2 * b - 2)
-                gram_rows(2 * b - 1)
+            more = b + 1 < N_HB
+            new_pq(b, 0)
+            new_pq(b, 1)
             if b + 2 < N_HB:
-                act_sig(b + 2)
-            e_mul(b, 1)
-            if b % 2 == 0 and b + 2 < N_HB:
-                c = (b + 2) // 2
-                quantize(gw[c], w_codes, w_scales, c * HL)
-            v_up(b)
-            if b > 0:
-                pquant(b - 1, 0)
+                act("t", b + 2)
+            e_mul(b, 0)
+            if not more:
+                x_mul(b, 0)
+                gate_mul(nc.gpsimd, b, 0)
             if b == 0:
-                gw[2] = interleave_gp(w_raw[2])
-            if b == 1:
-                nc.scalar.activation(
-                    out=squares[:], in_=e_raw[1][:, 2:4, :].rearrange("p j d -> p (j d)"), func=ACT.Square,
-                    accum_out=ssq_act[:, 0:1],
-                )
-            if b == 3:
-                gw[3] = interleave("v", w_raw[3])
-            if b == 4:
+                e_mul(b, 1)
                 nc.vector.scalar_tensor_tensor(
                     out=diag[:], in0=gram[:], scalar=1.0, in1=ident[:], op0=ALU.mult, op1=ALU.mult,
                     accum_out=ssq_mm[:, 0:1],
                 )
-            if b == 5:
                 tot = psum.tile([P, 2], F32, name="tot", tag="acc")
-                nc.tensor.matmul(out=tot[:], lhsT=ones[:], rhs=ssq_mm[:], start=True, stop=False)
-                nc.tensor.matmul(out=tot[:], lhsT=ones[:], rhs=ssq_act[:], start=False, stop=True)
-        for c in range(N_HL):
-            for g in range(G):
-                up_raw[c, g] = load_cols("up_raw", up_pre, c, g)
-
-        nc.scalar.activation(out=em[:], in_=tot[:, 0:1], func=ACT.Sqrt, scale=1.0 / (N_TOK * N_TOK))
-        act_silu(0)
-        act_silu(1)
-        gx = [interleave("s", x_raw[g]) for g in range(G)]
-        upmm(0, 0)
-        upmm(0, 1)
-        nc.vector.tensor_scalar(out=ema[:], in0=em[:], scalar1=0.05, scalar2=0.95, op0=ALU.mult, op1=ALU.add)
-        for b in range(N_HB):
-            x_mul(b, 0)
-            if b == 0:
-                nc.vector.tensor_scalar(out=emc[:], in0=ema[:], scalar1=1e-8, scalar2=None, op0=ALU.max)
-            x_mul(b, 1)
-            if b + 1 < N_HB:
-                upmm(b + 1, 0)
-                upmm(b + 1, 1)
-            if b == 0:
-                nc.vector.reciprocal(out=rec[:], in_=emc[:])
-            if b == 0:
-                pquant(N_HB - 1, 0)
-            if b == 1:
-                quantize(gx[0], x_codes, x_scales, 0)
-            if b > 0:
-                pquant(b - 1, 1)
-            new_pq(b, 1)
-            gate_mul(b, 0)
+                nc.tensor.matmul(out=tot[:], lhsT=ones[:], rhs=ssq_mm[:], start=True, stop=True)
+            if more:
+                up_mul(b, 0)
+                stage1(b + 1, 0)
             if b == 0:
                 nc.vector.tensor_scalar(
-                    out=sgv[:], in0=rec[:], scalar1=em[:, 0:1], scalar2=3.0, op0=ALU.mult, op1=ALU.min)
-            if b == 1:
-                quantize(gx[1], x_codes, x_scales, D)
-                stage2(0, 0)
-            if b > 0:
+                    out=msq[:], in0=tot[:, 0:1], scalar1=1.0 / (N_TOK * N_TOK), scalar2=None, op0=ALU.mult)
+                nc.gpsimd.tensor_tensor(out=em[:], in0=msq[:], in1=half[:], op=ALU.pow)
+                nc.gpsimd.tensor_scalar(out=ema[:], in0=em[:], scalar1=0.05, scalar2=0.95, op0=ALU.mult, op1=ALU.add)
+                nc.gpsimd.tensor_scalar(out=emc[:], in0=ema[:], scalar1=1e-8, scalar2=None, op0=ALU.max)
+            else:
+                e_mul(b, 1)
+            if not more:
+                x_mul(b, 1)
+                pquant(b - 1, 1)
                 stage2(b - 1, 1)
-                stage2(b, 0)
-            gate_mul(b, 1)
+                up_mul(b, 0)
+            up_mul(b, 1)
+            if more:
+                stage1(b + 1, 1)
             if b == 0:
-                nc.vector.tensor_scalar(out=sgs[:], in0=sgv[:], scalar1=1.0 / N_TOK, scalar2=None, op0=ALU.mult)
+                gx[1] = interleave("v", x_raw[1])
+            if b >= 1:
+                evac("v" if b % 2 else "s", (b - 1) * N_TILE, 0)
+                evac("s", (b - 1) * N_TILE + 1, 0)
             if b + 2 < N_HB:
-                act_silu(b + 2)
-            for a, k in ((0, 0),) * (b == 1) + ((1, b - 1), (0, b)) * (b > 0):
-                for hl in range(N_TILE):
-                    evac("s", k * N_TILE + hl, a)
-        pquant(N_HB - 1, 1)
-        stage2(N_HB - 1, 1)
-        evac("s", N_HB * N_TILE - 2, 1)
-        evac("v", N_HB * N_TILE - 1, 1)
+                act("L", b + 2)
+            if more:
+                x_mul(b, 0)
+                if b == 0:
+                    nc.vector.reciprocal(out=rec[:], in_=emc[:])
+                    quantize(gx[0], x_codes, x_scales, 0)
+                upmm(b + 1, 0)
+                x_mul(b, 1)
+                upmm(b + 1, 1)
+                if b == 0:
+                    nc.vector.tensor_scalar(
+                        out=sgv[:], in0=rec[:], scalar1=em[:, 0:1], scalar2=3.0, op0=ALU.mult, op1=ALU.min)
+                    quantize(gw[1], w_codes, w_scales, HL)
+                    quantize(gx[1], x_codes, x_scales, D)
+                    nc.vector.tensor_scalar(out=sgs[:], in0=sgv[:], scalar1=1.0 / N_TOK, scalar2=None, op0=ALU.mult)
+            if b >= 2:
+                evac("s", (b - 2) * N_TILE, 1)
+                evac("s", (b - 2) * N_TILE + 1, 1)
+            if b + 2 < N_HB:
+                act("T", b + 2)
+            if more:
+                if b >= 1:
+                    pquant(b - 1, 1)
+                    stage2(b - 1, 1)
+                if b in (2, 4):
+                    c = 1 + b // 2
+                    quantize(gw[c], w_codes, w_scales, c * HL)
+                pquant(b, 0)
+                stage2(b, 0)
+                for g in range(G):
+                    gate_mul(nc.gpsimd, b, g)
+                if b in (0, 2):
+                    c = 2 + b // 2
+                    gw[c] = group_tile()
+                if b < 4:
+                    c = 2 + b // 2
+                    interleave_gp(gw[c], w_raw[c], (b % 2) * HB, (b % 2 + 1) * HB)
+                if b == 0:
+                    w_raw[3] = load_cols("w_raw", W_down, 3, 0)
+                if b in (0, 2):
+                    c = 2 + b // 2
+                    load_gate(c, 0)
+                    load_gate(c, 1)
+                    for g in range(G):
+                        up_raw[c, g] = load_cols("up_raw", up_pre, c, g)
+            else:
+                pquant(b, 0)
+                stage2(b, 0)
+                gate_mul(nc.vector, b, 1)
+                pquant(b, 1)
+                stage2(b, 1)
+                evac("s", (b - 1) * N_TILE, 1)
+                evac("s", (b - 1) * N_TILE + 1, 1)
+                evac("s", b * N_TILE, 0)
+                evac("s", b * N_TILE + 1, 0)
+                evac("s", b * N_TILE, 1)
+                evac("v", b * N_TILE + 1, 1)

@@ -86,11 +86,11 @@ def tile_continuummemorysystem_pa_kernel(tc, err, W_down, gate_pre, up_pre, x_pr
         w_raw[0] = load_cols("w_raw", W_down, 0, 0)
         load_gate(0, 1, 0, HB)
         e_raw[1] = load_cols("e_raw", err, 0, 1)
-        up_raw[0, 0] = load_cols("up_raw", up_pre, 0, 0)
-        up_raw[0, 1] = load_cols("up_raw", up_pre, 0, 1)
+        w_raw[1] = load_cols("w_raw", W_down, 1, 0)
         load_gate(0, 0, HB, HL)
         load_gate(0, 1, HB, HL)
-        w_raw[1] = load_cols("w_raw", W_down, 1, 0)
+        up_raw[0, 0] = load_cols("up_raw", up_pre, 0, 0)
+        up_raw[0, 1] = load_cols("up_raw", up_pre, 0, 1)
 
         nc.gpsimd.memset(warm_in[:], 0.0)
         nc.scalar.activation(out=warm_out[:], in_=warm_in[:], func=ACT.Silu)
@@ -150,8 +150,9 @@ def tile_continuummemorysystem_pa_kernel(tc, err, W_down, gate_pre, up_pre, x_pr
             dh[b, g] = psum.tile([P, PACK, HB], BF16, name="dh", tag="dh", bufs=2)
             for t in range(PACK):
                 lo = g * K_PASS + t * P
+                s, e = divmod(t, 2)
                 nc.tensor.matmul_mx(
-                    out=dh[b, g][:, t, :],
+                    out=dh[b, g][:, 2 * e + s, :],
                     lhsT=e_codes[:, lo:lo + P].bitcast(FP8X4),
                     lhsT_scale=e_scales[:, lo:lo + P],
                     rhs=w_codes[:, b * HB:(b + 1) * HB].bitcast(FP8X4),
@@ -160,12 +161,11 @@ def tile_continuummemorysystem_pa_kernel(tc, err, W_down, gate_pre, up_pre, x_pr
                 )
 
         def e_mul(b, g):
-            for s in range(2):
-                pairs = ex[b][:, 2 * g + s, :, :]
-                nc.vector.scalar_tensor_tensor(
-                    out=pairs, in0=pairs, scalar=1.0, in1=dh[b, g][:, 2 * s:2 * s + 2, :].rearrange("p e h -> p h e"),
-                    op0=ALU.add, op1=ALU.mult,
-                )
+            pairs = ex[b][:, 2 * g:2 * g + 2, :, :].rearrange("p s h e -> p (s h) e")
+            nc.vector.scalar_tensor_tensor(
+                out=pairs, in0=pairs, scalar=1.0, in1=dh[b, g][:].rearrange("p (e s) h -> p (s h) e", e=2),
+                op0=ALU.add, op1=ALU.mult,
+            )
 
         def upmm(b, g):
             c, off = divmod(b * HB, HL)
@@ -201,7 +201,7 @@ def tile_continuummemorysystem_pa_kernel(tc, err, W_down, gate_pre, up_pre, x_pr
             )
 
         def up_mul(b, g):
-            product(nc.vector, b, g, 0, dh[b, g][:].rearrange("p (s e) h -> p h s e", e=2), lx)
+            product(nc.vector, b, g, 0, dh[b, g][:].rearrange("p (e s) h -> p h s e", e=2), lx)
 
         def gate_mul(engine, b, g):
             product(engine, b, g, 1, ex[b][:, 2 * g:2 * g + 2, :, :].rearrange("p s h e -> p h s e"), tx)
@@ -263,21 +263,20 @@ def tile_continuummemorysystem_pa_kernel(tc, err, W_down, gate_pre, up_pre, x_pr
         gw, gx = {}, {}
         gw[0] = interleave("v", w_raw[0])
         act("t", 0, 0, 1)
-        act("t", 0, 1, 2)
         err_turn(0)
+        act("t", 0, 1, 2)
         err_turn(1)
+        act("L", 0, 0, 1)
+        act("L", 0, 1, 2)
+        act("T", 0)
         quantize(gw[0], w_codes, w_scales, 0)
         quantize(e_grp[0], e_codes, e_scales, 0)
         stage1(0, 0)
+        new_pq(0, 0)
+        e_mul(0, 0)
         quantize(e_grp[1], e_codes, e_scales, K_PASS)
         stage1(0, 1)
-        act("L", 0)
-        act("T", 0)
-        nc.gpsimd.tensor_scalar(
-            out=up_first[:].rearrange("p (e s) h -> p s e h", e=2),
-            in0=up_raw[0, 0][:, :, 0:HB].rearrange("p (s e) h -> p s e h", e=2),
-            scalar1=-0.5, scalar2=0.0, op0=ALU.mult, op1=ALU.add,
-        )
+        up_mul(0, 0)
         gw[1] = group_tile()
         interleave_gp(gw[1], w_raw[1], 0, HL)
         x_raw[0] = load_cols("x_raw", x_pred, 0, 0)
@@ -289,6 +288,15 @@ def tile_continuummemorysystem_pa_kernel(tc, err, W_down, gate_pre, up_pre, x_pr
         w_raw[2] = load_cols("w_raw", W_down, 2, 0)
         gx[0] = group_tile()
         interleave_gp(gx[0], x_raw[0], 0, HL)
+        upmm(0, 1)
+        for what in ("t", "L", "T"):
+            act(what, 1)
+
+        act("t", 2)
+        stage1(1, 0)
+        e_mul(0, 1)
+        up_mul(0, 1)
+        stage1(1, 1)
         gram = psum.tile([P, P], F32, name="gram", tag="acc")
         for g in range(G):
             for j in range(PACK):
@@ -298,99 +306,113 @@ def tile_continuummemorysystem_pa_kernel(tc, err, W_down, gate_pre, up_pre, x_pr
                         out=gram[:], lhsT=blk, rhs=blk, start=(g == 0 and j == 0 and fb == 0),
                         stop=(g == G - 1 and j == PACK - 1 and fb == D // P - 1),
                     )
-        upmm(0, 1)
-        for what in ("t", "L", "T"):
-            act(what, 1)
+        nc.vector.tensor_scalar(
+            out=up_first[:].rearrange("p (e s) h -> p e s h", e=2),
+            in0=up_raw[0, 0][:, :, 0:HB].rearrange("p (s e) h -> p e s h", e=2),
+            scalar1=-0.5, scalar2=None, op0=ALU.mult,
+        )
+        quantize(gw[1], w_codes, w_scales, HL)
+        gx[1] = interleave("v", x_raw[1])
+        pquant(0, 0)
+        act("L", 2)
+        quantize(gx[1], x_codes, x_scales, D)
+        x_mul(0, 0)
+        x_mul(0, 1)
+        act("T", 2)
+        new_pq(0, 1)
+        for g in range(G):
+            gate_mul(nc.gpsimd, 0, g)
+        gw[2] = group_tile()
+        interleave_gp(gw[2], w_raw[2], 0, HB)
+        upmm(1, 0)
+        upmm(1, 1)
 
-        for b in range(N_HB):
+        w_raw[3] = load_cols("w_raw", W_down, 3, 0)
+        for b in range(1, N_HB):
             more = b + 1 < N_HB
             new_pq(b, 0)
-            new_pq(b, 1)
+            if not more:
+                new_pq(b, 1)
+            if b in (1, 2):
+                c = 1 + b
+                load_gate(c, 0)
+                load_gate(c, 1)
+                for g in range(G):
+                    up_raw[c, g] = load_cols("up_raw", up_pre, c, g)
             if b + 2 < N_HB:
                 act("t", b + 2)
             e_mul(b, 0)
-            if not more:
-                x_mul(b, 0)
-                gate_mul(nc.gpsimd, b, 0)
-            if b == 0:
-                e_mul(b, 1)
+            if b == 1:
                 nc.vector.scalar_tensor_tensor(
                     out=diag[:], in0=gram[:], scalar=1.0, in1=ident[:], op0=ALU.mult, op1=ALU.mult,
                     accum_out=ssq_mm[:, 0:1],
                 )
                 tot = psum.tile([P, 2], F32, name="tot", tag="acc")
                 nc.tensor.matmul(out=tot[:], lhsT=ones[:], rhs=ssq_mm[:], start=True, stop=True)
+            if b == 2:
+                nc.vector.reciprocal(out=rec[:], in_=emc[:])
+            if not more:
+                x_mul(b, 0)
+                gate_mul(nc.gpsimd, b, 0)
+                e_mul(b, 1)
+                x_mul(b, 1)
+            up_mul(b, 0)
             if more:
-                up_mul(b, 0)
                 stage1(b + 1, 0)
-            if b == 0:
+                e_mul(b, 1)
+            if b == 2:
+                nc.vector.tensor_scalar(
+                    out=sgv[:], in0=rec[:], scalar1=em[:, 0:1], scalar2=3.0, op0=ALU.mult, op1=ALU.min)
+            up_mul(b, 1)
+            if b == 1:
                 nc.vector.tensor_scalar(
                     out=msq[:], in0=tot[:, 0:1], scalar1=1.0 / (N_TOK * N_TOK), scalar2=None, op0=ALU.mult)
                 nc.gpsimd.tensor_tensor(out=em[:], in0=msq[:], in1=half[:], op=ALU.pow)
                 nc.gpsimd.tensor_scalar(out=ema[:], in0=em[:], scalar1=0.05, scalar2=0.95, op0=ALU.mult, op1=ALU.add)
                 nc.gpsimd.tensor_scalar(out=emc[:], in0=ema[:], scalar1=1e-8, scalar2=None, op0=ALU.max)
-            else:
-                e_mul(b, 1)
-            if not more:
-                x_mul(b, 1)
-                pquant(b - 1, 1)
-                stage2(b - 1, 1)
-                up_mul(b, 0)
-            up_mul(b, 1)
+            if b == 2:
+                nc.vector.tensor_scalar(out=sgs[:], in0=sgv[:], scalar1=1.0 / N_TOK, scalar2=None, op0=ALU.mult)
+                evac("s", 0, 0)
+                evac("s", 1, 0)
             if more:
                 stage1(b + 1, 1)
-            if b == 0:
-                gx[1] = interleave("v", x_raw[1])
-            if b >= 1:
-                evac("v" if b % 2 else "s", (b - 1) * N_TILE, 0)
+            if b >= 2:
+                evac("s", (b - 1) * N_TILE, 0)
                 evac("s", (b - 1) * N_TILE + 1, 0)
             if b + 2 < N_HB:
                 act("L", b + 2)
             if more:
                 x_mul(b, 0)
-                if b == 0:
-                    nc.vector.reciprocal(out=rec[:], in_=emc[:])
-                    quantize(gx[0], x_codes, x_scales, 0)
                 upmm(b + 1, 0)
                 x_mul(b, 1)
                 upmm(b + 1, 1)
-                if b == 0:
-                    nc.vector.tensor_scalar(
-                        out=sgv[:], in0=rec[:], scalar1=em[:, 0:1], scalar2=3.0, op0=ALU.mult, op1=ALU.min)
-                    quantize(gw[1], w_codes, w_scales, HL)
-                    quantize(gx[1], x_codes, x_scales, D)
-                    nc.vector.tensor_scalar(out=sgs[:], in0=sgv[:], scalar1=1.0 / N_TOK, scalar2=None, op0=ALU.mult)
             if b >= 2:
                 evac("s", (b - 2) * N_TILE, 1)
                 evac("s", (b - 2) * N_TILE + 1, 1)
             if b + 2 < N_HB:
                 act("T", b + 2)
             if more:
-                if b >= 1:
-                    pquant(b - 1, 1)
-                    stage2(b - 1, 1)
+                if b == 1:
+                    quantize(gx[0], x_codes, x_scales, 0)
+                    stage2(0, 0)
+                pquant(b - 1, 1)
+                stage2(b - 1, 1)
                 if b in (2, 4):
                     c = 1 + b // 2
                     quantize(gw[c], w_codes, w_scales, c * HL)
                 pquant(b, 0)
                 stage2(b, 0)
+                new_pq(b, 1)
                 for g in range(G):
                     gate_mul(nc.gpsimd, b, g)
-                if b in (0, 2):
-                    c = 2 + b // 2
-                    gw[c] = group_tile()
+                if b == 2:
+                    gw[3] = group_tile()
                 if b < 4:
                     c = 2 + b // 2
                     interleave_gp(gw[c], w_raw[c], (b % 2) * HB, (b % 2 + 1) * HB)
-                if b == 0:
-                    w_raw[3] = load_cols("w_raw", W_down, 3, 0)
-                if b in (0, 2):
-                    c = 2 + b // 2
-                    load_gate(c, 0)
-                    load_gate(c, 1)
-                    for g in range(G):
-                        up_raw[c, g] = load_cols("up_raw", up_pre, c, g)
             else:
+                pquant(b - 1, 1)
+                stage2(b - 1, 1)
                 pquant(b, 0)
                 stage2(b, 0)
                 gate_mul(nc.vector, b, 1)

@@ -66,12 +66,15 @@ def tile_continuummemorysystem_pa_kernel(tc, err, W_down, gate_pre, up_pre, x_pr
         sgv = keep.tile([P, 1], F32, name="sgv", tag="sgv")
         sgs = keep.tile([P, 1], F32, name="sgs", tag="sgs")
 
-        def load_cols(name, src, c, g):
-            t = raw.tile([P, PACK, HL], BF16, name=name, tag="raw")
+        def load_more(t, src, c, g, lo, hi):
             nc.sync.dma_start(
-                out=t[:],
-                in_=src[g * K_PASS:(g + 1) * K_PASS, c * HL:(c + 1) * HL].rearrange("(p j) h -> p j h", j=PACK),
+                out=t[:, :, lo:hi],
+                in_=src[g * K_PASS:(g + 1) * K_PASS, c * HL + lo:c * HL + hi].rearrange("(p j) h -> p j h", j=PACK),
             )
+
+        def load_cols(name, src, c, g, lo=0, hi=HL):
+            t = raw.tile([P, PACK, HL], BF16, name=name, tag="raw")
+            load_more(t, src, c, g, lo, hi)
             return t
 
         def load_gate(c, g, lo=0, hi=HL):
@@ -82,14 +85,16 @@ def tile_continuummemorysystem_pa_kernel(tc, err, W_down, gate_pre, up_pre, x_pr
 
         w_raw, e_raw, x_raw, up_raw = {}, {}, {}, {}
         load_gate(0, 0, 0, HB)
+        up_raw[0, 0] = load_cols("up_raw", up_pre, 0, 0, 0, HB)
         e_raw[0] = load_cols("e_raw", err, 0, 0)
-        w_raw[0] = load_cols("w_raw", W_down, 0, 0)
+        w_raw[0] = load_cols("w_raw", W_down, 0, 0, 0, HB)
         load_gate(0, 1, 0, HB)
         e_raw[1] = load_cols("e_raw", err, 0, 1)
         w_raw[1] = load_cols("w_raw", W_down, 1, 0)
+        load_more(w_raw[0], W_down, 0, 0, HB, HL)
         load_gate(0, 0, HB, HL)
         load_gate(0, 1, HB, HL)
-        up_raw[0, 0] = load_cols("up_raw", up_pre, 0, 0)
+        load_more(up_raw[0, 0], up_pre, 0, 0, HB, HL)
         up_raw[0, 1] = load_cols("up_raw", up_pre, 0, 1)
 
         nc.gpsimd.memset(warm_in[:], 0.0)
@@ -105,10 +110,11 @@ def tile_continuummemorysystem_pa_kernel(tc, err, W_down, gate_pre, up_pre, x_pr
             t = grp.tile([P, HL * PACK], BF16, name="grouped", tag="grouped", align_bytes=64)
             return t
 
-        def interleave(engine, src):
-            t = group_tile()
-            dst4 = t[:].rearrange("p (c i j) -> p c j i", i=4, j=PACK)
-            src4 = src[:].rearrange("p j (c i) -> p c j i", i=4)
+        def interleave(engine, src, t=None, lo=0, hi=HL):
+            if t is None:
+                t = group_tile()
+            dst4 = t[:, lo * PACK:hi * PACK].rearrange("p (c i j) -> p c j i", i=4, j=PACK)
+            src4 = src[:, :, lo:hi].rearrange("p j (c i) -> p c j i", i=4)
             if engine == "v":
                 nc.vector.tensor_copy(out=dst4, in_=src4)
             else:
@@ -123,11 +129,11 @@ def tile_continuummemorysystem_pa_kernel(tc, err, W_down, gate_pre, up_pre, x_pr
                     scalar1=1.0, scalar2=0.0, op0=ALU.mult, op1=ALU.add,
                 )
 
-        def quantize(t, codes, scales, lo):
+        def quantize(t, codes, scales, base, lo=0, hi=HL):
             nc.vector.quantize_mx(
-                out=codes[:, lo:lo + HL].bitcast(FP8X4),
-                scales=scales[:, lo:lo + HL],
-                in_=t[:],
+                out=codes[:, base + lo:base + hi].bitcast(FP8X4),
+                scales=scales[:, base + lo:base + hi],
+                in_=t[:, lo * PACK:hi * PACK],
             )
 
         def gate_slab(b):
@@ -261,15 +267,22 @@ def tile_continuummemorysystem_pa_kernel(tc, err, W_down, gate_pre, up_pre, x_pr
         ctx.enter_context(tc.manual_schedule(engines={ENG.Activation, ENG.DVE, ENG.Pool, ENG.PE}))
 
         gw, gx = {}, {}
-        gw[0] = interleave("v", w_raw[0])
+        nc.vector.tensor_scalar(
+            out=up_first[:].rearrange("p (e s) h -> p e s h", e=2),
+            in0=up_raw[0, 0][:, :, 0:HB].rearrange("p (s e) h -> p e s h", e=2),
+            scalar1=-0.5, scalar2=None, op0=ALU.mult,
+        )
+        act("T", 0, 0, 1)
+        x_mul(0, 0)
+        gw[0] = interleave("v", w_raw[0], None, 0, HB)
         act("t", 0, 0, 1)
         err_turn(0)
         act("t", 0, 1, 2)
         err_turn(1)
         act("L", 0, 0, 1)
         act("L", 0, 1, 2)
-        act("T", 0)
-        quantize(gw[0], w_codes, w_scales, 0)
+        act("T", 0, 1, 2)
+        quantize(gw[0], w_codes, w_scales, 0, 0, HB)
         quantize(e_grp[0], e_codes, e_scales, 0)
         stage1(0, 0)
         new_pq(0, 0)
@@ -288,15 +301,6 @@ def tile_continuummemorysystem_pa_kernel(tc, err, W_down, gate_pre, up_pre, x_pr
         w_raw[2] = load_cols("w_raw", W_down, 2, 0)
         gx[0] = group_tile()
         interleave_gp(gx[0], x_raw[0], 0, HL)
-        upmm(0, 1)
-        for what in ("t", "L", "T"):
-            act(what, 1)
-
-        act("t", 2)
-        stage1(1, 0)
-        e_mul(0, 1)
-        up_mul(0, 1)
-        stage1(1, 1)
         gram = psum.tile([P, P], F32, name="gram", tag="acc")
         for g in range(G):
             for j in range(PACK):
@@ -306,17 +310,33 @@ def tile_continuummemorysystem_pa_kernel(tc, err, W_down, gate_pre, up_pre, x_pr
                         out=gram[:], lhsT=blk, rhs=blk, start=(g == 0 and j == 0 and fb == 0),
                         stop=(g == G - 1 and j == PACK - 1 and fb == D // P - 1),
                     )
-        nc.vector.tensor_scalar(
-            out=up_first[:].rearrange("p (e s) h -> p e s h", e=2),
-            in0=up_raw[0, 0][:, :, 0:HB].rearrange("p (s e) h -> p e s h", e=2),
-            scalar1=-0.5, scalar2=None, op0=ALU.mult,
+        upmm(0, 1)
+        for what in ("t", "L", "T"):
+            act(what, 1)
+
+        act("t", 2)
+        e_mul(0, 1)
+        interleave("v", w_raw[0], gw[0], HB, HL)
+        up_mul(0, 1)
+        quantize(gw[0], w_codes, w_scales, 0, HB, HL)
+        stage1(1, 0)
+        stage1(1, 1)
+        nc.vector.scalar_tensor_tensor(
+            out=diag[:], in0=gram[:], scalar=1.0, in1=ident[:], op0=ALU.mult, op1=ALU.mult,
+            accum_out=ssq_mm[:, 0:1],
         )
+        tot = psum.tile([P, 2], F32, name="tot", tag="acc")
+        nc.tensor.matmul(out=tot[:], lhsT=ones[:], rhs=ssq_mm[:], start=True, stop=True)
         quantize(gw[1], w_codes, w_scales, HL)
         gx[1] = interleave("v", x_raw[1])
+        nc.vector.tensor_scalar(
+            out=msq[:], in0=tot[:, 0:1], scalar1=1.0 / (N_TOK * N_TOK), scalar2=None, op0=ALU.mult)
         pquant(0, 0)
+        nc.gpsimd.tensor_tensor(out=em[:], in0=msq[:], in1=half[:], op=ALU.pow)
+        nc.gpsimd.tensor_scalar(out=ema[:], in0=em[:], scalar1=0.05, scalar2=0.95, op0=ALU.mult, op1=ALU.add)
+        nc.gpsimd.tensor_scalar(out=emc[:], in0=ema[:], scalar1=1e-8, scalar2=None, op0=ALU.max)
         act("L", 2)
         quantize(gx[1], x_codes, x_scales, D)
-        x_mul(0, 0)
         x_mul(0, 1)
         act("T", 2)
         new_pq(0, 1)
@@ -343,13 +363,6 @@ def tile_continuummemorysystem_pa_kernel(tc, err, W_down, gate_pre, up_pre, x_pr
                 act("t", b + 2)
             e_mul(b, 0)
             if b == 1:
-                nc.vector.scalar_tensor_tensor(
-                    out=diag[:], in0=gram[:], scalar=1.0, in1=ident[:], op0=ALU.mult, op1=ALU.mult,
-                    accum_out=ssq_mm[:, 0:1],
-                )
-                tot = psum.tile([P, 2], F32, name="tot", tag="acc")
-                nc.tensor.matmul(out=tot[:], lhsT=ones[:], rhs=ssq_mm[:], start=True, stop=True)
-            if b == 2:
                 nc.vector.reciprocal(out=rec[:], in_=emc[:])
             if not more:
                 x_mul(b, 0)
@@ -360,20 +373,12 @@ def tile_continuummemorysystem_pa_kernel(tc, err, W_down, gate_pre, up_pre, x_pr
             if more:
                 stage1(b + 1, 0)
                 e_mul(b, 1)
-            if b == 2:
+            if b == 1:
                 nc.vector.tensor_scalar(
                     out=sgv[:], in0=rec[:], scalar1=em[:, 0:1], scalar2=3.0, op0=ALU.mult, op1=ALU.min)
             up_mul(b, 1)
             if b == 1:
-                nc.vector.tensor_scalar(
-                    out=msq[:], in0=tot[:, 0:1], scalar1=1.0 / (N_TOK * N_TOK), scalar2=None, op0=ALU.mult)
-                nc.gpsimd.tensor_tensor(out=em[:], in0=msq[:], in1=half[:], op=ALU.pow)
-                nc.gpsimd.tensor_scalar(out=ema[:], in0=em[:], scalar1=0.05, scalar2=0.95, op0=ALU.mult, op1=ALU.add)
-                nc.gpsimd.tensor_scalar(out=emc[:], in0=ema[:], scalar1=1e-8, scalar2=None, op0=ALU.max)
-            if b == 2:
                 nc.vector.tensor_scalar(out=sgs[:], in0=sgv[:], scalar1=1.0 / N_TOK, scalar2=None, op0=ALU.mult)
-                evac("s", 0, 0)
-                evac("s", 1, 0)
             if more:
                 stage1(b + 1, 1)
             if b >= 2:
@@ -389,12 +394,15 @@ def tile_continuummemorysystem_pa_kernel(tc, err, W_down, gate_pre, up_pre, x_pr
             if b >= 2:
                 evac("s", (b - 2) * N_TILE, 1)
                 evac("s", (b - 2) * N_TILE + 1, 1)
-            if b + 2 < N_HB:
+            if b + 2 < N_HB and b > 1:
                 act("T", b + 2)
             if more:
                 if b == 1:
                     quantize(gx[0], x_codes, x_scales, 0)
                     stage2(0, 0)
+                    evac("s", 0, 0)
+                    evac("s", 1, 0)
+                    act("T", b + 2)
                 pquant(b - 1, 1)
                 stage2(b - 1, 1)
                 if b in (2, 4):

@@ -90,8 +90,8 @@ def tile_continuummemorysystem_pa_kernel(tc, err, W_down, gate_pre, up_pre, x_pr
         w_raw[0] = load_cols("w_raw", W_down, 0, 0, 0, HB)
         load_gate(0, 1, 0, HB)
         e_raw[1] = load_cols("e_raw", err, 0, 1)
-        w_raw[1] = load_cols("w_raw", W_down, 1, 0)
         load_more(w_raw[0], W_down, 0, 0, HB, HL)
+        w_raw[1] = load_cols("w_raw", W_down, 1, 0)
         load_gate(0, 0, HB, HL)
         load_gate(0, 1, HB, HL)
         load_more(up_raw[0, 0], up_pre, 0, 0, HB, HL)
@@ -209,8 +209,17 @@ def tile_continuummemorysystem_pa_kernel(tc, err, W_down, gate_pre, up_pre, x_pr
         def up_mul(b, g):
             product(nc.vector, b, g, 0, dh[b, g][:].rearrange("p (e s) h -> p h s e", e=2), lx)
 
-        def gate_mul(engine, b, g):
-            product(engine, b, g, 1, ex[b][:, 2 * g:2 * g + 2, :, :].rearrange("p s h e -> p h s e"), tx)
+        def gate_mul(engine, b, g, lo=0, hi=HB):
+            product(engine, b, g, 1, ex[b][:, 2 * g:2 * g + 2, lo:hi, :].rearrange("p s h e -> p h s e"), tx, lo, hi)
+
+        def pquant_half(b, a, g):
+            if g == 0:
+                pc[b, a] = prod.tile([P, G * HB], U32, name="pc", tag="pc", bufs=4, align_bytes=64)
+                ps[b, a] = prod.tile([P, G * HB], U8, name="ps", tag="ps", bufs=4, align_bytes=64)
+            nc.vector.quantize_mx(
+                out=pc[b, a][:, g * HB:(g + 1) * HB].bitcast(FP8X4), scales=ps[b, a][:, g * HB:(g + 1) * HB],
+                in_=pq[b, a][:, g, :],
+            )
 
         def pquant(b, a):
             pc[b, a] = prod.tile([P, G * HB], U32, name="pc", tag="pc", bufs=4, align_bytes=64)
@@ -220,11 +229,12 @@ def tile_continuummemorysystem_pa_kernel(tc, err, W_down, gate_pre, up_pre, x_pr
                 in_=pq[b, a][:].rearrange("p g c -> p (g c)"),
             )
 
-        def stage2(b, a):
+        def stage2(b, a, halves=range(G)):
             for hl in range(N_TILE):
                 ht = b * N_TILE + hl
-                acc[ht, a] = psum.tile([P, D], F32, name="acc", tag="acc")
-                for g in range(G):
+                if 0 in halves:
+                    acc[ht, a] = psum.tile([P, D], F32, name="acc", tag="acc")
+                for g in halves:
                     lo = g * HB + hl * HT
                     nc.tensor.matmul_mx(
                         out=acc[ht, a][:],
@@ -285,8 +295,10 @@ def tile_continuummemorysystem_pa_kernel(tc, err, W_down, gate_pre, up_pre, x_pr
         quantize(gw[0], w_codes, w_scales, 0, 0, HB)
         quantize(e_grp[0], e_codes, e_scales, 0)
         stage1(0, 0)
+        interleave("v", w_raw[0], gw[0], HB, HL)
         new_pq(0, 0)
         e_mul(0, 0)
+        quantize(gw[0], w_codes, w_scales, 0, HB, HL)
         quantize(e_grp[1], e_codes, e_scales, K_PASS)
         stage1(0, 1)
         up_mul(0, 0)
@@ -316,22 +328,20 @@ def tile_continuummemorysystem_pa_kernel(tc, err, W_down, gate_pre, up_pre, x_pr
 
         act("t", 2)
         e_mul(0, 1)
-        interleave("v", w_raw[0], gw[0], HB, HL)
         up_mul(0, 1)
-        quantize(gw[0], w_codes, w_scales, 0, HB, HL)
         stage1(1, 0)
         stage1(1, 1)
+        quantize(gw[1], w_codes, w_scales, HL)
+        gx[1] = interleave("v", x_raw[1])
         nc.vector.scalar_tensor_tensor(
             out=diag[:], in0=gram[:], scalar=1.0, in1=ident[:], op0=ALU.mult, op1=ALU.mult,
             accum_out=ssq_mm[:, 0:1],
         )
         tot = psum.tile([P, 2], F32, name="tot", tag="acc")
         nc.tensor.matmul(out=tot[:], lhsT=ones[:], rhs=ssq_mm[:], start=True, stop=True)
-        quantize(gw[1], w_codes, w_scales, HL)
-        gx[1] = interleave("v", x_raw[1])
+        pquant(0, 0)
         nc.vector.tensor_scalar(
             out=msq[:], in0=tot[:, 0:1], scalar1=1.0 / (N_TOK * N_TOK), scalar2=None, op0=ALU.mult)
-        pquant(0, 0)
         nc.gpsimd.tensor_tensor(out=em[:], in0=msq[:], in1=half[:], op=ALU.pow)
         nc.gpsimd.tensor_scalar(out=ema[:], in0=em[:], scalar1=0.05, scalar2=0.95, op0=ALU.mult, op1=ALU.add)
         nc.gpsimd.tensor_scalar(out=emc[:], in0=ema[:], scalar1=1e-8, scalar2=None, op0=ALU.max)
@@ -359,20 +369,18 @@ def tile_continuummemorysystem_pa_kernel(tc, err, W_down, gate_pre, up_pre, x_pr
                 load_gate(c, 1)
                 for g in range(G):
                     up_raw[c, g] = load_cols("up_raw", up_pre, c, g)
+            if b >= 2:
+                evac("s", (b - 2) * N_TILE, 1)
+                evac("s", (b - 2) * N_TILE + 1, 1)
             if b + 2 < N_HB:
                 act("t", b + 2)
             e_mul(b, 0)
             if b == 1:
                 nc.vector.reciprocal(out=rec[:], in_=emc[:])
-            if not more:
-                x_mul(b, 0)
-                gate_mul(nc.gpsimd, b, 0)
-                e_mul(b, 1)
-                x_mul(b, 1)
             up_mul(b, 0)
             if more:
                 stage1(b + 1, 0)
-                e_mul(b, 1)
+            e_mul(b, 1)
             if b == 1:
                 nc.vector.tensor_scalar(
                     out=sgv[:], in0=rec[:], scalar1=em[:, 0:1], scalar2=3.0, op0=ALU.mult, op1=ALU.min)
@@ -391,9 +399,6 @@ def tile_continuummemorysystem_pa_kernel(tc, err, W_down, gate_pre, up_pre, x_pr
                 upmm(b + 1, 0)
                 x_mul(b, 1)
                 upmm(b + 1, 1)
-            if b >= 2:
-                evac("s", (b - 2) * N_TILE, 1)
-                evac("s", (b - 2) * N_TILE + 1, 1)
             if b + 2 < N_HB and b > 1:
                 act("T", b + 2)
             if more:
@@ -421,14 +426,20 @@ def tile_continuummemorysystem_pa_kernel(tc, err, W_down, gate_pre, up_pre, x_pr
             else:
                 pquant(b - 1, 1)
                 stage2(b - 1, 1)
-                pquant(b, 0)
-                stage2(b, 0)
-                gate_mul(nc.vector, b, 1)
-                pquant(b, 1)
-                stage2(b, 1)
                 evac("s", (b - 1) * N_TILE, 1)
                 evac("s", (b - 1) * N_TILE + 1, 1)
+                pquant(b, 0)
+                stage2(b, 0)
                 evac("s", b * N_TILE, 0)
                 evac("s", b * N_TILE + 1, 0)
+                x_mul(b, 0)
+                gate_mul(nc.gpsimd, b, 0, 0, HT)
+                x_mul(b, 1)
+                gate_mul(nc.vector, b, 0, HT, HB)
+                gate_mul(nc.vector, b, 1)
+                pquant_half(b, 1, 0)
+                stage2(b, 1, [0])
+                pquant_half(b, 1, 1)
+                stage2(b, 1, [1])
                 evac("s", b * N_TILE, 1)
                 evac("v", b * N_TILE + 1, 1)

@@ -146,19 +146,19 @@ def tile_continuummemorysystem_pa_kernel(tc, err, W_down, gate_pre, up_pre, x_pr
         def act(what, b, g_lo=0, g_hi=G):
             tiles, func, scale = funcs[what]
             if g_lo == 0:
-                tiles[b] = elem.tile([P, NQ, HB, 2], F32, name="f_" + what, tag="f_" + what, bufs=3 if what == "L" else 4)
-            pairs = gate_slab(b).rearrange("p (q e) h -> p q h e", e=2)
+                tiles[b] = elem.tile([P, G, HB, PACK], F32, name="f_" + what, tag="f_" + what, bufs=3 if what == "L" else 4)
             nc.scalar.activation(
-                out=tiles[b][:, 2 * g_lo:2 * g_hi, :, :], in_=pairs[:, 2 * g_lo:2 * g_hi, :, :], func=func, scale=scale,
+                out=tiles[b][:, g_lo:g_hi, :, :],
+                in_=gate_slab(b)[:, g_lo * PACK:g_hi * PACK, :].rearrange("p (g t) h -> p g h t", t=PACK),
+                func=func, scale=scale,
             )
 
         def stage1(b, g):
             dh[b, g] = psum.tile([P, PACK, HB], BF16, name="dh", tag="dh", bufs=2)
             for t in range(PACK):
                 lo = g * K_PASS + t * P
-                s, e = divmod(t, 2)
                 nc.tensor.matmul_mx(
-                    out=dh[b, g][:, 2 * e + s, :],
+                    out=dh[b, g][:, t, :],
                     lhsT=e_codes[:, lo:lo + P].bitcast(FP8X4),
                     lhsT_scale=e_scales[:, lo:lo + P],
                     rhs=w_codes[:, b * HB:(b + 1) * HB].bitcast(FP8X4),
@@ -167,29 +167,27 @@ def tile_continuummemorysystem_pa_kernel(tc, err, W_down, gate_pre, up_pre, x_pr
                 )
 
         def e_mul(b, g):
-            pairs = ex[b][:, 2 * g:2 * g + 2, :, :].rearrange("p s h e -> p (s h) e")
+            half_e = ex[b][:, g, :, :]
             nc.vector.scalar_tensor_tensor(
-                out=pairs, in0=pairs, scalar=1.0, in1=dh[b, g][:].rearrange("p (e s) h -> p (s h) e", e=2),
+                out=half_e, in0=half_e, scalar=1.0, in1=dh[b, g][:].rearrange("p t h -> p h t"),
                 op0=ALU.add, op1=ALU.mult,
             )
 
         def upmm(b, g):
             c, off = divmod(b * HB, HL)
-            ups[b, g] = psum.tile([P, 2, 2 * HB], BF16, name="ups", tag="ups", bufs=2)
-            for e in range(2):
+            ups[b, g] = psum.tile([P, PACK, HB], BF16, name="ups", tag="ups", bufs=2)
+            for t in range(0, PACK, 2):
                 nc.tensor.matmul(
-                    out=ups[b, g][:, e, :], lhsT=minus_bf[:],
-                    rhs=up_raw[c, g][:, e:PACK:2, off:off + HB], start=True, stop=True,
+                    out=ups[b, g][:, t:t + 2, :], lhsT=minus_bf[:],
+                    rhs=up_raw[c, g][:, t:t + 2, off:off + HB], start=True, stop=True,
                 )
 
         def x_mul(b, g):
-            pairs = tx[b][:, 2 * g:2 * g + 2, :, :].rearrange("p s h e -> p (s h) e")
-            if (b, g) == (0, 0):
-                other = up_first[:].rearrange("p (e s) h -> p (s h) e", e=2)
-            else:
-                other = ups[b, g][:].rearrange("p e n -> p n e")
+            half_x = tx[b][:, g, :, :]
+            other = up_first if (b, g) == (0, 0) else ups[b, g]
             nc.vector.scalar_tensor_tensor(
-                out=pairs, in0=pairs, scalar=1.0, in1=other, op0=ALU.subtract, op1=ALU.mult,
+                out=half_x, in0=half_x, scalar=1.0, in1=other[:].rearrange("p t h -> p h t"),
+                op0=ALU.subtract, op1=ALU.mult,
             )
 
         pq, pc, ps, acc = {}, {}, {}, {}
@@ -199,18 +197,18 @@ def tile_continuummemorysystem_pa_kernel(tc, err, W_down, gate_pre, up_pre, x_pr
                 [P, G, HB * PACK], BF16, name="pq%d" % a, tag="pq_last" if (b, a) == (N_HB - 1, 1) else "pq%d" % a,
                 bufs=2 if a == 0 else 1, align_bytes=64)
 
-        def product(engine, b, g, a, bank_or_e, factor, lo=0, hi=HB):
-            engine.tensor_tensor(
-                out=pq[b, a][:, g, lo * PACK:hi * PACK].rearrange("p (h s e) -> p h s e", s=2, e=2),
-                in0=bank_or_e,
-                in1=factor[b][:, 2 * g:2 * g + 2, lo:hi, :].rearrange("p s h e -> p h s e"), op=ALU.mult,
+        def up_mul(b, g):
+            nc.vector.tensor_tensor(
+                out=pq[b, 0][:, g, :].rearrange("p (h t) -> p h t", t=PACK),
+                in0=dh[b, g][:].rearrange("p t h -> p h t"), in1=lx[b][:, g, :, :], op=ALU.mult,
             )
 
-        def up_mul(b, g):
-            product(nc.vector, b, g, 0, dh[b, g][:].rearrange("p (e s) h -> p h s e", e=2), lx)
-
         def gate_mul(engine, b, g, lo=0, hi=HB):
-            product(engine, b, g, 1, ex[b][:, 2 * g:2 * g + 2, lo:hi, :].rearrange("p s h e -> p h s e"), tx, lo, hi)
+            engine.tensor_tensor(
+                out=pq[b, 1][:, g, lo * PACK:hi * PACK],
+                in0=ex[b][:, g, lo:hi, :].rearrange("p h t -> p (h t)"),
+                in1=tx[b][:, g, lo:hi, :].rearrange("p h t -> p (h t)"), op=ALU.mult,
+            )
 
         def pquant_half(b, a, g):
             if g == 0:
@@ -255,7 +253,7 @@ def tile_continuummemorysystem_pa_kernel(tc, err, W_down, gate_pre, up_pre, x_pr
 
         e_grp = {}
 
-        def err_turn(g):
+        def err_turn(g, engines):
             words = e_raw[g][:].rearrange("p j d -> p (j d)").bitcast(F32)
             e_grp[g] = group_tile()
             egw = e_grp[g][:].bitcast(F32).rearrange("p (t m u) -> p t m u", t=PACK, u=2)
@@ -269,26 +267,26 @@ def tile_continuummemorysystem_pa_kernel(tc, err, W_down, gate_pre, up_pre, x_pr
                             in_=words[:, t * 256 + u:(t + 1) * 256:2],
                             identity=ident[:],
                         )
-                nc.scalar.copy(
-                    out=egw[:, 2 * half_t:2 * half_t + 2, :, :],
-                    in_=xt[:].rearrange("p (tt u) m -> p tt m u", u=2),
-                )
+                src = xt[:].rearrange("p (tt u) m -> p tt m u", u=2)
+                if engines[half_t] == "v":
+                    nc.vector.tensor_copy(out=egw[:, 2 * half_t:2 * half_t + 2, :, :], in_=src)
+                else:
+                    nc.scalar.copy(out=egw[:, 2 * half_t:2 * half_t + 2, :, :], in_=src)
 
         ctx.enter_context(tc.manual_schedule(engines={ENG.Activation, ENG.DVE, ENG.Pool, ENG.PE}))
 
         gw, gx = {}, {}
         nc.vector.tensor_scalar(
-            out=up_first[:].rearrange("p (e s) h -> p e s h", e=2),
-            in0=up_raw[0, 0][:, :, 0:HB].rearrange("p (s e) h -> p e s h", e=2),
+            out=up_first[:], in0=up_raw[0, 0][:, :, 0:HB],
             scalar1=-0.5, scalar2=None, op0=ALU.mult,
         )
         act("T", 0, 0, 1)
         x_mul(0, 0)
         gw[0] = interleave("v", w_raw[0], None, 0, HB)
         act("t", 0, 0, 1)
-        err_turn(0)
+        err_turn(0, "vv")
         act("t", 0, 1, 2)
-        err_turn(1)
+        err_turn(1, "ss")
         act("L", 0, 0, 1)
         act("L", 0, 1, 2)
         act("T", 0, 1, 2)
@@ -350,7 +348,7 @@ def tile_continuummemorysystem_pa_kernel(tc, err, W_down, gate_pre, up_pre, x_pr
         x_mul(0, 1)
         act("T", 2)
         new_pq(0, 1)
-        for g in range(G):
+        for g in (1, 0):
             gate_mul(nc.gpsimd, 0, g)
         gw[2] = group_tile()
         interleave_gp(gw[2], w_raw[2], 0, HB)
@@ -358,6 +356,7 @@ def tile_continuummemorysystem_pa_kernel(tc, err, W_down, gate_pre, up_pre, x_pr
         upmm(1, 1)
 
         w_raw[3] = load_cols("w_raw", W_down, 3, 0)
+        pending = []
         for b in range(1, N_HB):
             more = b + 1 < N_HB
             new_pq(b, 0)
@@ -369,9 +368,6 @@ def tile_continuummemorysystem_pa_kernel(tc, err, W_down, gate_pre, up_pre, x_pr
                 load_gate(c, 1)
                 for g in range(G):
                     up_raw[c, g] = load_cols("up_raw", up_pre, c, g)
-            if b >= 2:
-                evac("s", (b - 2) * N_TILE, 1)
-                evac("s", (b - 2) * N_TILE + 1, 1)
             if b + 2 < N_HB:
                 act("t", b + 2)
             e_mul(b, 0)
@@ -380,6 +376,12 @@ def tile_continuummemorysystem_pa_kernel(tc, err, W_down, gate_pre, up_pre, x_pr
             up_mul(b, 0)
             if more:
                 stage1(b + 1, 0)
+            for args in pending:
+                stage2(*args)
+            pending = []
+            if b >= 2:
+                evac("s", (b - 2) * N_TILE, 1)
+                evac("s", (b - 2) * N_TILE + 1, 1)
             e_mul(b, 1)
             if b == 1:
                 nc.vector.tensor_scalar(
@@ -409,12 +411,12 @@ def tile_continuummemorysystem_pa_kernel(tc, err, W_down, gate_pre, up_pre, x_pr
                     evac("s", 1, 0)
                     act("T", b + 2)
                 pquant(b - 1, 1)
-                stage2(b - 1, 1)
+                pending.append((b - 1, 1))
                 if b in (2, 4):
                     c = 1 + b // 2
                     quantize(gw[c], w_codes, w_scales, c * HL)
                 pquant(b, 0)
-                stage2(b, 0)
+                pending.append((b, 0))
                 new_pq(b, 1)
                 for g in range(G):
                     gate_mul(nc.gpsimd, b, g)

from contextlib import ExitStack

import concourse.mybir as mybir
from concourse.masks import make_identity

F32 = mybir.dt.float32
BF16 = mybir.dt.bfloat16
U32 = mybir.dt.uint32
U8 = mybir.dt.uint8
FP8X4 = mybir.dt.float8_e4m3fn_x4
ACT = mybir.ActivationFunctionType
ALU = mybir.AluOpType
ENG = mybir.EngineType

N_TOK, D, H = 1024, 512, 2048
FLOPS = 3 * 2 * N_TOK * D * H

P = 128
PACK = 4
K_PASS = P * PACK
G = N_TOK // K_PASS
HT = 128
HB = 256
N_HB = H // HB
HL = 512
N_HL = H // HL
NQ = G * PACK // 2
N_TILE = HB // HT


def tile_continuummemorysystem_pa_kernel(tc, err, W_down, gate_pre, up_pre, x_pred, out_0, out_1):
    nc = tc.nc
    outs = (out_0, out_1)

    with ExitStack() as ctx:
        keep = ctx.enter_context(tc.tile_pool(name="keep", bufs=1))
        raw = ctx.enter_context(tc.tile_pool(name="raw", bufs=8))
        grp = ctx.enter_context(tc.tile_pool(name="grp", bufs=4))
        elem = ctx.enter_context(tc.tile_pool(name="elem", bufs=3))
        prod = ctx.enter_context(tc.tile_pool(name="prod", bufs=2))
        stage = ctx.enter_context(tc.tile_pool(name="stage", bufs=8))
        psum = ctx.enter_context(tc.psum_pool(name="psum", bufs=4))

        gate_sb = [keep.tile([P, G * PACK, HL], BF16, name="gate%d" % c, tag="gate%d" % c) for c in range(N_HL)]
        w_codes = keep.tile([P, H], U32, name="w_codes", tag="w_codes", align_bytes=64)
        w_scales = keep.tile([P, H], U8, name="w_scales", tag="w_scales", align_bytes=64)
        e_codes = keep.tile([P, N_TOK], U32, name="e_codes", tag="e_codes", align_bytes=64)
        e_scales = keep.tile([P, N_TOK], U8, name="e_scales", tag="e_scales", align_bytes=64)
        x_codes = keep.tile([P, G * D], U32, name="x_codes", tag="x_codes", align_bytes=64)
        x_scales = keep.tile([P, G * D], U8, name="x_scales", tag="x_scales", align_bytes=64)
        ident = keep.tile([P, P], F32, name="ident", tag="ident")
        ident_bf = keep.tile([P, P], BF16, name="ident_bf", tag="ident_bf")
        minus_bf = keep.tile([P, P], BF16, name="minus_bf", tag="minus_bf")
        ones = keep.tile([P, P], F32, name="ones", tag="ones")
        diag = keep.tile([P, P], F32, name="diag", tag="diag")
        half = keep.tile([P, 1], F32, name="half", tag="half")
        msq = keep.tile([P, 1], F32, name="msq", tag="msq")
        up_first = keep.tile([P, PACK, HB], BF16, name="up_first", tag="up_first")
        ssq_mm = keep.tile([P, 2], F32, name="ssq_mm", tag="ssq_mm")
        warm_in = keep.tile([P, 1], F32, name="warm_in", tag="warm_in")
        warm_out = keep.tile([P, 1], F32, name="warm_out", tag="warm_out")
        em = keep.tile([P, 1], F32, name="em", tag="em")
        ema = keep.tile([P, 1], F32, name="ema", tag="ema")
        emc = keep.tile([P, 1], F32, name="emc", tag="emc")
        rec = keep.tile([P, 1], F32, name="rec", tag="rec")
        sgv = keep.tile([P, 1], F32, name="sgv", tag="sgv")
        sgs = keep.tile([P, 1], F32, name="sgs", tag="sgs")

        def load_more(t, src, c, g, lo, hi):
            nc.sync.dma_start(
                out=t[:, :, lo:hi],
                in_=src[g * K_PASS:(g + 1) * K_PASS, c * HL + lo:c * HL + hi].rearrange("(p j) h -> p j h", j=PACK),
            )

        def load_cols(name, src, c, g, lo=0, hi=HL):
            t = raw.tile([P, PACK, HL], BF16, name=name, tag="raw")
            load_more(t, src, c, g, lo, hi)
            return t

        def load_gate(c, g, lo=0, hi=HL):
            nc.sync.dma_start(
                out=gate_sb[c][:, g * PACK:(g + 1) * PACK, lo:hi],
                in_=gate_pre[g * K_PASS:(g + 1) * K_PASS, c * HL + lo:c * HL + hi].rearrange("(p t) h -> p t h", t=PACK),
            )

        w_raw, e_raw, x_raw, up_raw = {}, {}, {}, {}
        load_gate(0, 0, 0, HB)
        up_raw[0, 0] = load_cols("up_raw", up_pre, 0, 0, 0, HB)
        e_raw[0] = load_cols("e_raw", err, 0, 0)
        w_raw[0] = load_cols("w_raw", W_down, 0, 0, 0, HB)
        load_gate(0, 1, 0, HB)
        e_raw[1] = load_cols("e_raw", err, 0, 1)
        load_more(w_raw[0], W_down, 0, 0, HB, HL)
        w_raw[1] = load_cols("w_raw", W_down, 1, 0)
        load_gate(0, 0, HB, HL)
        load_gate(0, 1, HB, HL)
        load_more(up_raw[0, 0], up_pre, 0, 0, HB, HL)
        up_raw[0, 1] = load_cols("up_raw", up_pre, 0, 1)

        nc.gpsimd.memset(warm_in[:], 0.0)
        nc.scalar.activation(out=warm_out[:], in_=warm_in[:], func=ACT.Silu)
        make_identity(nc, ident[:])
        nc.gpsimd.memset(ones[:], 1.0)
        nc.gpsimd.memset(ssq_mm[:], 0.0)
        nc.gpsimd.memset(half[:], 0.5)
        make_identity(nc, ident_bf[:])
        nc.gpsimd.tensor_scalar(out=minus_bf[:], in0=ident_bf[:], scalar1=-0.5, scalar2=0.0, op0=ALU.mult, op1=ALU.add)

        def group_tile():
            t = grp.tile([P, HL * PACK], BF16, name="grouped", tag="grouped", align_bytes=64)
            return t

        def interleave(engine, src, t=None, lo=0, hi=HL):
            if t is None:
                t = group_tile()
            dst4 = t[:, lo * PACK:hi * PACK].rearrange("p (c i j) -> p c j i", i=4, j=PACK)
            src4 = src[:, :, lo:hi].rearrange("p j (c i) -> p c j i", i=4)
            if engine == "v":
                nc.vector.tensor_copy(out=dst4, in_=src4)
            else:
                nc.scalar.copy(out=dst4, in_=src4)
            return t

        def interleave_gp(t, src, lo, hi):
            for lo in range(lo, hi, HT):
                nc.gpsimd.tensor_scalar(
                    out=t[:, lo * PACK:(lo + HT) * PACK].rearrange("p (w j) -> p w j", j=PACK),
                    in0=src[:, :, lo:lo + HT].rearrange("p j w -> p w j"),
                    scalar1=1.0, scalar2=0.0, op0=ALU.mult, op1=ALU.add,
                )

        def quantize(t, codes, scales, base, lo=0, hi=HL):
            nc.vector.quantize_mx(
                out=codes[:, base + lo:base + hi].bitcast(FP8X4),
                scales=scales[:, base + lo:base + hi],
                in_=t[:, lo * PACK:hi * PACK],
            )

        def gate_slab(b):
            c, off = divmod(b * HB, HL)
            return gate_sb[c][:, :, off:off + HB]

        ex, lx, tx, dh, ups = {}, {}, {}, {}, {}
        funcs = {"t": (ex, ACT.Tanh, 0.5), "L": (lx, ACT.Silu, 1.0), "T": (tx, ACT.Silu, -1.0)}

        def act(what, b, g_lo=0, g_hi=G):
            tiles, func, scale = funcs[what]
            if g_lo == 0:
                tiles[b] = elem.tile([P, G, HB, PACK], F32, name="f_" + what, tag="f_" + what, bufs=3 if what == "L" else 4)
            nc.scalar.activation(
                out=tiles[b][:, g_lo:g_hi, :, :],
                in_=gate_slab(b)[:, g_lo * PACK:g_hi * PACK, :].rearrange("p (g t) h -> p g h t", t=PACK),
                func=func, scale=scale,
            )

        def stage1(b, g):
            dh[b, g] = psum.tile([P, PACK, HB], BF16, name="dh", tag="dh", bufs=2)
            for t in range(PACK):
                lo = g * K_PASS + t * P
                nc.tensor.matmul_mx(
                    out=dh[b, g][:, t, :],
                    lhsT=e_codes[:, lo:lo + P].bitcast(FP8X4),
                    lhsT_scale=e_scales[:, lo:lo + P],
                    rhs=w_codes[:, b * HB:(b + 1) * HB].bitcast(FP8X4),
                    rhs_scale=w_scales[:, b * HB:(b + 1) * HB],
                    start=True, stop=True,
                )

        def e_mul(b, g):
            half_e = ex[b][:, g, :, :]
            nc.vector.scalar_tensor_tensor(
                out=half_e, in0=half_e, scalar=1.0, in1=dh[b, g][:].rearrange("p t h -> p h t"),
                op0=ALU.add, op1=ALU.mult,
            )

        def upmm(b, g):
            c, off = divmod(b * HB, HL)
            ups[b, g] = psum.tile([P, PACK, HB], BF16, name="ups", tag="ups", bufs=2)
            for t in range(0, PACK, 2):
                nc.tensor.matmul(
                    out=ups[b, g][:, t:t + 2, :], lhsT=minus_bf[:],
                    rhs=up_raw[c, g][:, t:t + 2, off:off + HB], start=True, stop=True,
                )

        def x_mul(b, g):
            half_x = tx[b][:, g, :, :]
            other = up_first if (b, g) == (0, 0) else ups[b, g]
            nc.vector.scalar_tensor_tensor(
                out=half_x, in0=half_x, scalar=1.0, in1=other[:].rearrange("p t h -> p h t"),
                op0=ALU.subtract, op1=ALU.mult,
            )

        pq, pc, ps, acc = {}, {}, {}, {}

        def new_pq(b, a):
            pq[b, a] = prod.tile(
                [P, G, HB * PACK], BF16, name="pq%d" % a, tag="pq_last" if (b, a) == (N_HB - 1, 1) else "pq%d" % a,
                bufs=2 if a == 0 else 1, align_bytes=64)

        def up_mul(b, g):
            nc.vector.tensor_tensor(
                out=pq[b, 0][:, g, :].rearrange("p (h t) -> p h t", t=PACK),
                in0=dh[b, g][:].rearrange("p t h -> p h t"), in1=lx[b][:, g, :, :], op=ALU.mult,
            )

        def gate_mul(engine, b, g, lo=0, hi=HB):
            engine.tensor_tensor(
                out=pq[b, 1][:, g, lo * PACK:hi * PACK],
                in0=ex[b][:, g, lo:hi, :].rearrange("p h t -> p (h t)"),
                in1=tx[b][:, g, lo:hi, :].rearrange("p h t -> p (h t)"), op=ALU.mult,
            )

        def pquant_half(b, a, g):
            if g == 0:
                pc[b, a] = prod.tile([P, G * HB], U32, name="pc", tag="pc", bufs=4, align_bytes=64)
                ps[b, a] = prod.tile([P, G * HB], U8, name="ps", tag="ps", bufs=4, align_bytes=64)
            nc.vector.quantize_mx(
                out=pc[b, a][:, g * HB:(g + 1) * HB].bitcast(FP8X4), scales=ps[b, a][:, g * HB:(g + 1) * HB],
                in_=pq[b, a][:, g, :],
            )

        def pquant(b, a):
            pc[b, a] = prod.tile([P, G * HB], U32, name="pc", tag="pc", bufs=4, align_bytes=64)
            ps[b, a] = prod.tile([P, G * HB], U8, name="ps", tag="ps", bufs=4, align_bytes=64)
            nc.vector.quantize_mx(
                out=pc[b, a][:].bitcast(FP8X4), scales=ps[b, a][:],
                in_=pq[b, a][:].rearrange("p g c -> p (g c)"),
            )

        def stage2(b, a, halves=range(G)):
            for hl in range(N_TILE):
                ht = b * N_TILE + hl
                if 0 in halves:
                    acc[ht, a] = psum.tile([P, D], F32, name="acc", tag="acc")
                for g in halves:
                    lo = g * HB + hl * HT
                    nc.tensor.matmul_mx(
                        out=acc[ht, a][:],
                        lhsT=pc[b, a][:, lo:lo + HT].bitcast(FP8X4),
                        lhsT_scale=ps[b, a][:, lo:lo + HT],
                        rhs=x_codes[:, g * D:(g + 1) * D].bitcast(FP8X4),
                        rhs_scale=x_scales[:, g * D:(g + 1) * D],
                        start=(g == 0), stop=(g == G - 1),
                    )

        def evac(engine, ht, a):
            res = stage.tile([P, D], F32, name="res", tag="res")
            if engine == "v":
                nc.vector.tensor_scalar(out=res[:], in0=acc[ht, a][:], scalar1=sgs[:, 0:1], scalar2=None, op0=ALU.mult)
            else:
                nc.scalar.activation(out=res[:], in_=acc[ht, a][:], func=ACT.Copy, scale=sgs[:, 0:1])
            nc.sync.dma_start(out=outs[a][ht * HT:(ht + 1) * HT, :], in_=res[:])

        e_grp = {}

        def err_turn(g, engines):
            words = e_raw[g][:].rearrange("p j d -> p (j d)").bitcast(F32)
            e_grp[g] = group_tile()
            egw = e_grp[g][:].bitcast(F32).rearrange("p (t m u) -> p t m u", t=PACK, u=2)
            for half_t in range(2):
                xt = psum.tile([P, PACK, P], F32, name="xt", tag="dh" if half_t else "ups", bufs=2)
                for tt in range(2):
                    t = 2 * half_t + tt
                    for u in range(2):
                        nc.tensor.transpose(
                            out=xt[:, 2 * tt + u, :],
                            in_=words[:, t * 256 + u:(t + 1) * 256:2],
                            identity=ident[:],
                        )
                src = xt[:].rearrange("p (tt u) m -> p tt m u", u=2)
                if engines[half_t] == "v":
                    nc.vector.tensor_copy(out=egw[:, 2 * half_t:2 * half_t + 2, :, :], in_=src)
                else:
                    nc.scalar.copy(out=egw[:, 2 * half_t:2 * half_t + 2, :, :], in_=src)

        ctx.enter_context(tc.manual_schedule(engines={ENG.Activation, ENG.DVE, ENG.Pool, ENG.PE}))

        gw, gx = {}, {}
        nc.vector.tensor_scalar(
            out=up_first[:], in0=up_raw[0, 0][:, :, 0:HB],
            scalar1=-0.5, scalar2=None, op0=ALU.mult,
        )
        act("T", 0, 0, 1)
        x_mul(0, 0)
        gw[0] = interleave("v", w_raw[0], None, 0, HB)
        act("t", 0, 0, 1)
        err_turn(0, "vv")
        act("t", 0, 1, 2)
        err_turn(1, "ss")
        act("L", 0, 0, 1)
        act("L", 0, 1, 2)
        act("T", 0, 1, 2)
        quantize(gw[0], w_codes, w_scales, 0, 0, HB)
        quantize(e_grp[0], e_codes, e_scales, 0)
        stage1(0, 0)
        interleave("v", w_raw[0], gw[0], HB, HL)
        new_pq(0, 0)
        e_mul(0, 0)
        quantize(gw[0], w_codes, w_scales, 0, HB, HL)
        quantize(e_grp[1], e_codes, e_scales, K_PASS)
        stage1(0, 1)
        up_mul(0, 0)
        gw[1] = group_tile()
        interleave_gp(gw[1], w_raw[1], 0, HL)
        x_raw[0] = load_cols("x_raw", x_pred, 0, 0)
        x_raw[1] = load_cols("x_raw", x_pred, 0, 1)
        load_gate(1, 0)
        load_gate(1, 1)
        for g in range(G):
            up_raw[1, g] = load_cols("up_raw", up_pre, 1, g)
        w_raw[2] = load_cols("w_raw", W_down, 2, 0)
        gx[0] = group_tile()
        interleave_gp(gx[0], x_raw[0], 0, HL)
        gram = psum.tile([P, P], F32, name="gram", tag="acc")
        for g in range(G):
            for j in range(PACK):
                for fb in range(D // P):
                    blk = e_raw[g][:, j, fb * P:(fb + 1) * P]
                    nc.tensor.matmul(
                        out=gram[:], lhsT=blk, rhs=blk, start=(g == 0 and j == 0 and fb == 0),
                        stop=(g == G - 1 and j == PACK - 1 and fb == D // P - 1),
                    )
        upmm(0, 1)
        for what in ("t", "L", "T"):
            act(what, 1)

        act("t", 2)
        e_mul(0, 1)
        up_mul(0, 1)
        stage1(1, 0)
        stage1(1, 1)
        quantize(gw[1], w_codes, w_scales, HL)
        gx[1] = interleave("v", x_raw[1])
        nc.vector.scalar_tensor_tensor(
            out=diag[:], in0=gram[:], scalar=1.0, in1=ident[:], op0=ALU.mult, op1=ALU.mult,
            accum_out=ssq_mm[:, 0:1],
        )
        tot = psum.tile([P, 2], F32, name="tot", tag="acc")
        nc.tensor.matmul(out=tot[:], lhsT=ones[:], rhs=ssq_mm[:], start=True, stop=True)
        pquant(0, 0)
        nc.vector.tensor_scalar(
            out=msq[:], in0=tot[:, 0:1], scalar1=1.0 / (N_TOK * N_TOK), scalar2=None, op0=ALU.mult)
        nc.gpsimd.tensor_tensor(out=em[:], in0=msq[:], in1=half[:], op=ALU.pow)
        nc.gpsimd.tensor_scalar(out=ema[:], in0=em[:], scalar1=0.05, scalar2=0.95, op0=ALU.mult, op1=ALU.add)
        nc.gpsimd.tensor_scalar(out=emc[:], in0=ema[:], scalar1=1e-8, scalar2=None, op0=ALU.max)
        act("L", 2)
        quantize(gx[1], x_codes, x_scales, D)
        x_mul(0, 1)
        act("T", 2)
        new_pq(0, 1)
        for g in (1, 0):
            gate_mul(nc.gpsimd, 0, g)
        gw[2] = group_tile()
        interleave_gp(gw[2], w_raw[2], 0, HB)
        upmm(1, 0)
        upmm(1, 1)

        w_raw[3] = load_cols("w_raw", W_down, 3, 0)
        pending = []
        for b in range(1, N_HB):
            more = b + 1 < N_HB
            new_pq(b, 0)
            if not more:
                new_pq(b, 1)
            if b in (1, 2):
                c = 1 + b
                load_gate(c, 0)
                load_gate(c, 1)
                for g in range(G):
                    up_raw[c, g] = load_cols("up_raw", up_pre, c, g)
            if b + 2 < N_HB:
                act("t", b + 2)
            e_mul(b, 0)
            if b == 1:
                nc.vector.reciprocal(out=rec[:], in_=emc[:])
            up_mul(b, 0)
            if more:
                stage1(b + 1, 0)
            for args in pending:
                stage2(*args)
            pending = []
            if b >= 2:
                evac("s", (b - 2) * N_TILE, 1)
                evac("s", (b - 2) * N_TILE + 1, 1)
            e_mul(b, 1)
            if b == 1:
                nc.vector.tensor_scalar(
                    out=sgv[:], in0=rec[:], scalar1=em[:, 0:1], scalar2=3.0, op0=ALU.mult, op1=ALU.min)
            up_mul(b, 1)
            if b == 1:
                nc.vector.tensor_scalar(out=sgs[:], in0=sgv[:], scalar1=1.0 / N_TOK, scalar2=None, op0=ALU.mult)
            if more:
                stage1(b + 1, 1)
            if b >= 2:
                evac("s", (b - 1) * N_TILE, 0)
                evac("s", (b - 1) * N_TILE + 1, 0)
            if b + 2 < N_HB:
                act("L", b + 2)
            if more:
                x_mul(b, 0)
                upmm(b + 1, 0)
                x_mul(b, 1)
                upmm(b + 1, 1)
            if b + 2 < N_HB and b > 1:
                act("T", b + 2)
            if more:
                if b == 1:
                    quantize(gx[0], x_codes, x_scales, 0)
                    stage2(0, 0)
                    evac("s", 0, 0)
                    evac("s", 1, 0)
                    act("T", b + 2)
                pquant(b - 1, 1)
                pending.append((b - 1, 1))
                if b in (2, 4):
                    c = 1 + b // 2
                    quantize(gw[c], w_codes, w_scales, c * HL)
                pquant(b, 0)
                pending.append((b, 0))
                new_pq(b, 1)
                for g in range(G):
                    gate_mul(nc.gpsimd, b, g)
                if b == 2:
                    gw[3] = group_tile()
                if b < 4:
                    c = 2 + b // 2
                    interleave_gp(gw[c], w_raw[c], (b % 2) * HB, (b % 2 + 1) * HB)
            else:
                pquant(b - 1, 1)
                stage2(b - 1, 1)
                evac("s", (b - 1) * N_TILE, 1)
                evac("s", (b - 1) * N_TILE + 1, 1)
                pquant(b, 0)
                stage2(b, 0)
                evac("s", b * N_TILE, 0)
                evac("s", b * N_TILE + 1, 0)
                x_mul(b, 0)
                gate_mul(nc.gpsimd, b, 0, 0, HT)
                x_mul(b, 1)
                gate_mul(nc.vector, b, 0, HT, HB)
                gate_mul(nc.vector, b, 1)
                pquant_half(b, 1, 0)
                stage2(b, 1, [0])
                pquant_half(b, 1, 1)
                stage2(b, 1, [1])
                evac("s", b * N_TILE, 1)
                evac("v", b * N_TILE + 1, 1)
